import numpy as np
import ml_dtypes


def mxq(x, axis, fmt="e4m3"):
    dtype, down = {"e4m3": (ml_dtypes.float8_e4m3fn, 7), "e5m2": (ml_dtypes.float8_e5m2, 14)}[fmt]
    v = np.moveaxis(np.asarray(x, np.float32).astype(ml_dtypes.bfloat16).astype(np.float64), axis, -1)
    blocks = v.reshape(v.shape[:-1] + (-1, 32))
    amax = np.abs(blocks).max(-1, keepdims=True)
    byte = np.maximum(np.where(amax > 0, np.frexp(amax)[1] - 1 + 127, 0) - down, 1)
    scale = np.exp2(byte - 127.0)
    codes = (blocks / scale).astype(np.float32).astype(dtype).astype(np.float64)
    return np.moveaxis((codes * scale).reshape(v.shape), -1, axis)


WIDE = False


def mx_kscale(k):
    if not WIDE:
        return np.ones(k)
    levels = np.array([10, -10, 5, -5, 0])
    a = np.random.permutation(np.resize(levels, k // 512 * 4)).reshape(k // 512, 4)
    idx = np.arange(k)
    return np.exp2(a[idx // 512, idx % 128 // 32])


BF16 = ml_dtypes.bfloat16


def bf(x):
    return np.asarray(x, np.float32).astype(BF16)


def f64(x):
    return np.asarray(x).astype(np.float64)


B, CI, C, VI, V, N, M = 3, 512, 128, 512, 128, 4096, 1024
EPS = 1e-5
QS = np.sqrt(2.0) / C ** 0.25


def instance_norm(x):
    mu = x.mean(-1, keepdims=True)
    var = np.square(x - mu).mean(-1, keepdims=True)
    return (x - mu) * (1.0 / np.sqrt(var + EPS))


def setup_inputs():
    u = mx_kscale(VI)
    g = np.exp2(np.random.uniform(-8.0, 1.0, (V, 1)))
    c = g * (np.random.standard_normal((B, V, N)) + 0.5 * np.random.standard_normal((B, V, 1)))
    return {"qp": bf(np.random.standard_normal((B, C, N)) * QS),
            "kp": bf(np.random.standard_normal((B, C, M)) * QS),
            "s": bf(np.random.standard_normal((B, VI, M)) * u[None, :, None]),
            "Ws": bf(np.random.standard_normal((V, VI)) / np.sqrt(VI) / u[None, :]),
            "bs_": bf(np.random.standard_normal(V) * 0.3),
            "c": bf(c)}


def reference(qp, kp, s, Ws, bs_, c):
    sp = (mxq(f64(Ws), 1, "e4m3") @ mxq(f64(s), 1, "e4m3")) + f64(bs_)[None, :, None]
    t = f64(kp).transpose(0, 2, 1) @ f64(qp)
    e = np.exp(t - t.max(1, keepdims=True))
    den = e.sum(1, keepdims=True)
    eq = mxq(e, 1, "e4m3")
    mean = (mxq(sp, 2, "e4m3") @ eq) / den
    mean_sq = (mxq(sp * sp, 2, "e4m3") @ eq) / den
    std = np.sqrt(np.maximum(mean_sq - mean * mean, 0.0))
    return instance_norm(f64(c)) * std + mean

@@ -1,0 +1,305 @@
+from contextlib import ExitStack
+
+import concourse.mybir as mybir
+from concourse.masks import make_identity
+
+F32 = mybir.dt.float32
+BF16 = mybir.dt.bfloat16
+U32 = mybir.dt.uint32
+U8 = mybir.dt.uint8
+FP8X4 = mybir.dt.float8_e4m3fn_x4
+ALU = mybir.AluOpType
+ACT = mybir.ActivationFunctionType
+AX = mybir.AxisListType
+
+P = 128
+B, C, VI, V, N, M = 3, 128, 512, 128, 4096, 1024
+EPS = 1e-5
+GROUP = 4
+GN = GROUP * P
+UNITS_B = N // P
+GROUPS_B = UNITS_B // GROUP
+UNITS = B * UNITS_B
+FLOPS = 2 * B * (V * VI * M + C * M * N + 2 * V * M * N)
+
+
+def tile_adaattn3dstylizer_pb_t_kernel(tc, qp, kp, s, Ws, bs_, c, out):
+    nc = tc.nc
+    with ExitStack() as ctx:
+        sb = ctx.enter_context(tc.tile_pool(name="sb", bufs=1))
+        ps = ctx.enter_context(tc.psum_pool(name="ps", bufs=1))
+        ctx.enter_context(tc.manual_schedule())
+        T = {}
+
+        ident_bf = sb.tile([P, P], BF16, name="ident_bf")
+        make_identity(nc, ident_bf[:])
+        ident_f = sb.tile([P, P], F32, name="ident_f")
+        make_identity(nc, ident_f[:])
+
+        def load_qk(b, first):
+            T["kp", b] = sb.tile([P, M], BF16, name="kp_sb", tag="kp", bufs=2)
+            nc.sync.dma_start(out=T["kp", b][:], in_=kp[b])
+            T["qp", b] = sb.tile([P, N], BF16, name="qp_sb", tag="qp", bufs=2)
+            nc.sync.dma_start(out=T["qp", b][:, 0:first], in_=qp[b][:, 0:first])
+
+        def load_rest(b, first):
+            nc.sync.dma_start(out=T["qp", b][:, first:N], in_=qp[b][:, first:N])
+
+        def load_s(b):
+            T["s", b] = sb.tile([P, 4, M], BF16, name="s_raw", tag="s_raw", bufs=1)
+            nc.sync.dma_start(out=T["s", b][:], in_=s[b].rearrange("(p j) m -> p j m", j=4))
+
+        def load_c(b):
+            T["c", b] = sb.tile([P, N], BF16, name="c_sb", tag="c", bufs=2)
+            nc.sync.dma_start(out=T["c", b][:], in_=c[b])
+
+        def weights():
+            ws_pl = sb.tile([P, 4, P], BF16, name="ws_pl")
+            nc.vector.tensor_copy(out=ws_pl[:], in_=T["ws"][:].rearrange("v (p j) -> v j p", j=4))
+            wt_ps = ps.tile([P, 4, P], BF16, name="wt_ps", tag="xt", bufs=2)
+            for j in range(4):
+                nc.tensor.transpose(wt_ps[:, j, :], ws_pl[:, j, :], ident_bf[:])
+            ws_g = sb.tile([P, V, 4], BF16, name="ws_g", align_bytes=64)
+            nc.vector.tensor_copy(out=ws_g[:], in_=wt_ps[:].rearrange("p j v -> p v j"))
+            T["ws_w"] = sb.tile([P, V], U32, name="ws_w", align_bytes=64)
+            T["ws_s"] = sb.tile([P, V], U8, name="ws_s", align_bytes=64)
+            nc.vector.quantize_mx(
+                out=T["ws_w"][:].bitcast(FP8X4), scales=T["ws_s"][:],
+                in_=ws_g[:].rearrange("p v j -> p (v j)"),
+            )
+
+        def style_regroup(b):
+            T["s_g", b] = sb.tile([P, M, 4], BF16, name="s_g", tag="s_g", align_bytes=64)
+            nc.gpsimd.tensor_scalar(
+                out=T["s_g", b][:], in0=T["s", b][:].rearrange("p j m -> p m j"),
+                scalar1=1.0, scalar2=0.0, op0=ALU.mult, op1=ALU.add,
+            )
+
+        def style(b):
+            s_w = sb.tile([P, M], U32, name="s_w", tag="s_w", align_bytes=64)
+            s_s = sb.tile([P, M], U8, name="s_s", tag="s_s", align_bytes=64)
+            nc.vector.quantize_mx(
+                out=s_w[:].bitcast(FP8X4), scales=s_s[:], in_=T["s_g", b][:].rearrange("p m j -> p (m j)")
+            )
+            sp_f = sb.tile([P, 2, V, 4], F32, name="sp_f", tag="sp_f")
+            for g in range(2):
+                sp_ps = ps.tile([P, 4, V], F32, name="sp_ps", tag="acc", bufs=2)
+                for t in range(4):
+                    cols = slice(P * (4 * g + t), P * (4 * g + t + 1))
+                    nc.tensor.matmul_mx(
+                        out=sp_ps[:, t, :],
+                        lhsT=s_w[:, cols].bitcast(FP8X4), lhsT_scale=s_s[:, cols],
+                        rhs=T["ws_w"][:].bitcast(FP8X4), rhs_scale=T["ws_s"][:],
+                        start=True, stop=True,
+                    )
+                nc.vector.tensor_tensor(
+                    out=sp_f[:, g], in0=sp_ps[:].rearrange("p t v -> p v t"),
+                    in1=T["bs"][:].unsqueeze(2).to_broadcast([P, V, 4]), op=ALU.add,
+                )
+            sp_g = sb.tile([P, 2, 2 * V * 4], BF16, name="sp_g", tag="sp_g", align_bytes=64)
+            flat = sp_f[:].rearrange("p g v t -> p (g v t)")
+            nc.gpsimd.tensor_scalar(
+                out=sp_g[:, 0, :], in0=flat, scalar1=1.0, scalar2=0.0, op0=ALU.mult, op1=ALU.add
+            )
+            nc.scalar.activation(out=sp_g[:, 1, :], in_=flat, func=ACT.Square)
+            T["sp_g", b] = sp_g
+
+        def style_quant(b):
+            T["sp_w", b] = sb.tile([P, 4 * V], U32, name="sp_w", tag="sp_w", bufs=2, align_bytes=64)
+            T["sp_s", b] = sb.tile([P, 4 * V], U8, name="sp_s", tag="sp_s", bufs=2, align_bytes=64)
+            nc.vector.quantize_mx(
+                out=T["sp_w", b][:].bitcast(FP8X4), scales=T["sp_s", b][:],
+                in_=T["sp_g", b][:].rearrange("p q x -> p (q x)"),
+            )
+
+        def stats_chunk(b, i):
+            if i == 0:
+                T["stats", b] = sb.tile([P, 8, 6], F32, name="stats", tag="stats", bufs=2)
+            nc.vector.bn_stats(out=T["stats", b][:, i, :], in_=T["c", b][:, 512 * i : 512 * (i + 1)])
+
+        def stats_end(b):
+            mv = sb.tile([P, 2], F32, name="mv", tag="mv", bufs=2)
+            nc.vector.bn_aggr(out=mv[:], in_=T["stats", b][:].rearrange("p a b -> p (a b)"))
+            ve = sb.tile([P, 1], F32, name="ve", tag="ve", bufs=2)
+            nc.vector.tensor_scalar_add(out=ve[:], in0=mv[:, 1:2], scalar1=EPS)
+            rstd2 = sb.tile([P, 1], F32, name="rstd2", tag="rstd2", bufs=2)
+            nc.vector.reciprocal(out=rstd2[:], in_=ve[:])
+            T["mv", b], T["rstd2", b] = mv, rstd2
+
+        def logits(i):
+            b, n0 = i // UNITS_B, P * (i % UNITS_B)
+            for h in range(2):
+                T["lg", i, h] = ps.tile([P, 512], F32, name="lg", tag="lg", bufs=4)
+                nc.tensor.matmul(
+                    T["lg", i, h][:], lhsT=T["qp", b][:, n0 : n0 + P],
+                    rhs=T["kp", b][:, 512 * h : 512 * (h + 1)], start=True, stop=True,
+                )
+
+        def maxima(i):
+            mx2 = sb.tile([P, 2], F32, name="mx2", tag="mx2", bufs=3)
+            for h in range(2):
+                nc.vector.tensor_reduce(out=mx2[:, h : h + 1], in_=T["lg", i, h][:], axis=AX.X, op=ALU.max)
+            T["negmax", i] = sb.tile([P, 1], F32, name="negmax", tag="negmax", bufs=3)
+            nc.vector.tensor_reduce(out=T["negmax", i][:], in_=mx2[:], axis=AX.X, op=ALU.max, negate=True)
+
+        def exps(i):
+            k, r = i // GROUP, i % GROUP
+            if r == 0:
+                T["dens", k] = sb.tile([P, GROUP, 2], F32, name="dens", tag="dens", bufs=3)
+            T["e", i] = sb.tile([P, M], BF16, name="e_sb", tag="e_sb", bufs=3)
+            for h in range(2):
+                nc.scalar.activation(
+                    out=T["e", i][:, 512 * h : 512 * (h + 1)], in_=T["lg", i, h][:], func=ACT.Exp,
+                    bias=T["negmax", i][:, 0:1], scale=1.0, accum_out=T["dens", k][:, r, h : h + 1],
+                )
+
+        def flip(i):
+            T["xt", i] = ps.tile([P, 8, P], BF16, name="xt", tag="xt", bufs=2)
+            for j in range(8):
+                nc.tensor.transpose(T["xt", i][:, j, :], T["e", i][:, P * j : P * (j + 1)], ident_bf[:])
+
+        def regroup(i, on_vector):
+            k, r = i // GROUP, i % GROUP
+            if r == 0:
+                T["e_g", k] = sb.tile([P, 2, GN, 4], BF16, name="e_g", tag="e_g", bufs=2, align_bytes=64)
+            src = T["xt", i][:].rearrange("p (g t) n -> p g n t", g=2)
+            dst = T["e_g", k][:, :, P * r : P * (r + 1), :]
+            if on_vector:
+                nc.vector.tensor_copy(out=dst, in_=src)
+            else:
+                nc.scalar.copy(out=dst, in_=src)
+
+        def recip(k):
+            den4 = sb.tile([P, GROUP], F32, name="den4", tag="den4", bufs=2)
+            nc.vector.tensor_reduce(out=den4[:], in_=T["dens", k][:], axis=AX.X, op=ALU.add)
+            T["r4", k] = sb.tile([P, GROUP], F32, name="r4", tag="r4", bufs=2)
+            nc.vector.reciprocal(out=T["r4", k][:], in_=den4[:])
+
+        def spread(k):
+            T["rb_ps", k] = ps.tile([P, GN], F32, name="rb_ps", tag="acc", bufs=2)
+            for u in range(GROUP):
+                nc.tensor.transpose(
+                    T["rb_ps", k][:, P * u : P * (u + 1)],
+                    T["r4", k][:, u : u + 1].to_broadcast([P, P]), ident_f[:],
+                )
+
+        def spread_out(k):
+            T["rb", k] = sb.tile([P, GN], F32, name="rb", tag="rb", bufs=2)
+            nc.scalar.copy(out=T["rb", k][:], in_=T["rb_ps", k][:])
+
+        def quant(k):
+            T["e_w", k] = sb.tile([P, 2, GN], U32, name="e_w", tag="e_w", bufs=2, align_bytes=64)
+            T["e_s", k] = sb.tile([P, 2, GN], U8, name="e_s", tag="e_s", bufs=2, align_bytes=64)
+            nc.vector.quantize_mx(
+                out=T["e_w", k][:].rearrange("p g n -> p (g n)").bitcast(FP8X4),
+                scales=T["e_s", k][:].rearrange("p g n -> p (g n)"),
+                in_=T["e_g", k][:].rearrange("p g n t -> p (g n t)"),
+            )
+
+        def sums(k):
+            b = k // GROUPS_B
+            for q in range(2):
+                T["acc", k, q] = ps.tile([P, GN], F32, name="acc", tag="acc", bufs=2)
+                for g in range(2):
+                    cols = slice(V * (2 * q + g), V * (2 * q + g + 1))
+                    nc.tensor.matmul_mx(
+                        out=T["acc", k, q][:],
+                        lhsT=T["sp_w", b][:, cols].bitcast(FP8X4), lhsT_scale=T["sp_s", b][:, cols],
+                        rhs=T["e_w", k][:, g, :].bitcast(FP8X4), rhs_scale=T["e_s", k][:, g, :],
+                        start=(g == 0), stop=(g == 1),
+                    )
+
+        def moments(k):
+            b, ns = k // GROUPS_B, slice(GN * (k % GROUPS_B), GN * (k % GROUPS_B + 1))
+            if k % GROUPS_B == 0:
+                T["mean", b] = sb.tile([P, N], F32, name="mean_b", tag="mean_b", bufs=2)
+                T["varc", b] = sb.tile([P, N], F32, name="varc_b", tag="varc_b", bufs=2)
+            mean = T["mean", b][:, ns]
+            nc.vector.tensor_tensor(out=mean, in0=T["acc", k, 0][:], in1=T["rb", k][:], op=ALU.mult)
+            msq = sb.tile([P, GN], F32, name="msq", tag="msq", bufs=2)
+            nc.vector.tensor_tensor(out=msq[:], in0=T["acc", k, 1][:], in1=T["rb", k][:], op=ALU.mult)
+            m2 = sb.tile([P, GN], F32, name="m2", tag="m2", bufs=2)
+            nc.gpsimd.tensor_tensor(out=m2[:], in0=mean, in1=mean, op=ALU.mult)
+            var = sb.tile([P, GN], F32, name="var", tag="var", bufs=2)
+            nc.gpsimd.tensor_tensor(out=var[:], in0=msq[:], in1=m2[:], op=ALU.subtract)
+            nc.gpsimd.tensor_scalar(
+                out=T["varc", b][:, ns], in0=var[:], scalar1=3.0e38, scalar2=0.0, op0=ALU.min, op1=ALU.max
+            )
+
+        def finish(b, lo, hi):
+            ns = slice(lo, hi)
+            x, mean = T["varc", b][:, ns], T["mean", b][:, ns]
+            nc.scalar.activation(out=x, in_=x, func=ACT.Sqrt, scale=T["rstd2", b][:, 0:1])
+            nc.vector.scalar_tensor_tensor(
+                out=x, in0=T["c", b][:, ns], scalar=T["mv", b][:, 0:1], in1=x,
+                op0=ALU.subtract, op1=ALU.mult,
+            )
+            nc.gpsimd.tensor_tensor(out=mean, in0=x, in1=mean, op=ALU.add)
+            nc.sync.dma_start(out=out[b][:, ns], in_=mean)
+
+        FIRST = 512
+        load_qk(0, FIRST)
+        T["ws"] = sb.tile([P, VI], BF16, name="ws_sb")
+        nc.sync.dma_start(out=T["ws"][:], in_=Ws)
+        T["bs"] = sb.tile([P, V], BF16, name="bs_b")
+        nc.sync.dma_start(out=T["bs"][:], in_=bs_.partition_broadcast(P))
+        load_s(0)
+        load_rest(0, FIRST)
+        load_c(0)
+        weights()
+        style_regroup(0)
+        logits(0)
+
+        def live(i):
+            return 0 <= i < UNITS
+
+        for i in range(UNITS + 8):
+            r, kd = i % GROUP, i // GROUP - 1
+            b, ib = i // UNITS_B, i % UNITS_B
+            has_kd = 0 <= kd < UNITS // GROUP
+            if live(i + 1):
+                logits(i + 1)
+            if live(i - 1):
+                flip(i - 1)
+            if r == 2 and has_kd:
+                sums(kd)
+            if live(i):
+                maxima(i)
+            if r == 1 and has_kd:
+                spread_out(kd)
+            if r != 1 and live(i - 2):
+                regroup(i - 2, False)
+            inter = ib == 9 and b < B
+            if inter and b >= 1:
+                stats_end(b - 1)
+                for j in range(4):
+                    finish(b - 1, 1024 * j, 1024 * (j + 1))
+            if live(i):
+                exps(i)
+            if r == 0 and has_kd:
+                recip(kd)
+                regroup(i - 1, True)
+                spread(kd)
+            if r == 1 and has_kd:
+                quant(kd)
+            if r == 2 and live(i):
+                stats_chunk(b, ib // GROUP)
+            if r == 3 and has_kd:
+                moments(kd)
+            if i == 3:
+                style(0)
+            if i == 4:
+                style_quant(0)
+            if ib == 2 and b + 1 < B:
+                load_s(b + 1)
+                load_qk(b + 1, N)
+                load_c(b + 1)
+            if ib == 5 and b + 1 < B:
+                style_regroup(b + 1)
+            if inter and b + 1 < B:
+                style(b + 1)
+            if ib == 10 and b + 1 < B:
+                style_quant(b + 1)
+        stats_end(B - 1)
+        for j in range(4):
+            finish(B - 1, 1024 * j, 1024 * (j + 1))

@@ -21,6 +21,10 @@ UNITS_B = N // P
 GROUPS_B = UNITS_B // GROUP
 UNITS = B * UNITS_B
 FLOPS = 2 * B * (V * VI * M + C * M * N + 2 * V * M * N)
+LEAD = 2
+TBUFS = 5
+LGBUFS = 3
+XTBUFS = 2
 
 
 def tile_adaattn3dstylizer_pb_t_kernel(tc, qp, kp, s, Ws, bs_, c, out):
@@ -53,56 +57,75 @@ def tile_adaattn3dstylizer_pb_t_kernel(tc, qp, kp, s, Ws, bs_, c, out):
             T["c", b] = sb.tile([P, N], BF16, name="c_sb", tag="c", bufs=2)
             nc.sync.dma_start(out=T["c", b][:], in_=c[b])
 
-        def weights():
-            ws_pl = sb.tile([P, 4, P], BF16, name="ws_pl")
-            nc.vector.tensor_copy(out=ws_pl[:], in_=T["ws"][:].rearrange("v (p j) -> v j p", j=4))
-            wt_ps = ps.tile([P, 4, P], BF16, name="wt_ps", tag="xt", bufs=2)
+        def weights_sort():
+            T["ws_pl"] = sb.tile([P, 4, P], BF16, name="ws_pl")
+            nc.vector.tensor_copy(out=T["ws_pl"][:], in_=T["ws"][:].rearrange("v (p j) -> v j p", j=4))
+
+        def weights_flip():
+            T["wt_ps"] = ps.tile([P, 4, P], BF16, name="wt_ps", tag="xt", bufs=XTBUFS)
             for j in range(4):
-                nc.tensor.transpose(wt_ps[:, j, :], ws_pl[:, j, :], ident_bf[:])
-            ws_g = sb.tile([P, V, 4], BF16, name="ws_g", align_bytes=64)
-            nc.vector.tensor_copy(out=ws_g[:], in_=wt_ps[:].rearrange("p j v -> p v j"))
+                nc.tensor.transpose(T["wt_ps"][:, j, :], T["ws_pl"][:, j, :], ident_bf[:])
+
+        def weights_out():
+            T["ws_g"] = sb.tile([P, V, 4], BF16, name="ws_g", align_bytes=64)
+            nc.vector.tensor_copy(out=T["ws_g"][:], in_=T["wt_ps"][:].rearrange("p j v -> p v j"))
+
+        def weights_quant():
             T["ws_w"] = sb.tile([P, V], U32, name="ws_w", align_bytes=64)
             T["ws_s"] = sb.tile([P, V], U8, name="ws_s", align_bytes=64)
             nc.vector.quantize_mx(
                 out=T["ws_w"][:].bitcast(FP8X4), scales=T["ws_s"][:],
-                in_=ws_g[:].rearrange("p v j -> p (v j)"),
+                in_=T["ws_g"][:].rearrange("p v j -> p (v j)"),
             )
 
-        def style_regroup(b):
-            T["s_g", b] = sb.tile([P, M, 4], BF16, name="s_g", tag="s_g", align_bytes=64)
-            nc.gpsimd.tensor_scalar(
-                out=T["s_g", b][:], in0=T["s", b][:].rearrange("p j m -> p m j"),
-                scalar1=1.0, scalar2=0.0, op0=ALU.mult, op1=ALU.add,
-            )
-
-        def style(b):
-            s_w = sb.tile([P, M], U32, name="s_w", tag="s_w", align_bytes=64)
-            s_s = sb.tile([P, M], U8, name="s_s", tag="s_s", align_bytes=64)
-            nc.vector.quantize_mx(
-                out=s_w[:].bitcast(FP8X4), scales=s_s[:], in_=T["s_g", b][:].rearrange("p m j -> p (m j)")
-            )
-            sp_f = sb.tile([P, 2, V, 4], F32, name="sp_f", tag="sp_f")
-            for g in range(2):
-                sp_ps = ps.tile([P, 4, V], F32, name="sp_ps", tag="acc", bufs=2)
-                for t in range(4):
-                    cols = slice(P * (4 * g + t), P * (4 * g + t + 1))
-                    nc.tensor.matmul_mx(
-                        out=sp_ps[:, t, :],
-                        lhsT=s_w[:, cols].bitcast(FP8X4), lhsT_scale=s_s[:, cols],
-                        rhs=T["ws_w"][:].bitcast(FP8X4), rhs_scale=T["ws_s"][:],
-                        start=True, stop=True,
-                    )
-                nc.vector.tensor_tensor(
-                    out=sp_f[:, g], in0=sp_ps[:].rearrange("p t v -> p v t"),
-                    in1=T["bs"][:].unsqueeze(2).to_broadcast([P, V, 4]), op=ALU.add,
+        def style_regroup(b, half, on_vector):
+            if half == 0:
+                T["s_g", b] = sb.tile([P, M, 4], BF16, name="s_g", tag="s_g", align_bytes=64)
+            ms = slice(512 * half, 512 * (half + 1))
+            src = T["s", b][:, :, ms].rearrange("p j m -> p m j")
+            if on_vector:
+                nc.vector.tensor_copy(out=T["s_g", b][:, ms, :], in_=src)
+            else:
+                nc.gpsimd.tensor_scalar(
+                    out=T["s_g", b][:, ms, :], in0=src, scalar1=1.0, scalar2=0.0, op0=ALU.mult, op1=ALU.add
                 )
-            sp_g = sb.tile([P, 2, 2 * V * 4], BF16, name="sp_g", tag="sp_g", align_bytes=64)
-            flat = sp_f[:].rearrange("p g v t -> p (g v t)")
-            nc.gpsimd.tensor_scalar(
-                out=sp_g[:, 0, :], in0=flat, scalar1=1.0, scalar2=0.0, op0=ALU.mult, op1=ALU.add
+
+        def style_words(b, g):
+            if g == 0:
+                T["s_w", b] = sb.tile([P, M], U32, name="s_w", tag="s_w", align_bytes=64)
+                T["s_s", b] = sb.tile([P, M], U8, name="s_s", tag="s_s", align_bytes=64)
+            ms = slice(512 * g, 512 * (g + 1))
+            nc.vector.quantize_mx(
+                out=T["s_w", b][:, ms].bitcast(FP8X4), scales=T["s_s", b][:, ms],
+                in_=T["s_g", b][:, ms, :].rearrange("p m j -> p (m j)"),
             )
-            nc.scalar.activation(out=sp_g[:, 1, :], in_=flat, func=ACT.Square)
-            T["sp_g", b] = sp_g
+
+        def style_project(b, g):
+            T["sp_ps", b, g] = ps.tile([P, 4, V], F32, name="sp_ps", tag="acc", bufs=2)
+            for t in range(4):
+                cols = slice(P * (4 * g + t), P * (4 * g + t + 1))
+                nc.tensor.matmul_mx(
+                    out=T["sp_ps", b, g][:, t, :],
+                    lhsT=T["s_w", b][:, cols].bitcast(FP8X4), lhsT_scale=T["s_s", b][:, cols],
+                    rhs=T["ws_w"][:].bitcast(FP8X4), rhs_scale=T["ws_s"][:],
+                    start=True, stop=True,
+                )
+
+        def style_bias(b, g):
+            if g == 0:
+                T["sp_f", b] = sb.tile([P, 2, V, 4], F32, name="sp_f", tag="sp_f")
+            nc.vector.tensor_tensor(
+                out=T["sp_f", b][:, g], in0=T["sp_ps", b, g][:].rearrange("p t v -> p v t"),
+                in1=T["bs"][:].unsqueeze(2).to_broadcast([P, V, 4]), op=ALU.add,
+            )
+
+        def style_round(b):
+            T["sp_g", b] = sb.tile([P, 2, 2 * V * 4], BF16, name="sp_g", tag="sp_g", align_bytes=64)
+            flat = T["sp_f", b][:].rearrange("p g v t -> p (g v t)")
+            nc.gpsimd.tensor_scalar(
+                out=T["sp_g", b][:, 0, :], in0=flat, scalar1=1.0, scalar2=0.0, op0=ALU.mult, op1=ALU.add
+            )
+            nc.scalar.activation(out=T["sp_g", b][:, 1, :], in_=flat, func=ACT.Square)
 
         def style_quant(b):
             T["sp_w", b] = sb.tile([P, 4 * V], U32, name="sp_w", tag="sp_w", bufs=2, align_bytes=64)
@@ -129,54 +152,57 @@ def tile_adaattn3dstylizer_pb_t_kernel(tc, qp, kp, s, Ws, bs_, c, out):
         def logits(i):
             b, n0 = i // UNITS_B, P * (i % UNITS_B)
             for h in range(2):
-                T["lg", i, h] = ps.tile([P, 512], F32, name="lg", tag="lg", bufs=4)
+                T["lg", i, h] = ps.tile([P, 512], F32, name="lg", tag="lg", bufs=LGBUFS)
                 nc.tensor.matmul(
                     T["lg", i, h][:], lhsT=T["qp", b][:, n0 : n0 + P],
                     rhs=T["kp", b][:, 512 * h : 512 * (h + 1)], start=True, stop=True,
                 )
 
-        def maxima(i):
-            mx2 = sb.tile([P, 2], F32, name="mx2", tag="mx2", bufs=3)
-            for h in range(2):
-                nc.vector.tensor_reduce(out=mx2[:, h : h + 1], in_=T["lg", i, h][:], axis=AX.X, op=ALU.max)
-            T["negmax", i] = sb.tile([P, 1], F32, name="negmax", tag="negmax", bufs=3)
-            nc.vector.tensor_reduce(out=T["negmax", i][:], in_=mx2[:], axis=AX.X, op=ALU.max, negate=True)
+        def max_half(i, h):
+            if h == 0:
+                T["mx2", i] = sb.tile([P, 2], F32, name="mx2", tag="mx2", bufs=3)
+                T["t", i] = sb.tile([P, M], F32, name="t_sb", tag="t_sb", bufs=TBUFS)
+            nc.vector.tensor_scalar(
+                out=T["t", i][:, 512 * h : 512 * (h + 1)], in0=T["lg", i, h][:], scalar1=1.0, scalar2=None,
+                op0=ALU.mult, op1=ALU.max, accum_out=T["mx2", i][:, h : h + 1],
+            )
+
+        def max_join(i):
+            T["negmax", i] = sb.tile([P, 1], F32, name="negmax", tag="negmax", bufs=TBUFS)
+            nc.vector.tensor_reduce(out=T["negmax", i][:], in_=T["mx2", i][:], axis=AX.X, op=ALU.max, negate=True)
 
         def exps(i):
             k, r = i // GROUP, i % GROUP
             if r == 0:
-                T["dens", k] = sb.tile([P, GROUP, 2], F32, name="dens", tag="dens", bufs=3)
+                T["dens", k] = sb.tile([P, GROUP], F32, name="dens", tag="dens", bufs=3)
             T["e", i] = sb.tile([P, M], BF16, name="e_sb", tag="e_sb", bufs=3)
-            for h in range(2):
-                nc.scalar.activation(
-                    out=T["e", i][:, 512 * h : 512 * (h + 1)], in_=T["lg", i, h][:], func=ACT.Exp,
-                    bias=T["negmax", i][:, 0:1], scale=1.0, accum_out=T["dens", k][:, r, h : h + 1],
-                )
+            nc.scalar.activation(
+                out=T["e", i][:], in_=T["t", i][:], func=ACT.Exp,
+                bias=T["negmax", i][:, 0:1], scale=1.0, accum_out=T["dens", k][:, r : r + 1],
+            )
 
         def flip(i):
-            T["xt", i] = ps.tile([P, 8, P], BF16, name="xt", tag="xt", bufs=2)
+            T["xt", i] = ps.tile([P, 8, P], BF16, name="xt", tag="xt", bufs=XTBUFS)
             for j in range(8):
                 nc.tensor.transpose(T["xt", i][:, j, :], T["e", i][:, P * j : P * (j + 1)], ident_bf[:])
 
-        def regroup(i, on_vector):
+        def regroup(i, gs, on_vector):
             k, r = i // GROUP, i % GROUP
-            if r == 0:
+            if ("e_g", k) not in T:
                 T["e_g", k] = sb.tile([P, 2, GN, 4], BF16, name="e_g", tag="e_g", bufs=2, align_bytes=64)
-            src = T["xt", i][:].rearrange("p (g t) n -> p g n t", g=2)
-            dst = T["e_g", k][:, :, P * r : P * (r + 1), :]
+            src = T["xt", i][:].rearrange("p (g t) n -> p g n t", g=2)[:, gs]
+            dst = T["e_g", k][:, gs, P * r : P * (r + 1), :]
             if on_vector:
                 nc.vector.tensor_copy(out=dst, in_=src)
             else:
                 nc.scalar.copy(out=dst, in_=src)
 
-        def recip(k):
-            den4 = sb.tile([P, GROUP], F32, name="den4", tag="den4", bufs=2)
-            nc.vector.tensor_reduce(out=den4[:], in_=T["dens", k][:], axis=AX.X, op=ALU.add)
+        def den_recip(k):
             T["r4", k] = sb.tile([P, GROUP], F32, name="r4", tag="r4", bufs=2)
-            nc.vector.reciprocal(out=T["r4", k][:], in_=den4[:])
+            nc.vector.reciprocal(out=T["r4", k][:], in_=T["dens", k][:])
 
         def spread(k):
-            T["rb_ps", k] = ps.tile([P, GN], F32, name="rb_ps", tag="acc", bufs=2)
+            T["rb_ps", k] = ps.tile([P, GN], F32, name="rb_ps", tag="misc", bufs=1)
             for u in range(GROUP):
                 nc.tensor.transpose(
                     T["rb_ps", k][:, P * u : P * (u + 1)],
@@ -187,29 +213,29 @@ def tile_adaattn3dstylizer_pb_t_kernel(tc, qp, kp, s, Ws, bs_, c, out):
             T["rb", k] = sb.tile([P, GN], F32, name="rb", tag="rb", bufs=2)
             nc.scalar.copy(out=T["rb", k][:], in_=T["rb_ps", k][:])
 
-        def quant(k):
-            T["e_w", k] = sb.tile([P, 2, GN], U32, name="e_w", tag="e_w", bufs=2, align_bytes=64)
-            T["e_s", k] = sb.tile([P, 2, GN], U8, name="e_s", tag="e_s", bufs=2, align_bytes=64)
+        def quant(k, g):
+            if ("e_w", k) not in T:
+                T["e_w", k] = sb.tile([P, 2, GN], U32, name="e_w", tag="e_w", bufs=2, align_bytes=64)
+                T["e_s", k] = sb.tile([P, 2, GN], U8, name="e_s", tag="e_s", bufs=2, align_bytes=64)
             nc.vector.quantize_mx(
-                out=T["e_w", k][:].rearrange("p g n -> p (g n)").bitcast(FP8X4),
-                scales=T["e_s", k][:].rearrange("p g n -> p (g n)"),
-                in_=T["e_g", k][:].rearrange("p g n t -> p (g n t)"),
+                out=T["e_w", k][:, g, :].bitcast(FP8X4), scales=T["e_s", k][:, g, :],
+                in_=T["e_g", k][:, g].rearrange("p n t -> p (n t)"),
             )
 
-        def sums(k):
+        def sums(k, g, first):
             b = k // GROUPS_B
             for q in range(2):
-                T["acc", k, q] = ps.tile([P, GN], F32, name="acc", tag="acc", bufs=2)
-                for g in range(2):
-                    cols = slice(V * (2 * q + g), V * (2 * q + g + 1))
-                    nc.tensor.matmul_mx(
-                        out=T["acc", k, q][:],
-                        lhsT=T["sp_w", b][:, cols].bitcast(FP8X4), lhsT_scale=T["sp_s", b][:, cols],
-                        rhs=T["e_w", k][:, g, :].bitcast(FP8X4), rhs_scale=T["e_s", k][:, g, :],
-                        start=(g == 0), stop=(g == 1),
-                    )
+                if first:
+                    T["acc", k, q] = ps.tile([P, GN], F32, name="acc", tag="acc", bufs=2)
+                cols = slice(V * (2 * q + g), V * (2 * q + g + 1))
+                nc.tensor.matmul_mx(
+                    out=T["acc", k, q][:],
+                    lhsT=T["sp_w", b][:, cols].bitcast(FP8X4), lhsT_scale=T["sp_s", b][:, cols],
+                    rhs=T["e_w", k][:, g, :].bitcast(FP8X4), rhs_scale=T["e_s", k][:, g, :],
+                    start=first, stop=not first,
+                )
 
-        def moments(k):
+        def moments(k, on_vector):
             b, ns = k // GROUPS_B, slice(GN * (k % GROUPS_B), GN * (k % GROUPS_B + 1))
             if k % GROUPS_B == 0:
                 T["mean", b] = sb.tile([P, N], F32, name="mean_b", tag="mean_b", bufs=2)
@@ -219,87 +245,176 @@ def tile_adaattn3dstylizer_pb_t_kernel(tc, qp, kp, s, Ws, bs_, c, out):
             msq = sb.tile([P, GN], F32, name="msq", tag="msq", bufs=2)
             nc.vector.tensor_tensor(out=msq[:], in0=T["acc", k, 1][:], in1=T["rb", k][:], op=ALU.mult)
             m2 = sb.tile([P, GN], F32, name="m2", tag="m2", bufs=2)
-            nc.gpsimd.tensor_tensor(out=m2[:], in0=mean, in1=mean, op=ALU.mult)
             var = sb.tile([P, GN], F32, name="var", tag="var", bufs=2)
-            nc.gpsimd.tensor_tensor(out=var[:], in0=msq[:], in1=m2[:], op=ALU.subtract)
-            nc.gpsimd.tensor_scalar(
-                out=T["varc", b][:, ns], in0=var[:], scalar1=3.0e38, scalar2=0.0, op0=ALU.min, op1=ALU.max
-            )
+            if on_vector:
+                nc.scalar.activation(out=m2[:], in_=mean, func=ACT.Square)
+                nc.vector.tensor_tensor(out=var[:], in0=msq[:], in1=m2[:], op=ALU.subtract)
+                nc.vector.tensor_scalar_max(out=T["varc", b][:, ns], in0=var[:], scalar1=0.0)
+            else:
+                nc.gpsimd.tensor_tensor(out=m2[:], in0=mean, in1=mean, op=ALU.mult)
+                nc.gpsimd.tensor_tensor(out=var[:], in0=msq[:], in1=m2[:], op=ALU.subtract)
+                nc.gpsimd.tensor_scalar(
+                    out=T["varc", b][:, ns], in0=var[:], scalar1=3.0e38, scalar2=0.0, op0=ALU.min, op1=ALU.max
+                )
 
-        def finish(b, lo, hi):
-            ns = slice(lo, hi)
-            x, mean = T["varc", b][:, ns], T["mean", b][:, ns]
+        def fin_sqrt(b, lo, hi):
+            x = T["varc", b][:, lo:hi]
             nc.scalar.activation(out=x, in_=x, func=ACT.Sqrt, scale=T["rstd2", b][:, 0:1])
+
+        def fin_scale(b, lo, hi):
+            x = T["varc", b][:, lo:hi]
             nc.vector.scalar_tensor_tensor(
-                out=x, in0=T["c", b][:, ns], scalar=T["mv", b][:, 0:1], in1=x,
+                out=x, in0=T["c", b][:, lo:hi], scalar=T["mv", b][:, 0:1], in1=x,
                 op0=ALU.subtract, op1=ALU.mult,
             )
-            nc.gpsimd.tensor_tensor(out=mean, in0=x, in1=mean, op=ALU.add)
-            nc.sync.dma_start(out=out[b][:, ns], in_=mean)
+
+        def fin_add(b, lo, hi, on_vector):
+            x, mean = T["varc", b][:, lo:hi], T["mean", b][:, lo:hi]
+            if on_vector:
+                nc.vector.tensor_tensor(out=mean, in0=x, in1=mean, op=ALU.add)
+            else:
+                nc.gpsimd.tensor_tensor(out=mean, in0=x, in1=mean, op=ALU.add)
+            nc.sync.dma_start(out=out[b][:, lo:hi], in_=mean)
 
         FIRST = 512
+        BOTH = slice(0, 2)
+        warm = sb.tile([P, 1], F32, name="warm")
+        nc.vector.memset(warm[:], 0.0)
+        nc.scalar.activation(out=warm[:], in_=warm[:], func=ACT.Exp)
         load_qk(0, FIRST)
         T["ws"] = sb.tile([P, VI], BF16, name="ws_sb")
         nc.sync.dma_start(out=T["ws"][:], in_=Ws)
+        load_s(0)
         T["bs"] = sb.tile([P, V], BF16, name="bs_b")
         nc.sync.dma_start(out=T["bs"][:], in_=bs_.partition_broadcast(P))
-        load_s(0)
         load_rest(0, FIRST)
         load_c(0)
-        weights()
-        style_regroup(0)
-        logits(0)
 
         def live(i):
             return 0 <= i < UNITS
 
-        for i in range(UNITS + 8):
+        LASTK = UNITS // GROUP - 1
+        J = 10
+        for i in range(-LEAD - 1, UNITS):
             r, kd = i % GROUP, i // GROUP - 1
             b, ib = i // UNITS_B, i % UNITS_B
-            has_kd = 0 <= kd < UNITS // GROUP
-            if live(i + 1):
-                logits(i + 1)
+            has_kd = 0 <= kd <= LASTK
+            has_kdd = 0 <= kd - 1 <= LASTK
+            nb = b + 1 if (0 <= b and b + 1 < B) else None
+            pb = b - 1 if 1 <= b < B else None
+            if live(i + LEAD + 1):
+                logits(i + LEAD + 1)
             if live(i - 1):
                 flip(i - 1)
             if r == 2 and has_kd:
-                sums(kd)
-            if live(i):
-                maxima(i)
-            if r == 1 and has_kd:
+                spread(kd)
+            if r == 3 and has_kd:
+                sums(kd, 0, True)
+                sums(kd, 1, False)
+            if i == -1:
+                weights_flip()
+            if i == 2:
+                style_project(0, 0)
+                style_project(0, 1)
+            if nb is not None and ib == J + 3:
+                style_project(nb, 0)
+                style_project(nb, 1)
+            if live(i + LEAD):
+                max_half(i + LEAD, 0)
+                max_half(i + LEAD, 1)
+            if live(i - 2):
+                if r == 3:
+                    regroup(i - 2, slice(0, 1), False)
+                else:
+                    regroup(i - 2, BOTH, False)
+            if r == 3 and has_kd:
                 spread_out(kd)
-            if r != 1 and live(i - 2):
-                regroup(i - 2, False)
-            inter = ib == 9 and b < B
-            if inter and b >= 1:
-                stats_end(b - 1)
+            if ib == J and pb is not None:
                 for j in range(4):
-                    finish(b - 1, 1024 * j, 1024 * (j + 1))
+                    fin_sqrt(pb, 1024 * j, 1024 * (j + 1))
+            if ib == J + 5 and nb is not None:
+                style_round(nb)
+            if i == 4:
+                style_round(0)
+            if r == 0 and has_kdd:
+                moments(kd - 1, False)
+            if r == 1 and has_kd:
+                den_recip(kd)
+            if r == 2 and has_kd:
+                quant(kd, 0)
+                quant(kd, 1)
+            if r == 3 and live(i - 2):
+                regroup(i - 2, slice(1, 2), True)
+            if i == -2:
+                weights_sort()
+            if i == -1:
+                style_regroup(0, 0, False)
+                style_regroup(0, 1, True)
+            if i == 0:
+                weights_out()
+            if i == 1:
+                style_words(0, 0)
+                weights_quant()
+                style_words(0, 1)
+            if i == 3:
+                style_bias(0, 0)
+                style_bias(0, 1)
+            if i == 5:
+                style_quant(0)
+            if live(i + LEAD):
+                max_join(i + LEAD)
+            if False:
+                stats_chunk(b, ib // GROUP)
+            if nb is not None:
+                if ib == 2:
+                    load_s(nb)
+                    load_qk(nb, N)
+                    load_c(nb)
+                if ib == 4:
+                    style_regroup(nb, 0, False)
+                    style_regroup(nb, 1, False)
+                if ib == J:
+                    style_words(nb, 0)
+                    style_words(nb, 1)
+                if ib == J + 4:
+                    style_bias(nb, 0)
+                    style_bias(nb, 1)
+                if ib == J + 7:
+                    style_quant(nb)
+            if ib == J and 0 <= b < B:
+                for j in range(8):
+                    stats_chunk(b, j)
+            if pb is not None:
+                if ib == J - 1:
+                    stats_end(pb)
+                if J + 1 <= ib <= J + 8:
+                    j = ib - J - 1
+                    fin_scale(pb, GN * j, GN * (j + 1))
+                    fin_add(pb, GN * j, GN * (j + 1), False)
             if live(i):
                 exps(i)
-            if r == 0 and has_kd:
-                recip(kd)
-                regroup(i - 1, True)
-                spread(kd)
-            if r == 1 and has_kd:
-                quant(kd)
-            if r == 2 and live(i):
-                stats_chunk(b, ib // GROUP)
-            if r == 3 and has_kd:
-                moments(kd)
-            if i == 3:
-                style(0)
-            if i == 4:
-                style_quant(0)
-            if ib == 2 and b + 1 < B:
-                load_s(b + 1)
-                load_qk(b + 1, N)
-                load_c(b + 1)
-            if ib == 5 and b + 1 < B:
-                style_regroup(b + 1)
-            if inter and b + 1 < B:
-                style(b + 1)
-            if ib == 10 and b + 1 < B:
-                style_quant(b + 1)
-        stats_end(B - 1)
-        for j in range(4):
-            finish(B - 1, 1024 * j, 1024 * (j + 1))
+        LB = B - 1
+        flip(UNITS - 1)
+        regroup(UNITS - 2, BOTH, False)
+        den_recip(LASTK)
+        spread(LASTK)
+        moments(LASTK - 1, False)
+        regroup(UNITS - 1, slice(0, 1), False)
+        regroup(UNITS - 1, slice(1, 2), True)
+        spread_out(LASTK)
+        stats_end(LB)
+        quant(LASTK, 1)
+        quant(LASTK, 0)
+        sums(LASTK, 1, True)
+        sums(LASTK, 0, False)
+        for j in range(6):
+            fin_sqrt(LB, GN * j, GN * (j + 1))
+        for j in range(2):
+            fin_scale(LB, GN * j, GN * (j + 1))
+            fin_add(LB, GN * j, GN * (j + 1), False)
+        moments(LASTK, True)
+        for j in range(2, 8):
+            if j >= 6:
+                fin_sqrt(LB, GN * j, GN * (j + 1))
+            fin_scale(LB, GN * j, GN * (j + 1))
+            fin_add(LB, GN * j, GN * (j + 1), j % 2 == 1)

@@ -323,9 +323,7 @@ def tile_adaattn3dstylizer_pb_t_kernel(tc, qp, kp, s, Ws, bs_, c, out):
                 max_half(i + LEAD, 0)
                 max_half(i + LEAD, 1)
             if live(i - 2):
-                if r == 3:
-                    regroup(i - 2, slice(0, 1), False)
-                else:
+                if r != 3:
                     regroup(i - 2, BOTH, False)
             if r == 3 and has_kd:
                 spread_out(kd)
@@ -344,7 +342,7 @@ def tile_adaattn3dstylizer_pb_t_kernel(tc, qp, kp, s, Ws, bs_, c, out):
                 quant(kd, 0)
                 quant(kd, 1)
             if r == 3 and live(i - 2):
-                regroup(i - 2, slice(1, 2), True)
+                regroup(i - 2, BOTH, True)
             if i == -2:
                 weights_sort()
             if i == -1:

@@ -59,7 +59,10 @@ def tile_adaattn3dstylizer_pb_t_kernel(tc, qp, kp, s, Ws, bs_, c, out):
 
         def weights_sort():
             T["ws_pl"] = sb.tile([P, 4, P], BF16, name="ws_pl")
-            nc.vector.tensor_copy(out=T["ws_pl"][:], in_=T["ws"][:].rearrange("v (p j) -> v j p", j=4))
+            nc.gpsimd.tensor_scalar(
+                out=T["ws_pl"][:], in0=T["ws"][:].rearrange("v (p j) -> v j p", j=4),
+                scalar1=1.0, scalar2=0.0, op0=ALU.mult, op1=ALU.add,
+            )
 
         def weights_flip():
             T["wt_ps"] = ps.tile([P, 4, P], BF16, name="wt_ps", tag="xt", bufs=XTBUFS)
@@ -68,7 +71,7 @@ def tile_adaattn3dstylizer_pb_t_kernel(tc, qp, kp, s, Ws, bs_, c, out):
 
         def weights_out():
             T["ws_g"] = sb.tile([P, V, 4], BF16, name="ws_g", align_bytes=64)
-            nc.vector.tensor_copy(out=T["ws_g"][:], in_=T["wt_ps"][:].rearrange("p j v -> p v j"))
+            nc.scalar.copy(out=T["ws_g"][:], in_=T["wt_ps"][:].rearrange("p j v -> p v j"))
 
         def weights_quant():
             T["ws_w"] = sb.tile([P, V], U32, name="ws_w", align_bytes=64)
@@ -101,7 +104,7 @@ def tile_adaattn3dstylizer_pb_t_kernel(tc, qp, kp, s, Ws, bs_, c, out):
             )
 
         def style_project(b, g):
-            T["sp_ps", b, g] = ps.tile([P, 4, V], F32, name="sp_ps", tag="acc", bufs=2)
+            T["sp_ps", b, g] = ps.tile([P, 4, V], F32, name="sp_ps", tag="misc", bufs=1)
             for t in range(4):
                 cols = slice(P * (4 * g + t), P * (4 * g + t + 1))
                 nc.tensor.matmul_mx(
@@ -119,20 +122,21 @@ def tile_adaattn3dstylizer_pb_t_kernel(tc, qp, kp, s, Ws, bs_, c, out):
                 in1=T["bs"][:].unsqueeze(2).to_broadcast([P, V, 4]), op=ALU.add,
             )
 
-        def style_round(b):
-            T["sp_g", b] = sb.tile([P, 2, 2 * V * 4], BF16, name="sp_g", tag="sp_g", align_bytes=64)
-            flat = T["sp_f", b][:].rearrange("p g v t -> p (g v t)")
+        def style_round(b, g):
+            if g == 0:
+                T["sp_g", b] = sb.tile([P, 2, 2, V * 4], BF16, name="sp_g", tag="sp_g", align_bytes=64)
+            flat = T["sp_f", b][:, g].rearrange("p v t -> p (v t)")
             nc.gpsimd.tensor_scalar(
-                out=T["sp_g", b][:, 0, :], in0=flat, scalar1=1.0, scalar2=0.0, op0=ALU.mult, op1=ALU.add
+                out=T["sp_g", b][:, 0, g, :], in0=flat, scalar1=1.0, scalar2=0.0, op0=ALU.mult, op1=ALU.add
             )
-            nc.scalar.activation(out=T["sp_g", b][:, 1, :], in_=flat, func=ACT.Square)
+            nc.scalar.activation(out=T["sp_g", b][:, 1, g, :], in_=flat, func=ACT.Square)
 
         def style_quant(b):
             T["sp_w", b] = sb.tile([P, 4 * V], U32, name="sp_w", tag="sp_w", bufs=2, align_bytes=64)
             T["sp_s", b] = sb.tile([P, 4 * V], U8, name="sp_s", tag="sp_s", bufs=2, align_bytes=64)
             nc.vector.quantize_mx(
                 out=T["sp_w", b][:].bitcast(FP8X4), scales=T["sp_s", b][:],
-                in_=T["sp_g", b][:].rearrange("p q x -> p (q x)"),
+                in_=T["sp_g", b][:].rearrange("p q g x -> p (q g x)"),
             )
 
         def stats_chunk(b, i):
@@ -143,11 +147,17 @@ def tile_adaattn3dstylizer_pb_t_kernel(tc, qp, kp, s, Ws, bs_, c, out):
         def stats_end(b):
             mv = sb.tile([P, 2], F32, name="mv", tag="mv", bufs=2)
             nc.vector.bn_aggr(out=mv[:], in_=T["stats", b][:].rearrange("p a b -> p (a b)"))
+            negmu = sb.tile([P, 1], F32, name="negmu", tag="negmu", bufs=2)
+            nc.vector.tensor_scalar_mul(out=negmu[:], in0=mv[:, 0:1], scalar1=-1.0)
             ve = sb.tile([P, 1], F32, name="ve", tag="ve", bufs=2)
             nc.vector.tensor_scalar_add(out=ve[:], in0=mv[:, 1:2], scalar1=EPS)
-            rstd2 = sb.tile([P, 1], F32, name="rstd2", tag="rstd2", bufs=2)
-            nc.vector.reciprocal(out=rstd2[:], in_=ve[:])
-            T["mv", b], T["rstd2", b] = mv, rstd2
+            T["mv", b], T["negmu", b], T["ve", b] = mv, negmu, ve
+
+        def stats_rstd(b):
+            sd = sb.tile([P, 1], F32, name="sd", tag="sd", bufs=2)
+            nc.scalar.activation(out=sd[:], in_=T["ve", b][:], func=ACT.Sqrt)
+            T["rstd", b] = sb.tile([P, 1], F32, name="rstd", tag="rstd", bufs=2)
+            nc.vector.reciprocal(out=T["rstd", b][:], in_=sd[:])
 
         def logits(i):
             b, n0 = i // UNITS_B, P * (i % UNITS_B)
@@ -259,20 +269,24 @@ def tile_adaattn3dstylizer_pb_t_kernel(tc, qp, kp, s, Ws, bs_, c, out):
 
         def fin_sqrt(b, lo, hi):
             x = T["varc", b][:, lo:hi]
-            nc.scalar.activation(out=x, in_=x, func=ACT.Sqrt, scale=T["rstd2", b][:, 0:1])
+            nc.scalar.activation(out=x, in_=x, func=ACT.Sqrt)
 
-        def fin_scale(b, lo, hi):
-            x = T["varc", b][:, lo:hi]
-            nc.vector.scalar_tensor_tensor(
-                out=x, in0=T["c", b][:, lo:hi], scalar=T["mv", b][:, 0:1], in1=x,
-                op0=ALU.subtract, op1=ALU.mult,
-            )
-
-        def fin_add(b, lo, hi, on_vector):
-            x, mean = T["varc", b][:, lo:hi], T["mean", b][:, lo:hi]
+        def fin_rest(b, lo, hi, on_vector):
+            x, mean, cc = T["varc", b][:, lo:hi], T["mean", b][:, lo:hi], T["c", b][:, lo:hi]
             if on_vector:
-                nc.vector.tensor_tensor(out=mean, in0=x, in1=mean, op=ALU.add)
+                nc.vector.scalar_tensor_tensor(
+                    out=x, in0=cc, scalar=T["mv", b][:, 0:1], in1=x, op0=ALU.subtract, op1=ALU.mult
+                )
+                nc.vector.scalar_tensor_tensor(
+                    out=mean, in0=x, scalar=T["rstd", b][:, 0:1], in1=mean, op0=ALU.mult, op1=ALU.add
+                )
             else:
+                cn = sb.tile([P, GN], F32, name="cn", tag="cn", bufs=2)
+                nc.gpsimd.tensor_scalar(
+                    out=cn[:, 0 : hi - lo], in0=cc, scalar1=T["negmu", b][:, 0:1], scalar2=T["rstd", b][:, 0:1],
+                    op0=ALU.add, op1=ALU.mult,
+                )
+                nc.gpsimd.tensor_tensor(out=x, in0=cn[:, 0 : hi - lo], in1=x, op=ALU.mult)
                 nc.gpsimd.tensor_tensor(out=mean, in0=x, in1=mean, op=ALU.add)
             nc.sync.dma_start(out=out[b][:, lo:hi], in_=mean)
 
@@ -293,76 +307,86 @@ def tile_adaattn3dstylizer_pb_t_kernel(tc, qp, kp, s, Ws, bs_, c, out):
         def live(i):
             return 0 <= i < UNITS
 
+        def group_ok(k):
+            return 0 <= k <= LASTK
+
         LASTK = UNITS // GROUP - 1
         J = 10
         for i in range(-LEAD - 1, UNITS):
             r, kd = i % GROUP, i // GROUP - 1
             b, ib = i // UNITS_B, i % UNITS_B
-            has_kd = 0 <= kd <= LASTK
-            has_kdd = 0 <= kd - 1 <= LASTK
+            gi = ib // GROUP
             nb = b + 1 if (0 <= b and b + 1 < B) else None
             pb = b - 1 if 1 <= b < B else None
+            split = ((i - 2) // GROUP) % 1 < 0
             if live(i + LEAD + 1):
                 logits(i + LEAD + 1)
             if live(i - 1):
                 flip(i - 1)
-            if r == 2 and has_kd:
+            if r == 2 and group_ok(kd):
                 spread(kd)
-            if r == 3 and has_kd:
+            if r == 3 and group_ok(kd):
                 sums(kd, 0, True)
                 sums(kd, 1, False)
             if i == -1:
                 weights_flip()
-            if i == 2:
+            if i == 3:
                 style_project(0, 0)
-                style_project(0, 1)
-            if nb is not None and ib == J + 3:
-                style_project(nb, 0)
-                style_project(nb, 1)
+            if nb is not None and r == 0 and gi in (4, 5):
+                style_project(nb, gi - 4)
             if live(i + LEAD):
                 max_half(i + LEAD, 0)
                 max_half(i + LEAD, 1)
             if live(i - 2):
-                if r != 3:
+                if r == 3:
+                    if split:
+                        regroup(i - 2, slice(0, 1), False)
+                else:
                     regroup(i - 2, BOTH, False)
-            if r == 3 and has_kd:
+            if r == 3 and group_ok(kd):
                 spread_out(kd)
             if ib == J and pb is not None:
                 for j in range(4):
                     fin_sqrt(pb, 1024 * j, 1024 * (j + 1))
-            if ib == J + 5 and nb is not None:
-                style_round(nb)
-            if i == 4:
-                style_round(0)
-            if r == 0 and has_kdd:
+            if i == 0:
+                weights_out()
+            if r == 0 and group_ok(kd - 1):
                 moments(kd - 1, False)
-            if r == 1 and has_kd:
+            if r == 1 and group_ok(kd):
                 den_recip(kd)
-            if r == 2 and has_kd:
+            if r == 2 and group_ok(kd):
                 quant(kd, 0)
                 quant(kd, 1)
             if r == 3 and live(i - 2):
-                regroup(i - 2, BOTH, True)
+                regroup(i - 2, slice(1, 2) if split else BOTH, True)
             if i == -2:
                 weights_sort()
-            if i == -1:
                 style_regroup(0, 0, False)
-                style_regroup(0, 1, True)
-            if i == 0:
-                weights_out()
+                style_regroup(0, 1, False)
             if i == 1:
-                style_words(0, 0)
                 weights_quant()
+            if i == 2:
+                style_words(0, 0)
                 style_words(0, 1)
-            if i == 3:
+            if i == 4:
                 style_bias(0, 0)
-                style_bias(0, 1)
+                style_project(0, 1)
             if i == 5:
-                style_quant(0)
+                style_bias(0, 1)
+                style_round(0, 0)
+            if i == 6:
+                style_round(0, 1)
+            if nb is not None and r == 1:
+                if gi in (2, 3):
+                    style_words(nb, gi - 2)
+                if gi in (4, 5):
+                    style_bias(nb, gi - 4)
+                if gi == 6:
+                    style_quant(nb)
+            if nb is not None and r == 3 and gi in (4, 5):
+                style_round(nb, gi - 4)
             if live(i + LEAD):
                 max_join(i + LEAD)
-            if False:
-                stats_chunk(b, ib // GROUP)
             if nb is not None:
                 if ib == 2:
                     load_s(nb)
@@ -371,26 +395,20 @@ def tile_adaattn3dstylizer_pb_t_kernel(tc, qp, kp, s, Ws, bs_, c, out):
                 if ib == 4:
                     style_regroup(nb, 0, False)
                     style_regroup(nb, 1, False)
-                if ib == J:
-                    style_words(nb, 0)
-                    style_words(nb, 1)
-                if ib == J + 4:
-                    style_bias(nb, 0)
-                    style_bias(nb, 1)
-                if ib == J + 7:
-                    style_quant(nb)
-            if ib == J and 0 <= b < B:
-                for j in range(8):
+            if ib == J and pb is not None:
+                for j in range(0 if pb == 0 else 4, 8):
+                    stats_chunk(pb, j)
+                stats_end(pb)
+                stats_rstd(pb)
+                for j in range(4 if b + 1 < B else 8):
                     stats_chunk(b, j)
-            if pb is not None:
-                if ib == J - 1:
-                    stats_end(pb)
-                if J + 1 <= ib <= J + 8:
-                    j = ib - J - 1
-                    fin_scale(pb, GN * j, GN * (j + 1))
-                    fin_add(pb, GN * j, GN * (j + 1), False)
+            if pb is not None and ib > J and (ib - J) % 2 == 1 and (ib - J) // 2 < 8:
+                j = (ib - J) // 2
+                fin_rest(pb, GN * j, GN * (j + 1), False)
             if live(i):
                 exps(i)
+            if i == 6:
+                style_quant(0)
         LB = B - 1
         flip(UNITS - 1)
         regroup(UNITS - 2, BOTH, False)
@@ -405,14 +423,13 @@ def tile_adaattn3dstylizer_pb_t_kernel(tc, qp, kp, s, Ws, bs_, c, out):
         quant(LASTK, 0)
         sums(LASTK, 1, True)
         sums(LASTK, 0, False)
+        stats_rstd(LB)
         for j in range(6):
             fin_sqrt(LB, GN * j, GN * (j + 1))
-        for j in range(2):
-            fin_scale(LB, GN * j, GN * (j + 1))
-            fin_add(LB, GN * j, GN * (j + 1), False)
+        for j in range(3):
+            fin_rest(LB, GN * j, GN * (j + 1), j > 0)
         moments(LASTK, True)
-        for j in range(2, 8):
+        for j in range(3, 8):
             if j >= 6:
                 fin_sqrt(LB, GN * j, GN * (j + 1))
-            fin_scale(LB, GN * j, GN * (j + 1))
-            fin_add(LB, GN * j, GN * (j + 1), j % 2 == 1)
+            fin_rest(LB, GN * j, GN * (j + 1), j not in (3, 4))

@@ -104,7 +104,7 @@ def tile_adaattn3dstylizer_pb_t_kernel(tc, qp, kp, s, Ws, bs_, c, out):
             )
 
         def style_project(b, g):
-            T["sp_ps", b, g] = ps.tile([P, 4, V], F32, name="sp_ps", tag="misc", bufs=1)
+            T["sp_ps", b, g] = ps.tile([P, 4, V], F32, name="sp_ps", tag="acc1", bufs=1)
             for t in range(4):
                 cols = slice(P * (4 * g + t), P * (4 * g + t + 1))
                 nc.tensor.matmul_mx(
@@ -211,13 +211,13 @@ def tile_adaattn3dstylizer_pb_t_kernel(tc, qp, kp, s, Ws, bs_, c, out):
             T["r4", k] = sb.tile([P, GROUP], F32, name="r4", tag="r4", bufs=2)
             nc.vector.reciprocal(out=T["r4", k][:], in_=T["dens", k][:])
 
-        def spread(k):
-            T["rb_ps", k] = ps.tile([P, GN], F32, name="rb_ps", tag="misc", bufs=1)
-            for u in range(GROUP):
-                nc.tensor.transpose(
-                    T["rb_ps", k][:, P * u : P * (u + 1)],
-                    T["r4", k][:, u : u + 1].to_broadcast([P, P]), ident_f[:],
-                )
+        def spread(k, u):
+            if u == 0:
+                T["rb_ps", k] = ps.tile([P, GN], F32, name="rb_ps", tag="misc", bufs=1)
+            nc.tensor.matmul(
+                T["rb_ps", k][:, P * u : P * (u + 1)],
+                lhsT=T["r4", k][:, u : u + 1].to_broadcast([P, P]), rhs=ident_f[:], start=True, stop=True,
+            )
 
         def spread_out(k):
             T["rb", k] = sb.tile([P, GN], F32, name="rb", tag="rb", bufs=2)
@@ -232,37 +232,41 @@ def tile_adaattn3dstylizer_pb_t_kernel(tc, qp, kp, s, Ws, bs_, c, out):
                 in_=T["e_g", k][:, g].rearrange("p n t -> p (n t)"),
             )
 
-        def sums(k, g, first):
+        def sums(k, q, g):
             b = k // GROUPS_B
-            for q in range(2):
-                if first:
-                    T["acc", k, q] = ps.tile([P, GN], F32, name="acc", tag="acc", bufs=2)
-                cols = slice(V * (2 * q + g), V * (2 * q + g + 1))
-                nc.tensor.matmul_mx(
-                    out=T["acc", k, q][:],
-                    lhsT=T["sp_w", b][:, cols].bitcast(FP8X4), lhsT_scale=T["sp_s", b][:, cols],
-                    rhs=T["e_w", k][:, g, :].bitcast(FP8X4), rhs_scale=T["e_s", k][:, g, :],
-                    start=first, stop=not first,
-                )
+            if g == 0:
+                T["acc", k, q] = ps.tile([P, GN], F32, name="acc", tag="acc%d" % q, bufs=1)
+            cols = slice(V * (2 * q + g), V * (2 * q + g + 1))
+            nc.tensor.matmul_mx(
+                out=T["acc", k, q][:],
+                lhsT=T["sp_w", b][:, cols].bitcast(FP8X4), lhsT_scale=T["sp_s", b][:, cols],
+                rhs=T["e_w", k][:, g, :].bitcast(FP8X4), rhs_scale=T["e_s", k][:, g, :],
+                start=(g == 0), stop=(g == 1),
+            )
 
-        def moments(k, on_vector):
+        def mom_mean(k, on_vector):
             b, ns = k // GROUPS_B, slice(GN * (k % GROUPS_B), GN * (k % GROUPS_B + 1))
             if k % GROUPS_B == 0:
                 T["mean", b] = sb.tile([P, N], F32, name="mean_b", tag="mean_b", bufs=2)
                 T["varc", b] = sb.tile([P, N], F32, name="varc_b", tag="varc_b", bufs=2)
             mean = T["mean", b][:, ns]
             nc.vector.tensor_tensor(out=mean, in0=T["acc", k, 0][:], in1=T["rb", k][:], op=ALU.mult)
+            T["m2", k] = sb.tile([P, GN], F32, name="m2", tag="m2", bufs=2)
+            if on_vector:
+                nc.scalar.activation(out=T["m2", k][:], in_=mean, func=ACT.Square)
+            else:
+                nc.gpsimd.tensor_tensor(out=T["m2", k][:], in0=mean, in1=mean, op=ALU.mult)
+
+        def mom_var(k, on_vector):
+            b, ns = k // GROUPS_B, slice(GN * (k % GROUPS_B), GN * (k % GROUPS_B + 1))
             msq = sb.tile([P, GN], F32, name="msq", tag="msq", bufs=2)
             nc.vector.tensor_tensor(out=msq[:], in0=T["acc", k, 1][:], in1=T["rb", k][:], op=ALU.mult)
-            m2 = sb.tile([P, GN], F32, name="m2", tag="m2", bufs=2)
             var = sb.tile([P, GN], F32, name="var", tag="var", bufs=2)
             if on_vector:
-                nc.scalar.activation(out=m2[:], in_=mean, func=ACT.Square)
-                nc.vector.tensor_tensor(out=var[:], in0=msq[:], in1=m2[:], op=ALU.subtract)
+                nc.vector.tensor_tensor(out=var[:], in0=msq[:], in1=T["m2", k][:], op=ALU.subtract)
                 nc.vector.tensor_scalar_max(out=T["varc", b][:, ns], in0=var[:], scalar1=0.0)
             else:
-                nc.gpsimd.tensor_tensor(out=m2[:], in0=mean, in1=mean, op=ALU.mult)
-                nc.gpsimd.tensor_tensor(out=var[:], in0=msq[:], in1=m2[:], op=ALU.subtract)
+                nc.gpsimd.tensor_tensor(out=var[:], in0=msq[:], in1=T["m2", k][:], op=ALU.subtract)
                 nc.gpsimd.tensor_scalar(
                     out=T["varc", b][:, ns], in0=var[:], scalar1=3.0e38, scalar2=0.0, op0=ALU.min, op1=ALU.max
                 )
@@ -311,54 +315,52 @@ def tile_adaattn3dstylizer_pb_t_kernel(tc, qp, kp, s, Ws, bs_, c, out):
             return 0 <= k <= LASTK
 
         LASTK = UNITS // GROUP - 1
-        J = 10
+        J = 14
         for i in range(-LEAD - 1, UNITS):
-            r, kd = i % GROUP, i // GROUP - 1
+            r = i % GROUP
             b, ib = i // UNITS_B, i % UNITS_B
             gi = ib // GROUP
             nb = b + 1 if (0 <= b and b + 1 < B) else None
             pb = b - 1 if 1 <= b < B else None
-            split = ((i - 2) // GROUP) % 1 < 0
             if live(i + LEAD + 1):
                 logits(i + LEAD + 1)
             if live(i - 1):
                 flip(i - 1)
-            if r == 2 and group_ok(kd):
-                spread(kd)
-            if r == 3 and group_ok(kd):
-                sums(kd, 0, True)
-                sums(kd, 1, False)
+            if group_ok((i - 8) // GROUP):
+                sums((i - 8) // GROUP, r // 2, r % 2)
             if i == -1:
                 weights_flip()
             if i == 3:
                 style_project(0, 0)
-            if nb is not None and r == 0 and gi in (4, 5):
+            if i == 4:
+                style_project(0, 1)
+            if nb is not None and r == 1 and gi in (4, 5):
                 style_project(nb, gi - 4)
             if live(i + LEAD):
                 max_half(i + LEAD, 0)
                 max_half(i + LEAD, 1)
-            if live(i - 2):
-                if r == 3:
-                    if split:
-                        regroup(i - 2, slice(0, 1), False)
-                else:
-                    regroup(i - 2, BOTH, False)
-            if r == 3 and group_ok(kd):
-                spread_out(kd)
+            if r == 1 and group_ok((i - 9) // GROUP):
+                spread_out((i - 9) // GROUP)
+            if group_ok((i - 5) // GROUP):
+                spread((i - 5) // GROUP, (i - 5) % GROUP)
+            if live(i - 2) and r != 1:
+                regroup(i - 2, BOTH, False)
             if ib == J and pb is not None:
                 for j in range(4):
                     fin_sqrt(pb, 1024 * j, 1024 * (j + 1))
             if i == 0:
                 weights_out()
-            if r == 0 and group_ok(kd - 1):
-                moments(kd - 1, False)
-            if r == 1 and group_ok(kd):
-                den_recip(kd)
-            if r == 2 and group_ok(kd):
-                quant(kd, 0)
-                quant(kd, 1)
-            if r == 3 and live(i - 2):
-                regroup(i - 2, slice(1, 2) if split else BOTH, True)
+            if r == 0 and group_ok((i - 4) // GROUP):
+                den_recip((i - 4) // GROUP)
+            if r == 0 and group_ok((i - 12) // GROUP):
+                mom_var((i - 12) // GROUP, False)
+            if r == 1 and live(i - 2):
+                regroup(i - 2, BOTH, True)
+            if r == 2 and group_ok((i - 6) // GROUP):
+                quant((i - 6) // GROUP, 0)
+                quant((i - 6) // GROUP, 1)
+            if r == 3 and group_ok((i - 11) // GROUP):
+                mom_mean((i - 11) // GROUP, False)
             if i == -2:
                 weights_sort()
                 style_regroup(0, 0, False)
@@ -370,21 +372,20 @@ def tile_adaattn3dstylizer_pb_t_kernel(tc, qp, kp, s, Ws, bs_, c, out):
                 style_words(0, 1)
             if i == 4:
                 style_bias(0, 0)
-                style_project(0, 1)
             if i == 5:
                 style_bias(0, 1)
                 style_round(0, 0)
             if i == 6:
                 style_round(0, 1)
-            if nb is not None and r == 1:
+            if nb is not None and r == 1 and gi in (4, 5):
+                style_bias(nb, gi - 4)
+            if nb is not None and r == 3:
                 if gi in (2, 3):
                     style_words(nb, gi - 2)
-                if gi in (4, 5):
-                    style_bias(nb, gi - 4)
                 if gi == 6:
                     style_quant(nb)
-            if nb is not None and r == 3 and gi in (4, 5):
-                style_round(nb, gi - 4)
+            if nb is not None and r == 1 and gi in (5, 6):
+                style_round(nb, gi - 5)
             if live(i + LEAD):
                 max_join(i + LEAD)
             if nb is not None:
@@ -405,31 +406,42 @@ def tile_adaattn3dstylizer_pb_t_kernel(tc, qp, kp, s, Ws, bs_, c, out):
             if pb is not None and ib > J and (ib - J) % 2 == 1 and (ib - J) // 2 < 8:
                 j = (ib - J) // 2
                 fin_rest(pb, GN * j, GN * (j + 1), False)
+            if i == UNITS - 2:
+                stats_end(B - 1)
             if live(i):
                 exps(i)
-            if i == 6:
+            if i == 7:
                 style_quant(0)
-        LB = B - 1
+        LB, KA, KB = B - 1, LASTK - 1, LASTK
         flip(UNITS - 1)
+        spread(KA, 3)
+        mom_var(KA - 1, False)
+        den_recip(KB)
         regroup(UNITS - 2, BOTH, False)
-        den_recip(LASTK)
-        spread(LASTK)
-        moments(LASTK - 1, False)
         regroup(UNITS - 1, slice(0, 1), False)
         regroup(UNITS - 1, slice(1, 2), True)
-        spread_out(LASTK)
-        stats_end(LB)
-        quant(LASTK, 1)
-        quant(LASTK, 0)
-        sums(LASTK, 1, True)
-        sums(LASTK, 0, False)
+        for p in range(4):
+            sums(KA, p // 2, p % 2)
+        spread_out(KA)
+        quant(KB, 1)
+        quant(KB, 0)
+        for u in range(GROUP):
+            spread(KB, u)
+        mom_mean(KA, True)
+        mom_var(KA, True)
+        spread_out(KB)
+        for p in range(4):
+            sums(KB, p // 2, p % 2)
         stats_rstd(LB)
-        for j in range(6):
+        for j in range(7):
             fin_sqrt(LB, GN * j, GN * (j + 1))
         for j in range(3):
-            fin_rest(LB, GN * j, GN * (j + 1), j > 0)
-        moments(LASTK, True)
-        for j in range(3, 8):
-            if j >= 6:
-                fin_sqrt(LB, GN * j, GN * (j + 1))
-            fin_rest(LB, GN * j, GN * (j + 1), j not in (3, 4))
+            fin_rest(LB, GN * j, GN * (j + 1), False)
+        fin_rest(LB, GN * 3, GN * 4, True)
+        mom_mean(KB, True)
+        fin_rest(LB, GN * 4, GN * 5, True)
+        mom_var(KB, True)
+        fin_rest(LB, GN * 5, GN * 6, True)
+        fin_sqrt(LB, GN * 7, GN * 8)
+        fin_rest(LB, GN * 6, GN * 7, True)
+        fin_rest(LB, GN * 7, GN * 8, True)

@@ -21,8 +21,8 @@ UNITS_B = N // P
 GROUPS_B = UNITS_B // GROUP
 UNITS = B * UNITS_B
 FLOPS = 2 * B * (V * VI * M + C * M * N + 2 * V * M * N)
-LEAD = 2
-TBUFS = 5
+LEAD = 3
+TBUFS = 6
 LGBUFS = 3
 XTBUFS = 2
 
@@ -104,7 +104,7 @@ def tile_adaattn3dstylizer_pb_t_kernel(tc, qp, kp, s, Ws, bs_, c, out):
             )
 
         def style_project(b, g):
-            T["sp_ps", b, g] = ps.tile([P, 4, V], F32, name="sp_ps", tag="acc1", bufs=1)
+            T["sp_ps", b, g] = ps.tile([P, 4, V], F32, name="sp_ps", tag="misc", bufs=1)
             for t in range(4):
                 cols = slice(P * (4 * g + t), P * (4 * g + t + 1))
                 nc.tensor.matmul_mx(
@@ -211,13 +211,13 @@ def tile_adaattn3dstylizer_pb_t_kernel(tc, qp, kp, s, Ws, bs_, c, out):
             T["r4", k] = sb.tile([P, GROUP], F32, name="r4", tag="r4", bufs=2)
             nc.vector.reciprocal(out=T["r4", k][:], in_=T["dens", k][:])
 
-        def spread(k, u):
-            if u == 0:
-                T["rb_ps", k] = ps.tile([P, GN], F32, name="rb_ps", tag="misc", bufs=1)
-            nc.tensor.matmul(
-                T["rb_ps", k][:, P * u : P * (u + 1)],
-                lhsT=T["r4", k][:, u : u + 1].to_broadcast([P, P]), rhs=ident_f[:], start=True, stop=True,
-            )
+        def spread(k):
+            T["rb_ps", k] = ps.tile([P, GN], F32, name="rb_ps", tag="misc", bufs=1)
+            for u in range(GROUP):
+                nc.tensor.transpose(
+                    T["rb_ps", k][:, P * u : P * (u + 1)],
+                    T["r4", k][:, u : u + 1].to_broadcast([P, P]), ident_f[:],
+                )
 
         def spread_out(k):
             T["rb", k] = sb.tile([P, GN], F32, name="rb", tag="rb", bufs=2)
@@ -232,41 +232,37 @@ def tile_adaattn3dstylizer_pb_t_kernel(tc, qp, kp, s, Ws, bs_, c, out):
                 in_=T["e_g", k][:, g].rearrange("p n t -> p (n t)"),
             )
 
-        def sums(k, q, g):
+        def sums(k, g, first):
             b = k // GROUPS_B
-            if g == 0:
-                T["acc", k, q] = ps.tile([P, GN], F32, name="acc", tag="acc%d" % q, bufs=1)
-            cols = slice(V * (2 * q + g), V * (2 * q + g + 1))
-            nc.tensor.matmul_mx(
-                out=T["acc", k, q][:],
-                lhsT=T["sp_w", b][:, cols].bitcast(FP8X4), lhsT_scale=T["sp_s", b][:, cols],
-                rhs=T["e_w", k][:, g, :].bitcast(FP8X4), rhs_scale=T["e_s", k][:, g, :],
-                start=(g == 0), stop=(g == 1),
-            )
+            for q in range(2):
+                if first:
+                    T["acc", k, q] = ps.tile([P, GN], F32, name="acc", tag="acc", bufs=2)
+                cols = slice(V * (2 * q + g), V * (2 * q + g + 1))
+                nc.tensor.matmul_mx(
+                    out=T["acc", k, q][:],
+                    lhsT=T["sp_w", b][:, cols].bitcast(FP8X4), lhsT_scale=T["sp_s", b][:, cols],
+                    rhs=T["e_w", k][:, g, :].bitcast(FP8X4), rhs_scale=T["e_s", k][:, g, :],
+                    start=first, stop=not first,
+                )
 
-        def mom_mean(k, on_vector):
+        def moments(k, on_vector):
             b, ns = k // GROUPS_B, slice(GN * (k % GROUPS_B), GN * (k % GROUPS_B + 1))
             if k % GROUPS_B == 0:
                 T["mean", b] = sb.tile([P, N], F32, name="mean_b", tag="mean_b", bufs=2)
                 T["varc", b] = sb.tile([P, N], F32, name="varc_b", tag="varc_b", bufs=2)
             mean = T["mean", b][:, ns]
             nc.vector.tensor_tensor(out=mean, in0=T["acc", k, 0][:], in1=T["rb", k][:], op=ALU.mult)
-            T["m2", k] = sb.tile([P, GN], F32, name="m2", tag="m2", bufs=2)
-            if on_vector:
-                nc.scalar.activation(out=T["m2", k][:], in_=mean, func=ACT.Square)
-            else:
-                nc.gpsimd.tensor_tensor(out=T["m2", k][:], in0=mean, in1=mean, op=ALU.mult)
-
-        def mom_var(k, on_vector):
-            b, ns = k // GROUPS_B, slice(GN * (k % GROUPS_B), GN * (k % GROUPS_B + 1))
             msq = sb.tile([P, GN], F32, name="msq", tag="msq", bufs=2)
             nc.vector.tensor_tensor(out=msq[:], in0=T["acc", k, 1][:], in1=T["rb", k][:], op=ALU.mult)
+            m2 = sb.tile([P, GN], F32, name="m2", tag="m2", bufs=2)
             var = sb.tile([P, GN], F32, name="var", tag="var", bufs=2)
             if on_vector:
-                nc.vector.tensor_tensor(out=var[:], in0=msq[:], in1=T["m2", k][:], op=ALU.subtract)
+                nc.scalar.activation(out=m2[:], in_=mean, func=ACT.Square)
+                nc.vector.tensor_tensor(out=var[:], in0=msq[:], in1=m2[:], op=ALU.subtract)
                 nc.vector.tensor_scalar_max(out=T["varc", b][:, ns], in0=var[:], scalar1=0.0)
             else:
-                nc.gpsimd.tensor_tensor(out=var[:], in0=msq[:], in1=T["m2", k][:], op=ALU.subtract)
+                nc.gpsimd.tensor_tensor(out=m2[:], in0=mean, in1=mean, op=ALU.mult)
+                nc.gpsimd.tensor_tensor(out=var[:], in0=msq[:], in1=m2[:], op=ALU.subtract)
                 nc.gpsimd.tensor_scalar(
                     out=T["varc", b][:, ns], in0=var[:], scalar1=3.0e38, scalar2=0.0, op0=ALU.min, op1=ALU.max
                 )
@@ -315,52 +311,54 @@ def tile_adaattn3dstylizer_pb_t_kernel(tc, qp, kp, s, Ws, bs_, c, out):
             return 0 <= k <= LASTK
 
         LASTK = UNITS // GROUP - 1
-        J = 14
+        J = 10
         for i in range(-LEAD - 1, UNITS):
-            r = i % GROUP
+            r, kd = i % GROUP, i // GROUP - 1
             b, ib = i // UNITS_B, i % UNITS_B
             gi = ib // GROUP
             nb = b + 1 if (0 <= b and b + 1 < B) else None
             pb = b - 1 if 1 <= b < B else None
-            if live(i + LEAD + 1):
-                logits(i + LEAD + 1)
+            split = ((i - 2) // GROUP) % 1 < 0
             if live(i - 1):
                 flip(i - 1)
-            if group_ok((i - 8) // GROUP):
-                sums((i - 8) // GROUP, r // 2, r % 2)
+            if live(i + LEAD + 1):
+                logits(i + LEAD + 1)
+            if r == 2 and group_ok(kd):
+                spread(kd)
+            if r == 3 and group_ok(kd):
+                sums(kd, 0, True)
+                sums(kd, 1, False)
             if i == -1:
                 weights_flip()
             if i == 3:
                 style_project(0, 0)
-            if i == 4:
-                style_project(0, 1)
-            if nb is not None and r == 1 and gi in (4, 5):
+            if nb is not None and r == 0 and gi in (4, 5):
                 style_project(nb, gi - 4)
             if live(i + LEAD):
                 max_half(i + LEAD, 0)
                 max_half(i + LEAD, 1)
-            if r == 1 and group_ok((i - 9) // GROUP):
-                spread_out((i - 9) // GROUP)
-            if group_ok((i - 5) // GROUP):
-                spread((i - 5) // GROUP, (i - 5) % GROUP)
-            if live(i - 2) and r != 1:
-                regroup(i - 2, BOTH, False)
+            if live(i - 2):
+                if r == 3:
+                    if split:
+                        regroup(i - 2, slice(0, 1), False)
+                else:
+                    regroup(i - 2, BOTH, False)
+            if r == 3 and group_ok(kd):
+                spread_out(kd)
             if ib == J and pb is not None:
                 for j in range(4):
                     fin_sqrt(pb, 1024 * j, 1024 * (j + 1))
             if i == 0:
                 weights_out()
-            if r == 0 and group_ok((i - 4) // GROUP):
-                den_recip((i - 4) // GROUP)
-            if r == 0 and group_ok((i - 12) // GROUP):
-                mom_var((i - 12) // GROUP, False)
-            if r == 1 and live(i - 2):
-                regroup(i - 2, BOTH, True)
-            if r == 2 and group_ok((i - 6) // GROUP):
-                quant((i - 6) // GROUP, 0)
-                quant((i - 6) // GROUP, 1)
-            if r == 3 and group_ok((i - 11) // GROUP):
-                mom_mean((i - 11) // GROUP, False)
+            if r == 0 and group_ok(kd - 1):
+                moments(kd - 1, False)
+            if r == 1 and group_ok(kd):
+                den_recip(kd)
+            if r == 2 and group_ok(kd):
+                quant(kd, 0)
+                quant(kd, 1)
+            if r == 3 and live(i - 2):
+                regroup(i - 2, slice(1, 2) if split else BOTH, True)
             if i == -2:
                 weights_sort()
                 style_regroup(0, 0, False)
@@ -372,20 +370,21 @@ def tile_adaattn3dstylizer_pb_t_kernel(tc, qp, kp, s, Ws, bs_, c, out):
                 style_words(0, 1)
             if i == 4:
                 style_bias(0, 0)
+                style_project(0, 1)
             if i == 5:
                 style_bias(0, 1)
                 style_round(0, 0)
             if i == 6:
                 style_round(0, 1)
-            if nb is not None and r == 1 and gi in (4, 5):
-                style_bias(nb, gi - 4)
-            if nb is not None and r == 3:
+            if nb is not None and r == 1:
                 if gi in (2, 3):
                     style_words(nb, gi - 2)
+                if gi in (4, 5):
+                    style_bias(nb, gi - 4)
                 if gi == 6:
                     style_quant(nb)
-            if nb is not None and r == 1 and gi in (5, 6):
-                style_round(nb, gi - 5)
+            if nb is not None and r == 3 and gi in (4, 5):
+                style_round(nb, gi - 4)
             if live(i + LEAD):
                 max_join(i + LEAD)
             if nb is not None:
@@ -406,42 +405,31 @@ def tile_adaattn3dstylizer_pb_t_kernel(tc, qp, kp, s, Ws, bs_, c, out):
             if pb is not None and ib > J and (ib - J) % 2 == 1 and (ib - J) // 2 < 8:
                 j = (ib - J) // 2
                 fin_rest(pb, GN * j, GN * (j + 1), False)
-            if i == UNITS - 2:
-                stats_end(B - 1)
             if live(i):
                 exps(i)
-            if i == 7:
+            if i == 6:
                 style_quant(0)
-        LB, KA, KB = B - 1, LASTK - 1, LASTK
+        LB = B - 1
         flip(UNITS - 1)
-        spread(KA, 3)
-        mom_var(KA - 1, False)
-        den_recip(KB)
         regroup(UNITS - 2, BOTH, False)
+        den_recip(LASTK)
+        spread(LASTK)
+        moments(LASTK - 1, False)
         regroup(UNITS - 1, slice(0, 1), False)
         regroup(UNITS - 1, slice(1, 2), True)
-        for p in range(4):
-            sums(KA, p // 2, p % 2)
-        spread_out(KA)
-        quant(KB, 1)
-        quant(KB, 0)
-        for u in range(GROUP):
-            spread(KB, u)
-        mom_mean(KA, True)
-        mom_var(KA, True)
-        spread_out(KB)
-        for p in range(4):
-            sums(KB, p // 2, p % 2)
+        spread_out(LASTK)
+        stats_end(LB)
+        quant(LASTK, 1)
+        quant(LASTK, 0)
+        sums(LASTK, 1, True)
+        sums(LASTK, 0, False)
         stats_rstd(LB)
-        for j in range(7):
+        for j in range(6):
             fin_sqrt(LB, GN * j, GN * (j + 1))
         for j in range(3):
-            fin_rest(LB, GN * j, GN * (j + 1), False)
-        fin_rest(LB, GN * 3, GN * 4, True)
-        mom_mean(KB, True)
-        fin_rest(LB, GN * 4, GN * 5, True)
-        mom_var(KB, True)
-        fin_rest(LB, GN * 5, GN * 6, True)
-        fin_sqrt(LB, GN * 7, GN * 8)
-        fin_rest(LB, GN * 6, GN * 7, True)
-        fin_rest(LB, GN * 7, GN * 8, True)
+            fin_rest(LB, GN * j, GN * (j + 1), j > 0)
+        moments(LASTK, True)
+        for j in range(3, 8):
+            if j >= 6:
+                fin_sqrt(LB, GN * j, GN * (j + 1))
+            fin_rest(LB, GN * j, GN * (j + 1), j not in (3, 4))

@@ -10,21 +10,19 @@ U8 = mybir.dt.uint8
 FP8X4 = mybir.dt.float8_e4m3fn_x4
 ALU = mybir.AluOpType
 ACT = mybir.ActivationFunctionType
-AX = mybir.AxisListType
 
 P = 128
 B, C, VI, V, N, M = 3, 128, 512, 128, 4096, 1024
 EPS = 1e-5
+TILES_B = N // P
+TILES = B * TILES_B
 GROUP = 4
 GN = GROUP * P
-UNITS_B = N // P
-GROUPS_B = UNITS_B // GROUP
-UNITS = B * UNITS_B
+GROUPS_B = TILES_B // GROUP
+GROUPS = TILES // GROUP
 FLOPS = 2 * B * (V * VI * M + C * M * N + 2 * V * M * N)
 LEAD = 3
-TBUFS = 6
-LGBUFS = 3
-XTBUFS = 2
+TBUFS = 7
 
 
 def tile_adaattn3dstylizer_pb_t_kernel(tc, qp, kp, s, Ws, bs_, c, out):
@@ -35,19 +33,16 @@ def tile_adaattn3dstylizer_pb_t_kernel(tc, qp, kp, s, Ws, bs_, c, out):
         ctx.enter_context(tc.manual_schedule())
         T = {}
 
-        ident_bf = sb.tile([P, P], BF16, name="ident_bf")
-        make_identity(nc, ident_bf[:])
-        ident_f = sb.tile([P, P], F32, name="ident_f")
-        make_identity(nc, ident_f[:])
+        ident = sb.tile([P, P], F32, name="ident")
 
-        def load_qk(b, first):
-            T["kp", b] = sb.tile([P, M], BF16, name="kp_sb", tag="kp", bufs=2)
+        def load_keys(b):
+            T["kp", b] = sb.tile([P, M], BF16, name="kp_raw", tag="kp_raw", bufs=2)
             nc.sync.dma_start(out=T["kp", b][:], in_=kp[b])
-            T["qp", b] = sb.tile([P, N], BF16, name="qp_sb", tag="qp", bufs=2)
-            nc.sync.dma_start(out=T["qp", b][:, 0:first], in_=qp[b][:, 0:first])
 
-        def load_rest(b, first):
-            nc.sync.dma_start(out=T["qp", b][:, first:N], in_=qp[b][:, first:N])
+        def load_queries(b, lo, hi):
+            if lo == 0:
+                T["qp", b] = sb.tile([P, N], BF16, name="qp_sb", tag="qp", bufs=2)
+            nc.sync.dma_start(out=T["qp", b][:, lo:hi], in_=qp[b][:, lo:hi])
 
         def load_s(b):
             T["s", b] = sb.tile([P, 4, M], BF16, name="s_raw", tag="s_raw", bufs=1)
@@ -57,41 +52,39 @@ def tile_adaattn3dstylizer_pb_t_kernel(tc, qp, kp, s, Ws, bs_, c, out):
             T["c", b] = sb.tile([P, N], BF16, name="c_sb", tag="c", bufs=2)
             nc.sync.dma_start(out=T["c", b][:], in_=c[b])
 
-        def weights_sort():
-            T["ws_pl"] = sb.tile([P, 4, P], BF16, name="ws_pl")
-            nc.gpsimd.tensor_scalar(
-                out=T["ws_pl"][:], in0=T["ws"][:].rearrange("v (p j) -> v j p", j=4),
-                scalar1=1.0, scalar2=0.0, op0=ALU.mult, op1=ALU.add,
+        def sort_keys(b):
+            T["ks", b] = sb.tile([P, M], BF16, name="kp_sorted", tag="kp_sorted", bufs=2)
+            nc.vector.tensor_copy(
+                out=T["ks", b][:].bitcast(F32).rearrange("c (g u p) -> c g u p", g=2, u=2),
+                in_=T["kp", b][:].bitcast(F32).rearrange("c (g p u) -> c g u p", g=2, u=2),
             )
 
         def weights_flip():
-            T["wt_ps"] = ps.tile([P, 4, P], BF16, name="wt_ps", tag="xt", bufs=XTBUFS)
-            for j in range(4):
-                nc.tensor.transpose(T["wt_ps"][:, j, :], T["ws_pl"][:, j, :], ident_bf[:])
+            words = T["ws"][:].bitcast(F32)
+            T["wt_ps"] = ps.tile([P, 2, P], F32, name="wt_ps", tag="tr", bufs=3)
+            for u in range(2):
+                nc.tensor.transpose(T["wt_ps"][:, u, :], words[:, u : 2 * P : 2], ident[:])
 
         def weights_out():
-            T["ws_g"] = sb.tile([P, V, 4], BF16, name="ws_g", align_bytes=64)
-            nc.scalar.copy(out=T["ws_g"][:], in_=T["wt_ps"][:].rearrange("p j v -> p v j"))
+            T["ws_g"] = sb.tile([P, V * 4], BF16, name="ws_g", align_bytes=64)
+            nc.scalar.copy(
+                out=T["ws_g"][:].bitcast(F32).rearrange("p (v u) -> p v u", u=2),
+                in_=T["wt_ps"][:].rearrange("p u v -> p v u"),
+            )
 
         def weights_quant():
             T["ws_w"] = sb.tile([P, V], U32, name="ws_w", align_bytes=64)
             T["ws_s"] = sb.tile([P, V], U8, name="ws_s", align_bytes=64)
-            nc.vector.quantize_mx(
-                out=T["ws_w"][:].bitcast(FP8X4), scales=T["ws_s"][:],
-                in_=T["ws_g"][:].rearrange("p v j -> p (v j)"),
-            )
+            nc.vector.quantize_mx(out=T["ws_w"][:].bitcast(FP8X4), scales=T["ws_s"][:], in_=T["ws_g"][:])
 
-        def style_regroup(b, half, on_vector):
-            if half == 0:
-                T["s_g", b] = sb.tile([P, M, 4], BF16, name="s_g", tag="s_g", align_bytes=64)
-            ms = slice(512 * half, 512 * (half + 1))
-            src = T["s", b][:, :, ms].rearrange("p j m -> p m j")
-            if on_vector:
-                nc.vector.tensor_copy(out=T["s_g", b][:, ms, :], in_=src)
-            else:
-                nc.gpsimd.tensor_scalar(
-                    out=T["s_g", b][:, ms, :], in0=src, scalar1=1.0, scalar2=0.0, op0=ALU.mult, op1=ALU.add
-                )
+        def style_regroup(b, piece):
+            if piece == 0:
+                T["s_g", b] = sb.tile([P, 2, 4, P, 4], BF16, name="s_g", tag="s_g", align_bytes=64)
+            g, t0 = piece // 2, 2 * (piece % 2)
+            src = T["s", b][:].rearrange("q j (g p t) -> q g t p j", g=2, t=4)[:, g, t0 : t0 + 2]
+            nc.gpsimd.tensor_scalar(
+                out=T["s_g", b][:, g, t0 : t0 + 2], in0=src, scalar1=1.0, scalar2=0.0, op0=ALU.mult, op1=ALU.add
+            )
 
         def style_words(b, g):
             if g == 0:
@@ -100,11 +93,11 @@ def tile_adaattn3dstylizer_pb_t_kernel(tc, qp, kp, s, Ws, bs_, c, out):
             ms = slice(512 * g, 512 * (g + 1))
             nc.vector.quantize_mx(
                 out=T["s_w", b][:, ms].bitcast(FP8X4), scales=T["s_s", b][:, ms],
-                in_=T["s_g", b][:, ms, :].rearrange("p m j -> p (m j)"),
+                in_=T["s_g", b][:, g].rearrange("q t p j -> q (t p j)"),
             )
 
         def style_project(b, g):
-            T["sp_ps", b, g] = ps.tile([P, 4, V], F32, name="sp_ps", tag="misc", bufs=1)
+            T["sp_ps", b, g] = ps.tile([P, 4, V], F32, name="sp_ps", tag="tr", bufs=3)
             for t in range(4):
                 cols = slice(P * (4 * g + t), P * (4 * g + t + 1))
                 nc.tensor.matmul_mx(
@@ -127,16 +120,16 @@ def tile_adaattn3dstylizer_pb_t_kernel(tc, qp, kp, s, Ws, bs_, c, out):
                 T["sp_g", b] = sb.tile([P, 2, 2, V * 4], BF16, name="sp_g", tag="sp_g", align_bytes=64)
             flat = T["sp_f", b][:, g].rearrange("p v t -> p (v t)")
             nc.gpsimd.tensor_scalar(
-                out=T["sp_g", b][:, 0, g, :], in0=flat, scalar1=1.0, scalar2=0.0, op0=ALU.mult, op1=ALU.add
+                out=T["sp_g", b][:, g, 0, :], in0=flat, scalar1=1.0, scalar2=0.0, op0=ALU.mult, op1=ALU.add
             )
-            nc.scalar.activation(out=T["sp_g", b][:, 1, g, :], in_=flat, func=ACT.Square)
+            nc.scalar.activation(out=T["sp_g", b][:, g, 1, :], in_=flat, func=ACT.Square)
 
         def style_quant(b):
             T["sp_w", b] = sb.tile([P, 4 * V], U32, name="sp_w", tag="sp_w", bufs=2, align_bytes=64)
             T["sp_s", b] = sb.tile([P, 4 * V], U8, name="sp_s", tag="sp_s", bufs=2, align_bytes=64)
             nc.vector.quantize_mx(
                 out=T["sp_w", b][:].bitcast(FP8X4), scales=T["sp_s", b][:],
-                in_=T["sp_g", b][:].rearrange("p q g x -> p (q g x)"),
+                in_=T["sp_g", b][:].rearrange("p g q x -> p (g q x)"),
             )
 
         def stats_chunk(b, i):
@@ -145,291 +138,290 @@ def tile_adaattn3dstylizer_pb_t_kernel(tc, qp, kp, s, Ws, bs_, c, out):
             nc.vector.bn_stats(out=T["stats", b][:, i, :], in_=T["c", b][:, 512 * i : 512 * (i + 1)])
 
         def stats_end(b):
-            mv = sb.tile([P, 2], F32, name="mv", tag="mv", bufs=2)
+            mv = sb.tile([P, 2], F32, name="mv", tag="mv", bufs=3)
             nc.vector.bn_aggr(out=mv[:], in_=T["stats", b][:].rearrange("p a b -> p (a b)"))
-            negmu = sb.tile([P, 1], F32, name="negmu", tag="negmu", bufs=2)
+            negmu = sb.tile([P, 1], F32, name="negmu", tag="negmu", bufs=3)
             nc.vector.tensor_scalar_mul(out=negmu[:], in0=mv[:, 0:1], scalar1=-1.0)
-            ve = sb.tile([P, 1], F32, name="ve", tag="ve", bufs=2)
+            ve = sb.tile([P, 1], F32, name="ve", tag="ve", bufs=3)
             nc.vector.tensor_scalar_add(out=ve[:], in0=mv[:, 1:2], scalar1=EPS)
             T["mv", b], T["negmu", b], T["ve", b] = mv, negmu, ve
 
         def stats_rstd(b):
-            sd = sb.tile([P, 1], F32, name="sd", tag="sd", bufs=2)
+            sd = sb.tile([P, 1], F32, name="sd", tag="sd", bufs=3)
             nc.scalar.activation(out=sd[:], in_=T["ve", b][:], func=ACT.Sqrt)
-            T["rstd", b] = sb.tile([P, 1], F32, name="rstd", tag="rstd", bufs=2)
+            T["rstd", b] = sb.tile([P, 1], F32, name="rstd", tag="rstd", bufs=3)
             nc.vector.reciprocal(out=T["rstd", b][:], in_=sd[:])
 
         def logits(i):
-            b, n0 = i // UNITS_B, P * (i % UNITS_B)
+            b, n0 = i // TILES_B, P * (i % TILES_B)
             for h in range(2):
-                T["lg", i, h] = ps.tile([P, 512], F32, name="lg", tag="lg", bufs=LGBUFS)
+                T["lg", i, h] = ps.tile([P, 512], F32, name="lg", tag="lg", bufs=3)
                 nc.tensor.matmul(
                     T["lg", i, h][:], lhsT=T["qp", b][:, n0 : n0 + P],
-                    rhs=T["kp", b][:, 512 * h : 512 * (h + 1)], start=True, stop=True,
+                    rhs=T["ks", b][:, 512 * h : 512 * (h + 1)], start=True, stop=True,
                 )
 
-        def max_half(i, h):
+        def negate(i, h):
             if h == 0:
-                T["mx2", i] = sb.tile([P, 2], F32, name="mx2", tag="mx2", bufs=3)
+                T["mn", i] = sb.tile([P, 2], F32, name="mn", tag="mn", bufs=TBUFS + 1)
                 T["t", i] = sb.tile([P, M], F32, name="t_sb", tag="t_sb", bufs=TBUFS)
+            mn = T["mn", i]
             nc.vector.tensor_scalar(
-                out=T["t", i][:, 512 * h : 512 * (h + 1)], in0=T["lg", i, h][:], scalar1=1.0, scalar2=None,
-                op0=ALU.mult, op1=ALU.max, accum_out=T["mx2", i][:, h : h + 1],
+                out=T["t", i][:, 512 * h : 512 * (h + 1)], in0=T["lg", i, h][:],
+                scalar1=-1.0, scalar2=None if h == 0 else mn[:, 0:1],
+                op0=ALU.mult, op1=ALU.min, accum_out=mn[:, h : h + 1],
             )
-
-        def max_join(i):
-            T["negmax", i] = sb.tile([P, 1], F32, name="negmax", tag="negmax", bufs=TBUFS)
-            nc.vector.tensor_reduce(out=T["negmax", i][:], in_=T["mx2", i][:], axis=AX.X, op=ALU.max, negate=True)
 
         def exps(i):
             k, r = i // GROUP, i % GROUP
             if r == 0:
-                T["dens", k] = sb.tile([P, GROUP], F32, name="dens", tag="dens", bufs=3)
+                T["dens", k] = sb.tile([P, GROUP], F32, name="dens", tag="dens", bufs=4)
             T["e", i] = sb.tile([P, M], BF16, name="e_sb", tag="e_sb", bufs=3)
             nc.scalar.activation(
                 out=T["e", i][:], in_=T["t", i][:], func=ACT.Exp,
-                bias=T["negmax", i][:, 0:1], scale=1.0, accum_out=T["dens", k][:, r : r + 1],
+                bias=T["mn", i][:, 1:2], scale=-1.0, accum_out=T["dens", k][:, r : r + 1],
             )
 
         def flip(i):
-            T["xt", i] = ps.tile([P, 8, P], BF16, name="xt", tag="xt", bufs=XTBUFS)
-            for j in range(8):
-                nc.tensor.transpose(T["xt", i][:, j, :], T["e", i][:, P * j : P * (j + 1)], ident_bf[:])
+            words = T["e", i][:].bitcast(F32)
+            T["xt", i] = ps.tile([P, 4, P], F32, name="xt", tag="tr", bufs=3)
+            for j in range(4):
+                nc.tensor.transpose(T["xt", i][:, j, :], words[:, P * j : P * (j + 1)], ident[:])
 
-        def regroup(i, gs, on_vector):
+        def regroup(i, on_vector):
             k, r = i // GROUP, i % GROUP
-            if ("e_g", k) not in T:
-                T["e_g", k] = sb.tile([P, 2, GN, 4], BF16, name="e_g", tag="e_g", bufs=2, align_bytes=64)
-            src = T["xt", i][:].rearrange("p (g t) n -> p g n t", g=2)[:, gs]
-            dst = T["e_g", k][:, gs, P * r : P * (r + 1), :]
+            if r == 0:
+                T["e_g", k] = sb.tile([P, GROUP, 2 * P * 4], BF16, name="e_g", tag="e_g", bufs=2, align_bytes=64)
+            src = T["xt", i][:].rearrange("p (g u) n -> p g n u", g=2)
+            dst = T["e_g", k][:, r, :].bitcast(F32).rearrange("p (g n u) -> p g n u", g=2, u=2)
             if on_vector:
                 nc.vector.tensor_copy(out=dst, in_=src)
             else:
                 nc.scalar.copy(out=dst, in_=src)
 
         def den_recip(k):
-            T["r4", k] = sb.tile([P, GROUP], F32, name="r4", tag="r4", bufs=2)
+            T["r4", k] = sb.tile([P, GROUP], F32, name="r4", tag="r4", bufs=4)
             nc.vector.reciprocal(out=T["r4", k][:], in_=T["dens", k][:])
 
-        def spread(k):
-            T["rb_ps", k] = ps.tile([P, GN], F32, name="rb_ps", tag="misc", bufs=1)
-            for u in range(GROUP):
-                nc.tensor.transpose(
-                    T["rb_ps", k][:, P * u : P * (u + 1)],
-                    T["r4", k][:, u : u + 1].to_broadcast([P, P]), ident_f[:],
-                )
-
-        def spread_out(k):
-            T["rb", k] = sb.tile([P, GN], F32, name="rb", tag="rb", bufs=2)
-            nc.scalar.copy(out=T["rb", k][:], in_=T["rb_ps", k][:])
-
-        def quant(k, g):
-            if ("e_w", k) not in T:
-                T["e_w", k] = sb.tile([P, 2, GN], U32, name="e_w", tag="e_w", bufs=2, align_bytes=64)
-                T["e_s", k] = sb.tile([P, 2, GN], U8, name="e_s", tag="e_s", bufs=2, align_bytes=64)
+        def quant(k):
+            T["e_w", k] = sb.tile([P, GROUP * 2 * P], U32, name="e_w", tag="e_w", bufs=3, align_bytes=64)
+            T["e_s", k] = sb.tile([P, GROUP * 2 * P], U8, name="e_s", tag="e_s", bufs=3, align_bytes=64)
             nc.vector.quantize_mx(
-                out=T["e_w", k][:, g, :].bitcast(FP8X4), scales=T["e_s", k][:, g, :],
-                in_=T["e_g", k][:, g].rearrange("p n t -> p (n t)"),
+                out=T["e_w", k][:].bitcast(FP8X4), scales=T["e_s", k][:],
+                in_=T["e_g", k][:].rearrange("p r x -> p (r x)"),
             )
 
-        def sums(k, g, first):
+        def sums(k, h):
             b = k // GROUPS_B
-            for q in range(2):
-                if first:
-                    T["acc", k, q] = ps.tile([P, GN], F32, name="acc", tag="acc", bufs=2)
-                cols = slice(V * (2 * q + g), V * (2 * q + g + 1))
-                nc.tensor.matmul_mx(
-                    out=T["acc", k, q][:],
-                    lhsT=T["sp_w", b][:, cols].bitcast(FP8X4), lhsT_scale=T["sp_s", b][:, cols],
-                    rhs=T["e_w", k][:, g, :].bitcast(FP8X4), rhs_scale=T["e_s", k][:, g, :],
-                    start=first, stop=not first,
-                )
+            T["ab", k, h] = ps.tile([P, 2, 2 * V], F32, name="ab", tag="ab", bufs=2)
+            for a in range(2):
+                for g in range(2):
+                    cols = slice(P * (2 * (2 * h + a) + g), P * (2 * (2 * h + a) + g + 1))
+                    vs = slice(2 * V * g, 2 * V * (g + 1))
+                    nc.tensor.matmul_mx(
+                        out=T["ab", k, h][:, a, :],
+                        lhsT=T["e_w", k][:, cols].bitcast(FP8X4), lhsT_scale=T["e_s", k][:, cols],
+                        rhs=T["sp_w", b][:, vs].bitcast(FP8X4), rhs_scale=T["sp_s", b][:, vs],
+                        start=g == 0, stop=g == 1,
+                    )
 
-        def moments(k, on_vector):
+        def means(k, h):
+            if h == 0:
+                T["mean", k] = sb.tile([P, GROUP, V], F32, name="mean", tag="mean", bufs=15)
+                T["x", k] = sb.tile([P, GN], F32, name="x", tag="x", bufs=15)
+            for a in range(2):
+                r = 2 * h + a
+                nc.scalar.activation(
+                    out=T["mean", k][:, r, :], in_=T["ab", k, h][:, a, 0:V], func=ACT.Copy,
+                    scale=T["r4", k][:, r : r + 1],
+                )
+            T["m2", k, h] = sb.tile([P, 2, V], F32, name="m2", tag="m2", bufs=3)
+            pair = T["mean", k][:, 2 * h : 2 * h + 2, :]
+            nc.gpsimd.tensor_tensor(out=T["m2", k, h][:], in0=pair, in1=pair, op=ALU.mult)
+
+        def variances(k, h):
+            x = T["x", k]
+            for a in range(2):
+                r = 2 * h + a
+                nc.vector.scalar_tensor_tensor(
+                    out=x[:, P * r : P * (r + 1)], in0=T["ab", k, h][:, a, V : 2 * V],
+                    scalar=T["r4", k][:, r : r + 1], in1=T["m2", k, h][:, a, :],
+                    op0=ALU.mult, op1=ALU.subtract,
+                )
+            pair = x[:, GN // 2 * h : GN // 2 * (h + 1)]
+            nc.gpsimd.tensor_scalar(out=pair, in0=pair, scalar1=3.0e38, scalar2=0.0, op0=ALU.min, op1=ALU.max)
+
+        def deviations(k):
+            xt = ps.tile([P, GROUP, P], F32, name="x_ps", tag="tr", bufs=3)
+            for r in range(GROUP):
+                nc.tensor.transpose(xt[:, r, :], T["x", k][:, P * r : P * (r + 1)], ident[:])
+            nc.scalar.activation(
+                out=T["x", k][:], in_=xt[:].rearrange("p r n -> p (r n)"), func=ACT.Sqrt
+            )
+
+        def final_content(k):
             b, ns = k // GROUPS_B, slice(GN * (k % GROUPS_B), GN * (k % GROUPS_B + 1))
-            if k % GROUPS_B == 0:
-                T["mean", b] = sb.tile([P, N], F32, name="mean_b", tag="mean_b", bufs=2)
-                T["varc", b] = sb.tile([P, N], F32, name="varc_b", tag="varc_b", bufs=2)
-            mean = T["mean", b][:, ns]
-            nc.vector.tensor_tensor(out=mean, in0=T["acc", k, 0][:], in1=T["rb", k][:], op=ALU.mult)
-            msq = sb.tile([P, GN], F32, name="msq", tag="msq", bufs=2)
-            nc.vector.tensor_tensor(out=msq[:], in0=T["acc", k, 1][:], in1=T["rb", k][:], op=ALU.mult)
-            m2 = sb.tile([P, GN], F32, name="m2", tag="m2", bufs=2)
-            var = sb.tile([P, GN], F32, name="var", tag="var", bufs=2)
-            if on_vector:
-                nc.scalar.activation(out=m2[:], in_=mean, func=ACT.Square)
-                nc.vector.tensor_tensor(out=var[:], in0=msq[:], in1=m2[:], op=ALU.subtract)
-                nc.vector.tensor_scalar_max(out=T["varc", b][:, ns], in0=var[:], scalar1=0.0)
+            cn = sb.tile([P, GN], F32, name="cn", tag="cn", bufs=2)
+            nc.gpsimd.tensor_scalar(
+                out=cn[:], in0=T["c", b][:, ns], scalar1=T["negmu", b][:, 0:1], scalar2=T["rstd", b][:, 0:1],
+                op0=ALU.add, op1=ALU.mult,
+            )
+            nc.gpsimd.tensor_tensor(out=T["x", k][:], in0=cn[:], in1=T["x", k][:], op=ALU.mult)
+
+        def final_flip(k):
+            T["mt", k] = ps.tile([P, GROUP, P], F32, name="m_ps", tag="tr", bufs=3)
+            for r in range(GROUP):
+                nc.tensor.transpose(T["mt", k][:, r, :], T["mean", k][:, r, :], ident[:])
+
+        def final_out(k, plain):
+            b, ns = k // GROUPS_B, slice(GN * (k % GROUPS_B), GN * (k % GROUPS_B + 1))
+            x, mt = T["x", k], T["mt", k][:].rearrange("p r n -> p (r n)")
+            if plain:
+                nc.vector.tensor_tensor(out=x[:], in0=mt, in1=x[:], op=ALU.add)
             else:
-                nc.gpsimd.tensor_tensor(out=m2[:], in0=mean, in1=mean, op=ALU.mult)
-                nc.gpsimd.tensor_tensor(out=var[:], in0=msq[:], in1=m2[:], op=ALU.subtract)
-                nc.gpsimd.tensor_scalar(
-                    out=T["varc", b][:, ns], in0=var[:], scalar1=3.0e38, scalar2=0.0, op0=ALU.min, op1=ALU.max
-                )
-
-        def fin_sqrt(b, lo, hi):
-            x = T["varc", b][:, lo:hi]
-            nc.scalar.activation(out=x, in_=x, func=ACT.Sqrt)
-
-        def fin_rest(b, lo, hi, on_vector):
-            x, mean, cc = T["varc", b][:, lo:hi], T["mean", b][:, lo:hi], T["c", b][:, lo:hi]
-            if on_vector:
                 nc.vector.scalar_tensor_tensor(
-                    out=x, in0=cc, scalar=T["mv", b][:, 0:1], in1=x, op0=ALU.subtract, op1=ALU.mult
+                    out=x[:], in0=T["c", b][:, ns], scalar=T["mv", b][:, 0:1], in1=x[:],
+                    op0=ALU.subtract, op1=ALU.mult,
                 )
                 nc.vector.scalar_tensor_tensor(
-                    out=mean, in0=x, scalar=T["rstd", b][:, 0:1], in1=mean, op0=ALU.mult, op1=ALU.add
+                    out=x[:], in0=x[:], scalar=T["rstd", b][:, 0:1], in1=mt, op0=ALU.mult, op1=ALU.add
                 )
-            else:
-                cn = sb.tile([P, GN], F32, name="cn", tag="cn", bufs=2)
-                nc.gpsimd.tensor_scalar(
-                    out=cn[:, 0 : hi - lo], in0=cc, scalar1=T["negmu", b][:, 0:1], scalar2=T["rstd", b][:, 0:1],
-                    op0=ALU.add, op1=ALU.mult,
-                )
-                nc.gpsimd.tensor_tensor(out=x, in0=cn[:, 0 : hi - lo], in1=x, op=ALU.mult)
-                nc.gpsimd.tensor_tensor(out=mean, in0=x, in1=mean, op=ALU.add)
-            nc.sync.dma_start(out=out[b][:, lo:hi], in_=mean)
+            nc.sync.dma_start(out=out[b][:, ns], in_=x[:])
 
         FIRST = 512
-        BOTH = slice(0, 2)
         warm = sb.tile([P, 1], F32, name="warm")
         nc.vector.memset(warm[:], 0.0)
         nc.scalar.activation(out=warm[:], in_=warm[:], func=ACT.Exp)
-        load_qk(0, FIRST)
+        load_keys(0)
+        load_queries(0, 0, FIRST)
         T["ws"] = sb.tile([P, VI], BF16, name="ws_sb")
         nc.sync.dma_start(out=T["ws"][:], in_=Ws)
         load_s(0)
         T["bs"] = sb.tile([P, V], BF16, name="bs_b")
         nc.sync.dma_start(out=T["bs"][:], in_=bs_.partition_broadcast(P))
-        load_rest(0, FIRST)
+        load_queries(0, FIRST, N)
         load_c(0)
+        make_identity(nc, ident[:])
+        sort_keys(0)
+        for piece in range(4):
+            style_regroup(0, piece)
 
         def live(i):
-            return 0 <= i < UNITS
+            return 0 <= i < TILES
 
-        def group_ok(k):
-            return 0 <= k <= LASTK
+        DONE1, DONE2 = 11, 20
+        BLOCK1, BLOCK2 = 4 * DONE1 + 10, 4 * DONE2 + 8
+        finals = {}
+        for n in range(DONE1):
+            finals[BLOCK1 + 3 + 5 * n // 2] = n
+        for n in range(DONE1, DONE2):
+            finals[BLOCK2 + 1 + (n - DONE1)] = n
 
-        LASTK = UNITS // GROUP - 1
-        J = 10
-        for i in range(-LEAD - 1, UNITS):
-            r, kd = i % GROUP, i // GROUP - 1
-            b, ib = i // UNITS_B, i % UNITS_B
-            gi = ib // GROUP
-            nb = b + 1 if (0 <= b and b + 1 < B) else None
-            pb = b - 1 if 1 <= b < B else None
-            split = ((i - 2) // GROUP) % 1 < 0
+        for i in range(-LEAD - 1, TILES + 2):
+            k, r = i // GROUP, i % GROUP
+            b, ib = i // TILES_B, i % TILES_B
+            nb = b + 1 if 0 <= b and b + 1 < B else None
             if live(i - 1):
                 flip(i - 1)
             if live(i + LEAD + 1):
                 logits(i + LEAD + 1)
-            if r == 2 and group_ok(kd):
-                spread(kd)
-            if r == 3 and group_ok(kd):
-                sums(kd, 0, True)
-                sums(kd, 1, False)
-            if i == -1:
+            if r == 2 and 0 <= k - 1:
+                sums(k - 1, 0)
+            if r == 0 and 0 <= k - 2 < GROUPS - 1:
+                sums(k - 2, 1)
+            if i in finals:
+                final_flip(finals[i])
+            if i == -3:
                 weights_flip()
-            if i == 3:
-                style_project(0, 0)
-            if nb is not None and r == 0 and gi in (4, 5):
-                style_project(nb, gi - 4)
-            if live(i + LEAD):
-                max_half(i + LEAD, 0)
-                max_half(i + LEAD, 1)
-            if live(i - 2):
-                if r == 3:
-                    if split:
-                        regroup(i - 2, slice(0, 1), False)
-                else:
-                    regroup(i - 2, BOTH, False)
-            if r == 3 and group_ok(kd):
-                spread_out(kd)
-            if ib == J and pb is not None:
-                for j in range(4):
-                    fin_sqrt(pb, 1024 * j, 1024 * (j + 1))
-            if i == 0:
-                weights_out()
-            if r == 0 and group_ok(kd - 1):
-                moments(kd - 1, False)
-            if r == 1 and group_ok(kd):
-                den_recip(kd)
-            if r == 2 and group_ok(kd):
-                quant(kd, 0)
-                quant(kd, 1)
-            if r == 3 and live(i - 2):
-                regroup(i - 2, slice(1, 2) if split else BOTH, True)
-            if i == -2:
-                weights_sort()
-                style_regroup(0, 0, False)
-                style_regroup(0, 1, False)
-            if i == 1:
-                weights_quant()
             if i == 2:
-                style_words(0, 0)
-                style_words(0, 1)
-            if i == 4:
-                style_bias(0, 0)
+                style_project(0, 0)
                 style_project(0, 1)
-            if i == 5:
+            if nb is not None and ib in (18, 20):
+                style_project(nb, (ib - 18) // 2)
+            if live(i + LEAD):
+                negate(i + LEAD, 1)
+            if live(i + LEAD + 1):
+                negate(i + LEAD + 1, 0)
+            if live(i - 2):
+                regroup(i - 2, False)
+            if i == -3:
+                weights_out()
+            if r == 3 and 0 <= k - 1:
+                means(k - 1, 0)
+            if r == 1 and 0 <= k - 2:
+                means(k - 2, 1)
+            if i == -2:
+                weights_quant()
+            if i in (0, 1):
+                style_words(0, i)
+            if i == 2:
+                style_bias(0, 0)
                 style_bias(0, 1)
                 style_round(0, 0)
-            if i == 6:
                 style_round(0, 1)
-            if nb is not None and r == 1:
-                if gi in (2, 3):
-                    style_words(nb, gi - 2)
-                if gi in (4, 5):
-                    style_bias(nb, gi - 4)
-                if gi == 6:
-                    style_quant(nb)
-            if nb is not None and r == 3 and gi in (4, 5):
-                style_round(nb, gi - 4)
-            if live(i + LEAD):
-                max_join(i + LEAD)
+            if i == 3:
+                style_quant(0)
+            if r == 1 and 0 <= k - 1:
+                den_recip(k - 1)
+                quant(k - 1)
+            if r == 0 and 0 <= k - 2:
+                variances(k - 2, 0)
+            if r == 2 and 0 <= k - 2 and k - 2 < GROUPS - 1:
+                variances(k - 2, 1)
+            if i in finals:
+                final_out(finals[i], True)
+            if i == BLOCK1:
+                for j in range(DONE1):
+                    deviations(j)
+                for q in range(2):
+                    for j in range(8):
+                        stats_chunk(q, j)
+                    stats_end(q)
+                    stats_rstd(q)
+            if i == BLOCK2:
+                for j in range(DONE1, DONE2):
+                    deviations(j)
+                for j in range(8):
+                    stats_chunk(2, j)
+                stats_end(2)
+                stats_rstd(2)
+            if i + 1 in finals:
+                final_content(finals[i + 1])
             if nb is not None:
                 if ib == 2:
                     load_s(nb)
-                    load_qk(nb, N)
-                    load_c(nb)
-                if ib == 4:
-                    style_regroup(nb, 0, False)
-                    style_regroup(nb, 1, False)
-            if ib == J and pb is not None:
-                for j in range(0 if pb == 0 else 4, 8):
-                    stats_chunk(pb, j)
-                stats_end(pb)
-                stats_rstd(pb)
-                for j in range(4 if b + 1 < B else 8):
-                    stats_chunk(b, j)
-            if pb is not None and ib > J and (ib - J) % 2 == 1 and (ib - J) // 2 < 8:
-                j = (ib - J) // 2
-                fin_rest(pb, GN * j, GN * (j + 1), False)
+                    load_keys(nb)
+                    load_queries(nb, 0, N)
+                    if nb == 1:
+                        load_c(nb)
+                if ib in (6, 8, 10, 12):
+                    style_regroup(nb, (ib - 6) // 2)
+                if ib in (14, 16):
+                    style_words(nb, (ib - 14) // 2)
+                if ib == 20:
+                    sort_keys(nb)
+                if ib in (19, 21):
+                    style_bias(nb, (ib - 19) // 2)
+                if ib in (21, 23):
+                    style_round(nb, (ib - 21) // 2)
+                if ib == 25:
+                    style_quant(nb)
+            if i - 1 in finals and finals[i - 1] == GROUPS_B - 1:
+                load_c(2)
             if live(i):
                 exps(i)
-            if i == 6:
-                style_quant(0)
-        LB = B - 1
-        flip(UNITS - 1)
-        regroup(UNITS - 2, BOTH, False)
-        den_recip(LASTK)
-        spread(LASTK)
-        moments(LASTK - 1, False)
-        regroup(UNITS - 1, slice(0, 1), False)
-        regroup(UNITS - 1, slice(1, 2), True)
-        spread_out(LASTK)
-        stats_end(LB)
-        quant(LASTK, 1)
-        quant(LASTK, 0)
-        sums(LASTK, 1, True)
-        sums(LASTK, 0, False)
-        stats_rstd(LB)
-        for j in range(6):
-            fin_sqrt(LB, GN * j, GN * (j + 1))
-        for j in range(3):
-            fin_rest(LB, GN * j, GN * (j + 1), j > 0)
-        moments(LASTK, True)
-        for j in range(3, 8):
-            if j >= 6:
-                fin_sqrt(LB, GN * j, GN * (j + 1))
-            fin_rest(LB, GN * j, GN * (j + 1), j not in (3, 4))
+        LK = GROUPS - 1
+        sums(LK, 0)
+        sums(LK, 1)
+        means(LK, 0)
+        variances(LK - 1, 1)
+        means(LK, 1)
+        for j in range(DONE2, LK):
+            deviations(j)
+            final_flip(j)
+            final_out(j, False)
+        variances(LK, 0)
+        variances(LK, 1)
+        deviations(LK)
+        final_flip(LK)
+        final_out(LK, False)

@@ -23,6 +23,7 @@ GROUPS = TILES // GROUP
 FLOPS = 2 * B * (V * VI * M + C * M * N + 2 * V * M * N)
 LEAD = 3
 TBUFS = 7
+FILL = 2
 
 
 def tile_adaattn3dstylizer_pb_t_kernel(tc, qp, kp, s, Ws, bs_, c, out):
@@ -199,33 +200,35 @@ def tile_adaattn3dstylizer_pb_t_kernel(tc, qp, kp, s, Ws, bs_, c, out):
             else:
                 nc.scalar.copy(out=dst, in_=src)
 
-        def den_recip(k):
-            T["r4", k] = sb.tile([P, GROUP], F32, name="r4", tag="r4", bufs=4)
-            nc.vector.reciprocal(out=T["r4", k][:], in_=T["dens", k][:])
-
-        def quant(k):
-            T["e_w", k] = sb.tile([P, GROUP * 2 * P], U32, name="e_w", tag="e_w", bufs=3, align_bytes=64)
-            T["e_s", k] = sb.tile([P, GROUP * 2 * P], U8, name="e_s", tag="e_s", bufs=3, align_bytes=64)
+        def quant(k, lo, hi):
+            if lo == 0:
+                T["r4", k] = sb.tile([P, GROUP], F32, name="r4", tag="r4", bufs=4)
+                T["e_w", k] = sb.tile([P, GROUP * 2 * P], U32, name="e_w", tag="e_w", bufs=3, align_bytes=64)
+                T["e_s", k] = sb.tile([P, GROUP * 2 * P], U8, name="e_s", tag="e_s", bufs=3, align_bytes=64)
+            nc.vector.reciprocal(out=T["r4", k][:, lo:hi], in_=T["dens", k][:, lo:hi])
+            cols = slice(2 * P * lo, 2 * P * hi)
             nc.vector.quantize_mx(
-                out=T["e_w", k][:].bitcast(FP8X4), scales=T["e_s", k][:],
-                in_=T["e_g", k][:].rearrange("p r x -> p (r x)"),
+                out=T["e_w", k][:, cols].bitcast(FP8X4), scales=T["e_s", k][:, cols],
+                in_=T["e_g", k][:, lo:hi, :].rearrange("p r x -> p (r x)"),
             )
 
-        def sums(k, h):
-            b = k // GROUPS_B
-            T["ab", k, h] = ps.tile([P, 2, 2 * V], F32, name="ab", tag="ab", bufs=2)
-            for a in range(2):
-                for g in range(2):
-                    cols = slice(P * (2 * (2 * h + a) + g), P * (2 * (2 * h + a) + g + 1))
-                    vs = slice(2 * V * g, 2 * V * (g + 1))
-                    nc.tensor.matmul_mx(
-                        out=T["ab", k, h][:, a, :],
-                        lhsT=T["e_w", k][:, cols].bitcast(FP8X4), lhsT_scale=T["e_s", k][:, cols],
-                        rhs=T["sp_w", b][:, vs].bitcast(FP8X4), rhs_scale=T["sp_s", b][:, vs],
-                        start=g == 0, stop=g == 1,
-                    )
+        def sums(i):
+            k, r = i // GROUP, i % GROUP
+            b, h, a = k // GROUPS_B, r // 2, r % 2
+            if a == 0:
+                T["ab", k, h] = ps.tile([P, 2, 2 * V], F32, name="ab", tag="ab", bufs=2)
+            for n in range(FILL + 2):
+                g = max(n - FILL, 0)
+                cols = slice(P * (2 * r + g), P * (2 * r + g + 1))
+                vs = slice(2 * V * g, 2 * V * (g + 1))
+                nc.tensor.matmul_mx(
+                    out=T["ab", k, h][:, a, :],
+                    lhsT=T["e_w", k][:, cols].bitcast(FP8X4), lhsT_scale=T["e_s", k][:, cols],
+                    rhs=T["sp_w", b][:, vs].bitcast(FP8X4), rhs_scale=T["sp_s", b][:, vs],
+                    start=n <= FILL, stop=n < FILL or n == FILL + 1,
+                )
 
-        def means(k, h):
+        def means(k, h, on_scalar=False):
             if h == 0:
                 T["mean", k] = sb.tile([P, GROUP, V], F32, name="mean", tag="mean", bufs=15)
                 T["x", k] = sb.tile([P, GN], F32, name="x", tag="x", bufs=15)
@@ -237,9 +240,12 @@ def tile_adaattn3dstylizer_pb_t_kernel(tc, qp, kp, s, Ws, bs_, c, out):
                 )
             T["m2", k, h] = sb.tile([P, 2, V], F32, name="m2", tag="m2", bufs=3)
             pair = T["mean", k][:, 2 * h : 2 * h + 2, :]
-            nc.gpsimd.tensor_tensor(out=T["m2", k, h][:], in0=pair, in1=pair, op=ALU.mult)
+            if on_scalar:
+                nc.scalar.activation(out=T["m2", k, h][:], in_=pair, func=ACT.Square)
+            else:
+                nc.gpsimd.tensor_tensor(out=T["m2", k, h][:], in0=pair, in1=pair, op=ALU.mult)
 
-        def variances(k, h):
+        def variances(k, h, on_vector=False):
             x = T["x", k]
             for a in range(2):
                 r = 2 * h + a
@@ -249,14 +255,20 @@ def tile_adaattn3dstylizer_pb_t_kernel(tc, qp, kp, s, Ws, bs_, c, out):
                     op0=ALU.mult, op1=ALU.subtract,
                 )
             pair = x[:, GN // 2 * h : GN // 2 * (h + 1)]
-            nc.gpsimd.tensor_scalar(out=pair, in0=pair, scalar1=3.0e38, scalar2=0.0, op0=ALU.min, op1=ALU.max)
+            if on_vector:
+                nc.vector.tensor_scalar_max(out=pair, in0=pair, scalar1=0.0)
+            else:
+                nc.gpsimd.tensor_scalar(
+                    out=pair, in0=pair, scalar1=3.0e38, scalar2=0.0, op0=ALU.min, op1=ALU.max
+                )
 
-        def deviations(k):
+        def deviations(k, lo=0, hi=GROUP):
             xt = ps.tile([P, GROUP, P], F32, name="x_ps", tag="tr", bufs=3)
-            for r in range(GROUP):
+            for r in range(lo, hi):
                 nc.tensor.transpose(xt[:, r, :], T["x", k][:, P * r : P * (r + 1)], ident[:])
             nc.scalar.activation(
-                out=T["x", k][:], in_=xt[:].rearrange("p r n -> p (r n)"), func=ACT.Sqrt
+                out=T["x", k][:, P * lo : P * hi], in_=xt[:, lo:hi, :].rearrange("p r n -> p (r n)"),
+                func=ACT.Sqrt,
             )
 
         def final_content(k):
@@ -268,25 +280,26 @@ def tile_adaattn3dstylizer_pb_t_kernel(tc, qp, kp, s, Ws, bs_, c, out):
             )
             nc.gpsimd.tensor_tensor(out=T["x", k][:], in0=cn[:], in1=T["x", k][:], op=ALU.mult)
 
-        def final_flip(k):
+        def final_flip(k, lo=0, hi=GROUP):
             T["mt", k] = ps.tile([P, GROUP, P], F32, name="m_ps", tag="tr", bufs=3)
-            for r in range(GROUP):
+            for r in range(lo, hi):
                 nc.tensor.transpose(T["mt", k][:, r, :], T["mean", k][:, r, :], ident[:])
 
-        def final_out(k, plain):
-            b, ns = k // GROUPS_B, slice(GN * (k % GROUPS_B), GN * (k % GROUPS_B + 1))
-            x, mt = T["x", k], T["mt", k][:].rearrange("p r n -> p (r n)")
+        def final_out(k, plain, lo=0, hi=GROUP):
+            b, n0 = k // GROUPS_B, GN * (k % GROUPS_B)
+            ns = slice(n0 + P * lo, n0 + P * hi)
+            x, mt = T["x", k][:, P * lo : P * hi], T["mt", k][:, lo:hi, :].rearrange("p r n -> p (r n)")
             if plain:
-                nc.vector.tensor_tensor(out=x[:], in0=mt, in1=x[:], op=ALU.add)
+                nc.vector.tensor_tensor(out=x, in0=mt, in1=x, op=ALU.add)
             else:
                 nc.vector.scalar_tensor_tensor(
-                    out=x[:], in0=T["c", b][:, ns], scalar=T["mv", b][:, 0:1], in1=x[:],
+                    out=x, in0=T["c", b][:, ns], scalar=T["mv", b][:, 0:1], in1=x,
                     op0=ALU.subtract, op1=ALU.mult,
                 )
                 nc.vector.scalar_tensor_tensor(
-                    out=x[:], in0=x[:], scalar=T["rstd", b][:, 0:1], in1=mt, op0=ALU.mult, op1=ALU.add
+                    out=x, in0=x, scalar=T["rstd", b][:, 0:1], in1=mt, op0=ALU.mult, op1=ALU.add
                 )
-            nc.sync.dma_start(out=out[b][:, ns], in_=x[:])
+            nc.sync.dma_start(out=out[b][:, ns], in_=x)
 
         FIRST = 512
         warm = sb.tile([P, 1], F32, name="warm")
@@ -309,26 +322,28 @@ def tile_adaattn3dstylizer_pb_t_kernel(tc, qp, kp, s, Ws, bs_, c, out):
         def live(i):
             return 0 <= i < TILES
 
-        DONE1, DONE2 = 11, 20
+        DONE1, DONE2 = 11, 19
         BLOCK1, BLOCK2 = 4 * DONE1 + 10, 4 * DONE2 + 8
+        LAST, LK = TILES - 1, GROUPS - 1
         finals = {}
         for n in range(DONE1):
-            finals[BLOCK1 + 3 + 5 * n // 2] = n
+            finals[BLOCK1 + 2 + 5 * n // 2] = n
         for n in range(DONE1, DONE2):
             finals[BLOCK2 + 1 + (n - DONE1)] = n
 
-        for i in range(-LEAD - 1, TILES + 2):
+        for i in range(-LEAD - 1, TILES):
             k, r = i // GROUP, i % GROUP
             b, ib = i // TILES_B, i % TILES_B
             nb = b + 1 if 0 <= b and b + 1 < B else None
             if live(i - 1):
                 flip(i - 1)
-            if live(i + LEAD + 1):
+            if live(i + LEAD + 1) and i - 1 not in (BLOCK1, BLOCK2):
                 logits(i + LEAD + 1)
-            if r == 2 and 0 <= k - 1:
-                sums(k - 1, 0)
-            if r == 0 and 0 <= k - 2 < GROUPS - 1:
-                sums(k - 2, 1)
+            if i == LAST - 1:
+                sums(i - 6)
+                sums(i - 5)
+            elif live(i - 6) and i < LAST - 1:
+                sums(i - 6)
             if i in finals:
                 final_flip(finals[i])
             if i == -3:
@@ -346,10 +361,10 @@ def tile_adaattn3dstylizer_pb_t_kernel(tc, qp, kp, s, Ws, bs_, c, out):
                 regroup(i - 2, False)
             if i == -3:
                 weights_out()
-            if r == 3 and 0 <= k - 1:
-                means(k - 1, 0)
-            if r == 1 and 0 <= k - 2:
-                means(k - 2, 1)
+            if r in (0, 2) and 0 <= k - 2:
+                means(k - 2, r // 2)
+            if i == LAST:
+                means(LK - 1, 0)
             if i == -2:
                 weights_quant()
             if i in (0, 1):
@@ -361,26 +376,30 @@ def tile_adaattn3dstylizer_pb_t_kernel(tc, qp, kp, s, Ws, bs_, c, out):
                 style_round(0, 1)
             if i == 3:
                 style_quant(0)
+            if r in (1, 3) and 0 <= k - 2:
+                variances(k - 2, r // 2)
             if r == 1 and 0 <= k - 1:
-                den_recip(k - 1)
-                quant(k - 1)
-            if r == 0 and 0 <= k - 2:
-                variances(k - 2, 0)
-            if r == 2 and 0 <= k - 2 and k - 2 < GROUPS - 1:
-                variances(k - 2, 1)
+                quant(k - 1, 0, GROUP)
+            if i == LAST:
+                quant(LK, 0, 2)
+            if 20 <= i < 52 and r == 2:
+                stats_chunk(0, (i - 20) // 4)
             if i in finals:
                 final_out(finals[i], True)
             if i == BLOCK1:
+                stats_end(0)
                 for j in range(DONE1):
                     deviations(j)
-                for q in range(2):
-                    for j in range(8):
-                        stats_chunk(q, j)
-                    stats_end(q)
-                    stats_rstd(q)
+                logits(i + LEAD + 2)
+                for j in range(8):
+                    stats_chunk(1, j)
+                stats_end(1)
+                stats_rstd(0)
+                stats_rstd(1)
             if i == BLOCK2:
                 for j in range(DONE1, DONE2):
                     deviations(j)
+                logits(i + LEAD + 2)
                 for j in range(8):
                     stats_chunk(2, j)
                 stats_end(2)
@@ -410,18 +429,35 @@ def tile_adaattn3dstylizer_pb_t_kernel(tc, qp, kp, s, Ws, bs_, c, out):
                 load_c(2)
             if live(i):
                 exps(i)
-        LK = GROUPS - 1
-        sums(LK, 0)
-        sums(LK, 1)
-        means(LK, 0)
-        variances(LK - 1, 1)
-        means(LK, 1)
-        for j in range(DONE2, LK):
+        sums(LAST - 5)
+        sums(LAST - 4)
+        flip(LAST)
+        regroup(LAST - 1, True)
+        variances(LK - 1, 0, True)
+        means(LK - 1, 1, True)
+        sums(LAST - 3)
+        sums(LAST - 2)
+        regroup(LAST, True)
+        variances(LK - 1, 1, True)
+        quant(LK, 2, GROUP)
+        for j in range(DONE2, DONE2 + 2):
             deviations(j)
+        sums(LAST - 1)
+        sums(LAST)
+        means(LK, 0, True)
+        means(LK, 1, True)
+        variances(LK, 0, True)
+        variances(LK, 1, True)
+        for j in range(DONE2 + 2, LK):
+            deviations(j)
+        for j in range(DONE2, DONE2 + 2):
             final_flip(j)
             final_out(j, False)
-        variances(LK, 0)
-        variances(LK, 1)
-        deviations(LK)
-        final_flip(LK)
-        final_out(LK, False)
+        for h in range(2):
+            deviations(LK, 2 * h, 2 * h + 2)
+        for j in range(DONE2 + 2, LK):
+            final_flip(j)
+            final_out(j, False)
+        for h in range(2):
+            final_flip(LK, 2 * h, 2 * h + 2)
+            final_out(LK, False, 2 * h, 2 * h + 2)

@@ -22,6 +22,9 @@ GROUPS_B = TILES_B // GROUP
 GROUPS = TILES // GROUP
 FLOPS = 2 * B * (V * VI * M + C * M * N + 2 * V * M * N)
 LEAD = 3
+QT = 2
+FC = 2
+LAG = 5
 TBUFS = 7
 FILL = 2
 
@@ -62,7 +65,7 @@ def tile_adaattn3dstylizer_pb_t_kernel(tc, qp, kp, s, Ws, bs_, c, out):
 
         def weights_flip():
             words = T["ws"][:].bitcast(F32)
-            T["wt_ps"] = ps.tile([P, 2, P], F32, name="wt_ps", tag="tr", bufs=3)
+            T["wt_ps"] = ps.tile([P, 2, P], F32, name="wt_ps", tag="mt", bufs=1)
             for u in range(2):
                 nc.tensor.transpose(T["wt_ps"][:, u, :], words[:, u : 2 * P : 2], ident[:])
 
@@ -81,10 +84,10 @@ def tile_adaattn3dstylizer_pb_t_kernel(tc, qp, kp, s, Ws, bs_, c, out):
         def style_regroup(b, piece):
             if piece == 0:
                 T["s_g", b] = sb.tile([P, 2, 4, P, 4], BF16, name="s_g", tag="s_g", align_bytes=64)
-            g, t0 = piece // 2, 2 * (piece % 2)
-            src = T["s", b][:].rearrange("q j (g p t) -> q g t p j", g=2, t=4)[:, g, t0 : t0 + 2]
+            g, t = piece // 4, piece % 4
+            src = T["s", b][:].rearrange("q j (g p t) -> q g t p j", g=2, t=4)[:, g, t]
             nc.gpsimd.tensor_scalar(
-                out=T["s_g", b][:, g, t0 : t0 + 2], in0=src, scalar1=1.0, scalar2=0.0, op0=ALU.mult, op1=ALU.add
+                out=T["s_g", b][:, g, t], in0=src, scalar1=1.0, scalar2=0.0, op0=ALU.mult, op1=ALU.add
             )
 
         def style_words(b, g):
@@ -98,7 +101,7 @@ def tile_adaattn3dstylizer_pb_t_kernel(tc, qp, kp, s, Ws, bs_, c, out):
             )
 
         def style_project(b, g):
-            T["sp_ps", b, g] = ps.tile([P, 4, V], F32, name="sp_ps", tag="tr", bufs=3)
+            T["sp_ps", b, g] = ps.tile([P, 4, V], F32, name="sp_ps", tag="mt", bufs=1)
             for t in range(4):
                 cols = slice(P * (4 * g + t), P * (4 * g + t + 1))
                 nc.tensor.matmul_mx(
@@ -185,7 +188,7 @@ def tile_adaattn3dstylizer_pb_t_kernel(tc, qp, kp, s, Ws, bs_, c, out):
 
         def flip(i):
             words = T["e", i][:].bitcast(F32)
-            T["xt", i] = ps.tile([P, 4, P], F32, name="xt", tag="tr", bufs=3)
+            T["xt", i] = ps.tile([P, 4, P], F32, name="xt", tag="tr", bufs=2)
             for j in range(4):
                 nc.tensor.transpose(T["xt", i][:, j, :], words[:, P * j : P * (j + 1)], ident[:])
 
@@ -262,8 +265,9 @@ def tile_adaattn3dstylizer_pb_t_kernel(tc, qp, kp, s, Ws, bs_, c, out):
                     out=pair, in0=pair, scalar1=3.0e38, scalar2=0.0, op0=ALU.min, op1=ALU.max
                 )
 
-        def deviations(k, lo=0, hi=GROUP):
-            xt = ps.tile([P, GROUP, P], F32, name="x_ps", tag="tr", bufs=3)
+        def deviations(k, lo=0, hi=GROUP, tail=False):
+            tag, bufs = ("lg", 3) if tail else (("tr", 2), ("mt", 1), ("tr", 2))[k % 3]
+            xt = ps.tile([P, GROUP, P], F32, name="x_ps", tag=tag, bufs=bufs)
             for r in range(lo, hi):
                 nc.tensor.transpose(xt[:, r, :], T["x", k][:, P * r : P * (r + 1)], ident[:])
             nc.scalar.activation(
@@ -280,8 +284,9 @@ def tile_adaattn3dstylizer_pb_t_kernel(tc, qp, kp, s, Ws, bs_, c, out):
             )
             nc.gpsimd.tensor_tensor(out=T["x", k][:], in0=cn[:], in1=T["x", k][:], op=ALU.mult)
 
-        def final_flip(k, lo=0, hi=GROUP):
-            T["mt", k] = ps.tile([P, GROUP, P], F32, name="m_ps", tag="tr", bufs=3)
+        def final_flip(k, lo=0, hi=GROUP, tail=False):
+            tag, bufs = ("lg", 3) if tail else ("mt", 1)
+            T["mt", k] = ps.tile([P, GROUP, P], F32, name="m_ps", tag=tag, bufs=bufs)
             for r in range(lo, hi):
                 nc.tensor.transpose(T["mt", k][:, r, :], T["mean", k][:, r, :], ident[:])
 
@@ -316,76 +321,94 @@ def tile_adaattn3dstylizer_pb_t_kernel(tc, qp, kp, s, Ws, bs_, c, out):
         load_c(0)
         make_identity(nc, ident[:])
         sort_keys(0)
-        for piece in range(4):
+        for piece in range(8):
             style_regroup(0, piece)
 
         def live(i):
             return 0 <= i < TILES
 
         DONE1, DONE2 = 11, 19
-        BLOCK1, BLOCK2 = 4 * DONE1 + 10, 4 * DONE2 + 8
         LAST, LK = TILES - 1, GROUPS - 1
+
+        def sums_slot(j):
+            return j + max(11 - j // 8, LAG)
+
+        BLOCK1, BLOCK2 = sums_slot(GROUP * DONE1 - 1) + 3, sums_slot(GROUP * DONE2 - 1) + 3
         finals = {}
         for n in range(DONE1):
             finals[BLOCK1 + 2 + 5 * n // 2] = n
         for n in range(DONE1, DONE2):
-            finals[BLOCK2 + 1 + (n - DONE1)] = n
+            finals[BLOCK2 + FC + (n - DONE1)] = n
 
         for i in range(-LEAD - 1, TILES):
             k, r = i // GROUP, i % GROUP
             b, ib = i // TILES_B, i % TILES_B
             nb = b + 1 if 0 <= b and b + 1 < B else None
+            for j in range(max(i - 16, 0), i):
+                if j % 2 == 1 and sums_slot(j) + 2 == i:
+                    variances(j // GROUP, j % GROUP // 2)
             if live(i - 1):
                 flip(i - 1)
             if live(i + LEAD + 1) and i - 1 not in (BLOCK1, BLOCK2):
                 logits(i + LEAD + 1)
-            if i == LAST - 1:
-                sums(i - 6)
-                sums(i - 5)
-            elif live(i - 6) and i < LAST - 1:
-                sums(i - 6)
+            for j in range(max(i - 12, 0), i):
+                if sums_slot(j) == i:
+                    sums(j)
             if i in finals:
                 final_flip(finals[i])
             if i == -3:
                 weights_flip()
-            if i == 2:
-                style_project(0, 0)
-                style_project(0, 1)
-            if nb is not None and ib in (18, 20):
-                style_project(nb, (ib - 18) // 2)
             if live(i + LEAD):
                 negate(i + LEAD, 1)
             if live(i + LEAD + 1):
                 negate(i + LEAD + 1, 0)
-            if live(i - 2):
+            if live(i - 2) and i - 1 not in (BLOCK1, BLOCK2):
                 regroup(i - 2, False)
             if i == -3:
                 weights_out()
-            if r in (0, 2) and 0 <= k - 2:
-                means(k - 2, r // 2)
-            if i == LAST:
-                means(LK - 1, 0)
-            if i == -2:
-                weights_quant()
-            if i in (0, 1):
-                style_words(0, i)
+            for j in range(max(i - 16, 0), i):
+                if j % 2 == 1 and sums_slot(j) + 1 == i:
+                    means(j // GROUP, j % GROUP // 2)
             if i == 2:
-                style_bias(0, 0)
-                style_bias(0, 1)
-                style_round(0, 0)
-                style_round(0, 1)
-            if i == 3:
+                weights_quant()
+            if i in (3, 4):
+                style_words(0, i - 3)
+            if i in (5, 6):
+                style_project(0, i - 5)
+                style_bias(0, i - 5)
+            if i in (8, 9):
+                style_round(0, i - 8)
+            if i == 10:
                 style_quant(0)
-            if r in (1, 3) and 0 <= k - 2:
-                variances(k - 2, r // 2)
-            if r == 1 and 0 <= k - 1:
-                quant(k - 1, 0, GROUP)
-            if i == LAST:
-                quant(LK, 0, 2)
+            j = i - 2 - QT + 1
+            if live(j) and j % QT == 0:
+                quant(j // GROUP, j % GROUP, j % GROUP + QT)
             if 20 <= i < 52 and r == 2:
                 stats_chunk(0, (i - 20) // 4)
             if i in finals:
                 final_out(finals[i], True)
+            if nb is not None:
+                if ib == 2:
+                    load_s(nb)
+                    load_keys(nb)
+                    load_queries(nb, 0, N)
+                    if nb == 1:
+                        load_c(nb)
+                if 6 <= ib < 14:
+                    style_regroup(nb, ib - 6)
+                if ib in (14, 16):
+                    style_words(nb, (ib - 14) // 2)
+                if ib == 20:
+                    sort_keys(nb)
+                if ib in (18, 20):
+                    style_project(nb, (ib - 18) // 2)
+                    style_bias(nb, (ib - 18) // 2)
+                if ib in (21, 23):
+                    style_round(nb, (ib - 21) // 2)
+                if ib == 25:
+                    style_quant(nb)
+            if i in (BLOCK1, BLOCK2):
+                regroup(i - 1, False)
             if i == BLOCK1:
                 stats_end(0)
                 for j in range(DONE1):
@@ -404,60 +427,43 @@ def tile_adaattn3dstylizer_pb_t_kernel(tc, qp, kp, s, Ws, bs_, c, out):
                     stats_chunk(2, j)
                 stats_end(2)
                 stats_rstd(2)
-            if i + 1 in finals:
-                final_content(finals[i + 1])
-            if nb is not None:
-                if ib == 2:
-                    load_s(nb)
-                    load_keys(nb)
-                    load_queries(nb, 0, N)
-                    if nb == 1:
-                        load_c(nb)
-                if ib in (6, 8, 10, 12):
-                    style_regroup(nb, (ib - 6) // 2)
-                if ib in (14, 16):
-                    style_words(nb, (ib - 14) // 2)
-                if ib == 20:
-                    sort_keys(nb)
-                if ib in (19, 21):
-                    style_bias(nb, (ib - 19) // 2)
-                if ib in (21, 23):
-                    style_round(nb, (ib - 21) // 2)
-                if ib == 25:
-                    style_quant(nb)
+            if i + FC in finals:
+                final_content(finals[i + FC])
             if i - 1 in finals and finals[i - 1] == GROUPS_B - 1:
                 load_c(2)
             if live(i):
                 exps(i)
-        sums(LAST - 5)
-        sums(LAST - 4)
-        flip(LAST)
-        regroup(LAST - 1, True)
         variances(LK - 1, 0, True)
+        sums(LAST - 4)
+        deviations(DONE2, tail=True)
+        deviations(DONE2 + 1, tail=True)
+        flip(LAST)
         means(LK - 1, 1, True)
+        regroup(LAST - 1, True)
         sums(LAST - 3)
         sums(LAST - 2)
+        final_flip(DONE2, tail=True)
+        final_out(DONE2, False)
+        deviations(DONE2 + 2, tail=True)
         regroup(LAST, True)
         variances(LK - 1, 1, True)
         quant(LK, 2, GROUP)
-        for j in range(DONE2, DONE2 + 2):
-            deviations(j)
+        means(LK, 0, True)
+        final_flip(DONE2 + 1, tail=True)
+        final_out(DONE2 + 1, False)
         sums(LAST - 1)
         sums(LAST)
-        means(LK, 0, True)
-        means(LK, 1, True)
         variances(LK, 0, True)
+        deviations(LK - 1, tail=True)
+        means(LK, 1, True)
+        final_flip(DONE2 + 2, tail=True)
+        final_out(DONE2 + 2, False)
         variances(LK, 1, True)
-        for j in range(DONE2 + 2, LK):
-            deviations(j)
-        for j in range(DONE2, DONE2 + 2):
-            final_flip(j)
-            final_out(j, False)
-        for h in range(2):
-            deviations(LK, 2 * h, 2 * h + 2)
-        for j in range(DONE2 + 2, LK):
-            final_flip(j)
-            final_out(j, False)
-        for h in range(2):
-            final_flip(LK, 2 * h, 2 * h + 2)
-            final_out(LK, False, 2 * h, 2 * h + 2)
+        deviations(LK, 0, 2, tail=True)
+        final_flip(LK - 1, tail=True)
+        final_out(LK - 1, False)
+        final_flip(LK, 0, 2, tail=True)
+        deviations(LK, 2, 4, tail=True)
+        final_out(LK, False, 0, 2)
+        final_flip(LK, 2, 4, tail=True)
+        final_out(LK, False, 2, 4)

@@ -26,7 +26,6 @@ QT = 2
 FC = 2
 LAG = 5
 TBUFS = 7
-FILL = 2
 
 
 def tile_adaattn3dstylizer_pb_t_kernel(tc, qp, kp, s, Ws, bs_, c, out):
@@ -220,15 +219,14 @@ def tile_adaattn3dstylizer_pb_t_kernel(tc, qp, kp, s, Ws, bs_, c, out):
             b, h, a = k // GROUPS_B, r // 2, r % 2
             if a == 0:
                 T["ab", k, h] = ps.tile([P, 2, 2 * V], F32, name="ab", tag="ab", bufs=2)
-            for n in range(FILL + 2):
-                g = max(n - FILL, 0)
+            for g in range(2):
                 cols = slice(P * (2 * r + g), P * (2 * r + g + 1))
                 vs = slice(2 * V * g, 2 * V * (g + 1))
                 nc.tensor.matmul_mx(
                     out=T["ab", k, h][:, a, :],
                     lhsT=T["e_w", k][:, cols].bitcast(FP8X4), lhsT_scale=T["e_s", k][:, cols],
                     rhs=T["sp_w", b][:, vs].bitcast(FP8X4), rhs_scale=T["sp_s", b][:, vs],
-                    start=n <= FILL, stop=n < FILL or n == FILL + 1,
+                    start=g == 0, stop=g == 1,
                 )
 
         def means(k, h, on_scalar=False):

@@ -23,9 +23,10 @@ GROUPS = TILES // GROUP
 FLOPS = 2 * B * (V * VI * M + C * M * N + 2 * V * M * N)
 LEAD = 3
 QT = 2
+VCOPY = 91
 FC = 2
-LAG = 5
-TBUFS = 7
+LAG = 6
+TBUFS = 8
 
 
 def tile_adaattn3dstylizer_pb_t_kernel(tc, qp, kp, s, Ws, bs_, c, out):
@@ -52,7 +53,7 @@ def tile_adaattn3dstylizer_pb_t_kernel(tc, qp, kp, s, Ws, bs_, c, out):
             nc.sync.dma_start(out=T["s", b][:], in_=s[b].rearrange("(p j) m -> p j m", j=4))
 
         def load_c(b):
-            T["c", b] = sb.tile([P, N], BF16, name="c_sb", tag="c", bufs=2)
+            T["c", b] = sb.tile([P, N], BF16, name="c_sb", tag="c", bufs=3)
             nc.sync.dma_start(out=T["c", b][:], in_=c[b])
 
         def sort_keys(b):
@@ -149,11 +150,13 @@ def tile_adaattn3dstylizer_pb_t_kernel(tc, qp, kp, s, Ws, bs_, c, out):
             nc.vector.tensor_scalar_add(out=ve[:], in0=mv[:, 1:2], scalar1=EPS)
             T["mv", b], T["negmu", b], T["ve", b] = mv, negmu, ve
 
-        def stats_rstd(b):
-            sd = sb.tile([P, 1], F32, name="sd", tag="sd", bufs=3)
-            nc.scalar.activation(out=sd[:], in_=T["ve", b][:], func=ACT.Sqrt)
+        def stats_root(b):
+            T["sd", b] = sb.tile([P, 1], F32, name="sd", tag="sd", bufs=3)
+            nc.scalar.activation(out=T["sd", b][:], in_=T["ve", b][:], func=ACT.Sqrt)
+
+        def stats_invert(b):
             T["rstd", b] = sb.tile([P, 1], F32, name="rstd", tag="rstd", bufs=3)
-            nc.vector.reciprocal(out=T["rstd", b][:], in_=sd[:])
+            nc.vector.reciprocal(out=T["rstd", b][:], in_=T["sd", b][:])
 
         def logits(i):
             b, n0 = i // TILES_B, P * (i % TILES_B)
@@ -231,8 +234,8 @@ def tile_adaattn3dstylizer_pb_t_kernel(tc, qp, kp, s, Ws, bs_, c, out):
 
         def means(k, h, on_scalar=False):
             if h == 0:
-                T["mean", k] = sb.tile([P, GROUP, V], F32, name="mean", tag="mean", bufs=15)
-                T["x", k] = sb.tile([P, GN], F32, name="x", tag="x", bufs=15)
+                T["mean", k] = sb.tile([P, GROUP, V], F32, name="mean", tag="mean", bufs=16)
+                T["x", k] = sb.tile([P, GN], F32, name="x", tag="x", bufs=16)
             for a in range(2):
                 r = 2 * h + a
                 nc.scalar.activation(
@@ -283,7 +286,7 @@ def tile_adaattn3dstylizer_pb_t_kernel(tc, qp, kp, s, Ws, bs_, c, out):
             nc.gpsimd.tensor_tensor(out=T["x", k][:], in0=cn[:], in1=T["x", k][:], op=ALU.mult)
 
         def final_flip(k, lo=0, hi=GROUP, tail=False):
-            tag, bufs = ("lg", 3) if tail else ("mt", 1)
+            tag, bufs = ("tr", 2) if tail and k % 3 else ("mt", 1)
             T["mt", k] = ps.tile([P, GROUP, P], F32, name="m_ps", tag=tag, bufs=bufs)
             for r in range(lo, hi):
                 nc.tensor.transpose(T["mt", k][:, r, :], T["mean", k][:, r, :], ident[:])
@@ -325,18 +328,16 @@ def tile_adaattn3dstylizer_pb_t_kernel(tc, qp, kp, s, Ws, bs_, c, out):
         def live(i):
             return 0 <= i < TILES
 
-        DONE1, DONE2 = 11, 19
+        DONE = 13
         LAST, LK = TILES - 1, GROUPS - 1
 
         def sums_slot(j):
             return j + max(11 - j // 8, LAG)
 
-        BLOCK1, BLOCK2 = sums_slot(GROUP * DONE1 - 1) + 3, sums_slot(GROUP * DONE2 - 1) + 3
+        BLOCK = sums_slot(GROUP * DONE - 1) + 3
         finals = {}
-        for n in range(DONE1):
-            finals[BLOCK1 + 2 + 5 * n // 2] = n
-        for n in range(DONE1, DONE2):
-            finals[BLOCK2 + FC + (n - DONE1)] = n
+        for n in range(DONE):
+            finals[BLOCK + 4 + 2 * n] = n
 
         for i in range(-LEAD - 1, TILES):
             k, r = i // GROUP, i % GROUP
@@ -345,9 +346,11 @@ def tile_adaattn3dstylizer_pb_t_kernel(tc, qp, kp, s, Ws, bs_, c, out):
             for j in range(max(i - 16, 0), i):
                 if j % 2 == 1 and sums_slot(j) + 2 == i:
                     variances(j // GROUP, j % GROUP // 2)
+            if i == BLOCK + 1:
+                logits(i + LEAD + 2)
             if live(i - 1):
                 flip(i - 1)
-            if live(i + LEAD + 1) and i - 1 not in (BLOCK1, BLOCK2):
+            if live(i + LEAD + 1) and i not in (BLOCK + 1, BLOCK + 2):
                 logits(i + LEAD + 1)
             for j in range(max(i - 12, 0), i):
                 if sums_slot(j) == i:
@@ -360,8 +363,8 @@ def tile_adaattn3dstylizer_pb_t_kernel(tc, qp, kp, s, Ws, bs_, c, out):
                 negate(i + LEAD, 1)
             if live(i + LEAD + 1):
                 negate(i + LEAD + 1, 0)
-            if live(i - 2) and i - 1 not in (BLOCK1, BLOCK2):
-                regroup(i - 2, False)
+            if live(i - 2) and i - 1 not in (BLOCK,):
+                regroup(i - 2, i - 2 >= VCOPY)
             if i == -3:
                 weights_out()
             for j in range(max(i - 16, 0), i):
@@ -381,87 +384,87 @@ def tile_adaattn3dstylizer_pb_t_kernel(tc, qp, kp, s, Ws, bs_, c, out):
             j = i - 2 - QT + 1
             if live(j) and j % QT == 0:
                 quant(j // GROUP, j % GROUP, j % GROUP + QT)
-            if 20 <= i < 52 and r == 2:
-                stats_chunk(0, (i - 20) // 4)
+            if 26 <= i < 58 and r == 2:
+                stats_chunk(0, (i - 26) // 4)
+            if i == 58:
+                stats_end(0)
             if i in finals:
                 final_out(finals[i], True)
             if nb is not None:
-                if ib == 2:
+                if ib == 0:
                     load_s(nb)
                     load_keys(nb)
                     load_queries(nb, 0, N)
-                    if nb == 1:
-                        load_c(nb)
-                if 6 <= ib < 14:
-                    style_regroup(nb, ib - 6)
-                if ib in (14, 16):
-                    style_words(nb, (ib - 14) // 2)
+                    load_c(nb)
+                if ib in (2, 4, 6, 8, 10, 12, 14, 16):
+                    style_regroup(nb, (ib - 2) // 2)
+                if ib in (12, 18):
+                    style_words(nb, (ib - 12) // 6)
                 if ib == 20:
                     sort_keys(nb)
-                if ib in (18, 20):
-                    style_project(nb, (ib - 18) // 2)
-                    style_bias(nb, (ib - 18) // 2)
-                if ib in (21, 23):
-                    style_round(nb, (ib - 21) // 2)
-                if ib == 25:
+                if ib in (14, 20):
+                    style_project(nb, (ib - 14) // 6)
+                    style_bias(nb, (ib - 14) // 6)
+                if ib in (16, 22):
+                    style_round(nb, (ib - 16) // 6)
+                if ib == 24:
                     style_quant(nb)
-            if i in (BLOCK1, BLOCK2):
+            if i in (BLOCK,):
                 regroup(i - 1, False)
-            if i == BLOCK1:
-                stats_end(0)
-                for j in range(DONE1):
+            if i == BLOCK:
+                stats_root(0)
+                for j in range(DONE):
                     deviations(j)
                 logits(i + LEAD + 2)
                 for j in range(8):
                     stats_chunk(1, j)
                 stats_end(1)
-                stats_rstd(0)
-                stats_rstd(1)
-            if i == BLOCK2:
-                for j in range(DONE1, DONE2):
-                    deviations(j)
-                logits(i + LEAD + 2)
+                stats_root(1)
                 for j in range(8):
                     stats_chunk(2, j)
                 stats_end(2)
-                stats_rstd(2)
+                stats_invert(0)
+                stats_invert(1)
             if i + FC in finals:
                 final_content(finals[i + FC])
-            if i - 1 in finals and finals[i - 1] == GROUPS_B - 1:
-                load_c(2)
             if live(i):
                 exps(i)
-        variances(LK - 1, 0, True)
+        variances(LK - 2, 1, True)
+        means(LK - 1, 0, True)
+        sums(LAST - 5)
         sums(LAST - 4)
-        deviations(DONE2, tail=True)
-        deviations(DONE2 + 1, tail=True)
-        flip(LAST)
         means(LK - 1, 1, True)
+        stats_root(2)
+        deviations(DONE, tail=True)
+        deviations(DONE + 1, tail=True)
         regroup(LAST - 1, True)
+        variances(LK - 1, 0, True)
+        flip(LAST)
         sums(LAST - 3)
         sums(LAST - 2)
-        final_flip(DONE2, tail=True)
-        final_out(DONE2, False)
-        deviations(DONE2 + 2, tail=True)
-        regroup(LAST, True)
         variances(LK - 1, 1, True)
+        regroup(LAST, True)
         quant(LK, 2, GROUP)
+        stats_invert(2)
         means(LK, 0, True)
-        final_flip(DONE2 + 1, tail=True)
-        final_out(DONE2 + 1, False)
+        deviations(DONE + 2, tail=True)
+        final_flip(DONE, tail=True)
+        final_out(DONE, False)
         sums(LAST - 1)
         sums(LAST)
         variances(LK, 0, True)
-        deviations(LK - 1, tail=True)
         means(LK, 1, True)
-        final_flip(DONE2 + 2, tail=True)
-        final_out(DONE2 + 2, False)
-        variances(LK, 1, True)
+        for j in range(DONE + 3, LK):
+            deviations(j, tail=True)
+            final_flip(j - 2, tail=True)
+            final_out(j - 2, False)
+            if j == DONE + 3:
+                variances(LK, 1, True)
         deviations(LK, 0, 2, tail=True)
-        final_flip(LK - 1, tail=True)
-        final_out(LK - 1, False)
-        final_flip(LK, 0, 2, tail=True)
         deviations(LK, 2, 4, tail=True)
-        final_out(LK, False, 0, 2)
-        final_flip(LK, 2, 4, tail=True)
-        final_out(LK, False, 2, 4)
+        for j in (LK - 2, LK - 1):
+            final_flip(j, tail=True)
+            final_out(j, False)
+        for h in range(2):
+            final_flip(LK, 2 * h, 2 * h + 2, tail=True)
+            final_out(LK, False, 2 * h, 2 * h + 2)

@@ -39,9 +39,11 @@ def tile_adaattn3dstylizer_pb_t_kernel(tc, qp, kp, s, Ws, bs_, c, out):
 
         ident = sb.tile([P, P], F32, name="ident")
 
-        def load_keys(b):
-            T["kp", b] = sb.tile([P, M], BF16, name="kp_raw", tag="kp_raw", bufs=2)
-            nc.sync.dma_start(out=T["kp", b][:], in_=kp[b])
+        def load_keys(b, g=None):
+            if g in (None, 0):
+                T["kp", b] = sb.tile([P, M], BF16, name="kp_raw", tag="kp_raw", bufs=2)
+            ms = slice(0, M) if g is None else slice(512 * g, 512 * (g + 1))
+            nc.sync.dma_start(out=T["kp", b][:, ms], in_=kp[b][:, ms])
 
         def load_queries(b, lo, hi):
             if lo == 0:
@@ -56,11 +58,13 @@ def tile_adaattn3dstylizer_pb_t_kernel(tc, qp, kp, s, Ws, bs_, c, out):
             T["c", b] = sb.tile([P, N], BF16, name="c_sb", tag="c", bufs=3)
             nc.sync.dma_start(out=T["c", b][:], in_=c[b])
 
-        def sort_keys(b):
-            T["ks", b] = sb.tile([P, M], BF16, name="kp_sorted", tag="kp_sorted", bufs=2)
+        def sort_keys(b, g):
+            if g == 0:
+                T["ks", b] = sb.tile([P, M], BF16, name="kp_sorted", tag="kp_sorted", bufs=2)
+            ms = slice(512 * g, 512 * (g + 1))
             nc.vector.tensor_copy(
-                out=T["ks", b][:].bitcast(F32).rearrange("c (g u p) -> c g u p", g=2, u=2),
-                in_=T["kp", b][:].bitcast(F32).rearrange("c (g p u) -> c g u p", g=2, u=2),
+                out=T["ks", b][:, ms].bitcast(F32).rearrange("c (u p) -> c u p", u=2),
+                in_=T["kp", b][:, ms].bitcast(F32).rearrange("c (p u) -> c u p", u=2),
             )
 
         def weights_flip():
@@ -145,9 +149,13 @@ def tile_adaattn3dstylizer_pb_t_kernel(tc, qp, kp, s, Ws, bs_, c, out):
             mv = sb.tile([P, 2], F32, name="mv", tag="mv", bufs=3)
             nc.vector.bn_aggr(out=mv[:], in_=T["stats", b][:].rearrange("p a b -> p (a b)"))
             negmu = sb.tile([P, 1], F32, name="negmu", tag="negmu", bufs=3)
-            nc.vector.tensor_scalar_mul(out=negmu[:], in0=mv[:, 0:1], scalar1=-1.0)
+            nc.gpsimd.tensor_scalar(
+                out=negmu[:], in0=mv[:, 0:1], scalar1=-1.0, scalar2=0.0, op0=ALU.mult, op1=ALU.add
+            )
             ve = sb.tile([P, 1], F32, name="ve", tag="ve", bufs=3)
-            nc.vector.tensor_scalar_add(out=ve[:], in0=mv[:, 1:2], scalar1=EPS)
+            nc.gpsimd.tensor_scalar(
+                out=ve[:], in0=mv[:, 1:2], scalar1=1.0, scalar2=EPS, op0=ALU.mult, op1=ALU.add
+            )
             T["mv", b], T["negmu", b], T["ve", b] = mv, negmu, ve
 
         def stats_root(b):
@@ -158,9 +166,9 @@ def tile_adaattn3dstylizer_pb_t_kernel(tc, qp, kp, s, Ws, bs_, c, out):
             T["rstd", b] = sb.tile([P, 1], F32, name="rstd", tag="rstd", bufs=3)
             nc.vector.reciprocal(out=T["rstd", b][:], in_=T["sd", b][:])
 
-        def logits(i):
+        def logits(i, halves=(0, 1)):
             b, n0 = i // TILES_B, P * (i % TILES_B)
-            for h in range(2):
+            for h in halves:
                 T["lg", i, h] = ps.tile([P, 512], F32, name="lg", tag="lg", bufs=3)
                 nc.tensor.matmul(
                     T["lg", i, h][:], lhsT=T["qp", b][:, n0 : n0 + P],
@@ -210,7 +218,8 @@ def tile_adaattn3dstylizer_pb_t_kernel(tc, qp, kp, s, Ws, bs_, c, out):
                 T["r4", k] = sb.tile([P, GROUP], F32, name="r4", tag="r4", bufs=4)
                 T["e_w", k] = sb.tile([P, GROUP * 2 * P], U32, name="e_w", tag="e_w", bufs=3, align_bytes=64)
                 T["e_s", k] = sb.tile([P, GROUP * 2 * P], U8, name="e_s", tag="e_s", bufs=3, align_bytes=64)
-            nc.vector.reciprocal(out=T["r4", k][:, lo:hi], in_=T["dens", k][:, lo:hi])
+            if hi == GROUP:
+                nc.vector.reciprocal(out=T["r4", k][:], in_=T["dens", k][:])
             cols = slice(2 * P * lo, 2 * P * hi)
             nc.vector.quantize_mx(
                 out=T["e_w", k][:, cols].bitcast(FP8X4), scales=T["e_s", k][:, cols],
@@ -291,6 +300,14 @@ def tile_adaattn3dstylizer_pb_t_kernel(tc, qp, kp, s, Ws, bs_, c, out):
             for r in range(lo, hi):
                 nc.tensor.transpose(T["mt", k][:, r, :], T["mean", k][:, r, :], ident[:])
 
+        def end_times(k, lo=0, hi=GROUP):
+            b, n0 = k // GROUPS_B, GN * (k % GROUPS_B)
+            x = T["x", k][:, P * lo : P * hi]
+            nc.vector.scalar_tensor_tensor(
+                out=x, in0=T["c", b][:, n0 + P * lo : n0 + P * hi], scalar=T["mv", b][:, 0:1], in1=x,
+                op0=ALU.subtract, op1=ALU.mult,
+            )
+
         def final_out(k, plain, lo=0, hi=GROUP):
             b, n0 = k // GROUPS_B, GN * (k % GROUPS_B)
             ns = slice(n0 + P * lo, n0 + P * hi)
@@ -298,10 +315,6 @@ def tile_adaattn3dstylizer_pb_t_kernel(tc, qp, kp, s, Ws, bs_, c, out):
             if plain:
                 nc.vector.tensor_tensor(out=x, in0=mt, in1=x, op=ALU.add)
             else:
-                nc.vector.scalar_tensor_tensor(
-                    out=x, in0=T["c", b][:, ns], scalar=T["mv", b][:, 0:1], in1=x,
-                    op0=ALU.subtract, op1=ALU.mult,
-                )
                 nc.vector.scalar_tensor_tensor(
                     out=x, in0=x, scalar=T["rstd", b][:, 0:1], in1=mt, op0=ALU.mult, op1=ALU.add
                 )
@@ -311,8 +324,10 @@ def tile_adaattn3dstylizer_pb_t_kernel(tc, qp, kp, s, Ws, bs_, c, out):
         warm = sb.tile([P, 1], F32, name="warm")
         nc.vector.memset(warm[:], 0.0)
         nc.scalar.activation(out=warm[:], in_=warm[:], func=ACT.Exp)
-        load_keys(0)
-        load_queries(0, 0, FIRST)
+        load_keys(0, 0)
+        load_queries(0, 0, P)
+        load_keys(0, 1)
+        load_queries(0, P, FIRST)
         T["ws"] = sb.tile([P, VI], BF16, name="ws_sb")
         nc.sync.dma_start(out=T["ws"][:], in_=Ws)
         load_s(0)
@@ -321,7 +336,8 @@ def tile_adaattn3dstylizer_pb_t_kernel(tc, qp, kp, s, Ws, bs_, c, out):
         load_queries(0, FIRST, N)
         load_c(0)
         make_identity(nc, ident[:])
-        sort_keys(0)
+        sort_keys(0, 0)
+        sort_keys(0, 1)
         for piece in range(8):
             style_regroup(0, piece)
 
@@ -350,7 +366,13 @@ def tile_adaattn3dstylizer_pb_t_kernel(tc, qp, kp, s, Ws, bs_, c, out):
                 logits(i + LEAD + 2)
             if live(i - 1):
                 flip(i - 1)
-            if live(i + LEAD + 1) and i not in (BLOCK + 1, BLOCK + 2):
+            if i < 0:
+                logits(i + LEAD + 1, (0,))
+                if live(i + LEAD):
+                    logits(i + LEAD, (1,))
+            elif live(i + LEAD + 1) and i not in (BLOCK + 1, BLOCK + 2):
+                if i == 0:
+                    logits(LEAD, (1,))
                 logits(i + LEAD + 1)
             for j in range(max(i - 12, 0), i):
                 if sums_slot(j) == i:
@@ -359,9 +381,11 @@ def tile_adaattn3dstylizer_pb_t_kernel(tc, qp, kp, s, Ws, bs_, c, out):
                 final_flip(finals[i])
             if i == -3:
                 weights_flip()
+            if i < 0:
+                negate(i + LEAD + 1, 0)
             if live(i + LEAD):
                 negate(i + LEAD, 1)
-            if live(i + LEAD + 1):
+            if i >= 0 and live(i + LEAD + 1):
                 negate(i + LEAD + 1, 0)
             if live(i - 2) and i - 1 not in (BLOCK,):
                 regroup(i - 2, i - 2 >= VCOPY)
@@ -396,18 +420,19 @@ def tile_adaattn3dstylizer_pb_t_kernel(tc, qp, kp, s, Ws, bs_, c, out):
                     load_keys(nb)
                     load_queries(nb, 0, N)
                     load_c(nb)
-                if ib in (2, 4, 6, 8, 10, 12, 14, 16):
-                    style_regroup(nb, (ib - 2) // 2)
-                if ib in (12, 18):
-                    style_words(nb, (ib - 12) // 6)
-                if ib == 20:
-                    sort_keys(nb)
-                if ib in (14, 20):
-                    style_project(nb, (ib - 14) // 6)
-                    style_bias(nb, (ib - 14) // 6)
-                if ib in (16, 22):
-                    style_round(nb, (ib - 16) // 6)
+                if 8 <= ib < 24 and ib % 2 == 0:
+                    style_regroup(nb, (ib - 8) // 2)
+                if ib in (16, 24):
+                    style_words(nb, (ib - 16) // 8)
                 if ib == 24:
+                    sort_keys(nb, 0)
+                    sort_keys(nb, 1)
+                if ib in (18, 26):
+                    style_project(nb, (ib - 18) // 8)
+                    style_bias(nb, (ib - 18) // 8)
+                if ib in (20, 28):
+                    style_round(nb, (ib - 20) // 8)
+                if ib == 30:
                     style_quant(nb)
             if i in (BLOCK,):
                 regroup(i - 1, False)
@@ -429,7 +454,7 @@ def tile_adaattn3dstylizer_pb_t_kernel(tc, qp, kp, s, Ws, bs_, c, out):
                 final_content(finals[i + FC])
             if live(i):
                 exps(i)
-        variances(LK - 2, 1, True)
+        variances(LK - 2, 1)
         means(LK - 1, 0, True)
         sums(LAST - 5)
         sums(LAST - 4)
@@ -438,33 +463,40 @@ def tile_adaattn3dstylizer_pb_t_kernel(tc, qp, kp, s, Ws, bs_, c, out):
         deviations(DONE, tail=True)
         deviations(DONE + 1, tail=True)
         regroup(LAST - 1, True)
-        variances(LK - 1, 0, True)
+        variances(LK - 1, 0)
         flip(LAST)
         sums(LAST - 3)
         sums(LAST - 2)
-        variances(LK - 1, 1, True)
+        variances(LK - 1, 1)
         regroup(LAST, True)
         quant(LK, 2, GROUP)
         stats_invert(2)
         means(LK, 0, True)
         deviations(DONE + 2, tail=True)
+        end_times(DONE)
         final_flip(DONE, tail=True)
-        final_out(DONE, False)
         sums(LAST - 1)
         sums(LAST)
-        variances(LK, 0, True)
+        variances(LK, 0)
+        end_times(DONE + 1)
+        final_out(DONE, False)
         means(LK, 1, True)
         for j in range(DONE + 3, LK):
             deviations(j, tail=True)
+            end_times(j - 1)
             final_flip(j - 2, tail=True)
             final_out(j - 2, False)
             if j == DONE + 3:
-                variances(LK, 1, True)
+                variances(LK, 1)
         deviations(LK, 0, 2, tail=True)
+        end_times(LK - 1)
+        final_flip(LK - 2, tail=True)
+        final_out(LK - 2, False)
         deviations(LK, 2, 4, tail=True)
-        for j in (LK - 2, LK - 1):
-            final_flip(j, tail=True)
-            final_out(j, False)
+        end_times(LK, 0, 2)
+        final_flip(LK - 1, tail=True)
+        final_out(LK - 1, False)
+        end_times(LK, 2, 4)
         for h in range(2):
             final_flip(LK, 2 * h, 2 * h + 2, tail=True)
             final_out(LK, False, 2 * h, 2 * h + 2)

@@ -58,15 +58,6 @@ def tile_adaattn3dstylizer_pb_t_kernel(tc, qp, kp, s, Ws, bs_, c, out):
             T["c", b] = sb.tile([P, N], BF16, name="c_sb", tag="c", bufs=3)
             nc.sync.dma_start(out=T["c", b][:], in_=c[b])
 
-        def sort_keys(b, g):
-            if g == 0:
-                T["ks", b] = sb.tile([P, M], BF16, name="kp_sorted", tag="kp_sorted", bufs=2)
-            ms = slice(512 * g, 512 * (g + 1))
-            nc.vector.tensor_copy(
-                out=T["ks", b][:, ms].bitcast(F32).rearrange("c (u p) -> c u p", u=2),
-                in_=T["kp", b][:, ms].bitcast(F32).rearrange("c (p u) -> c u p", u=2),
-            )
-
         def weights_flip():
             words = T["ws"][:].bitcast(F32)
             T["wt_ps"] = ps.tile([P, 2, P], F32, name="wt_ps", tag="mt", bufs=1)
@@ -172,7 +163,8 @@ def tile_adaattn3dstylizer_pb_t_kernel(tc, qp, kp, s, Ws, bs_, c, out):
                 T["lg", i, h] = ps.tile([P, 512], F32, name="lg", tag="lg", bufs=3)
                 nc.tensor.matmul(
                     T["lg", i, h][:], lhsT=T["qp", b][:, n0 : n0 + P],
-                    rhs=T["ks", b][:, 512 * h : 512 * (h + 1)], start=True, stop=True,
+                    rhs=T["kp", b][:, 512 * h : 512 * (h + 1)].rearrange("c (p u e) -> c u p e", u=2, e=2),
+                    start=True, stop=True,
                 )
 
         def negate(i, h):
@@ -336,8 +328,6 @@ def tile_adaattn3dstylizer_pb_t_kernel(tc, qp, kp, s, Ws, bs_, c, out):
         load_queries(0, FIRST, N)
         load_c(0)
         make_identity(nc, ident[:])
-        sort_keys(0, 0)
-        sort_keys(0, 1)
         for piece in range(8):
             style_regroup(0, piece)
 
@@ -353,7 +343,7 @@ def tile_adaattn3dstylizer_pb_t_kernel(tc, qp, kp, s, Ws, bs_, c, out):
         BLOCK = sums_slot(GROUP * DONE - 1) + 3
         finals = {}
         for n in range(DONE):
-            finals[BLOCK + 4 + 2 * n] = n
+            finals[BLOCK + 4 + 2 * (n + n // 4)] = n
 
         for i in range(-LEAD - 1, TILES):
             k, r = i // GROUP, i % GROUP
@@ -424,9 +414,6 @@ def tile_adaattn3dstylizer_pb_t_kernel(tc, qp, kp, s, Ws, bs_, c, out):
                     style_regroup(nb, (ib - 8) // 2)
                 if ib in (16, 24):
                     style_words(nb, (ib - 16) // 8)
-                if ib == 24:
-                    sort_keys(nb, 0)
-                    sort_keys(nb, 1)
                 if ib in (18, 26):
                     style_project(nb, (ib - 18) // 8)
                     style_bias(nb, (ib - 18) // 8)
@@ -455,31 +442,31 @@ def tile_adaattn3dstylizer_pb_t_kernel(tc, qp, kp, s, Ws, bs_, c, out):
             if live(i):
                 exps(i)
         variances(LK - 2, 1)
+        stats_root(2)
+        deviations(DONE, tail=True)
         means(LK - 1, 0, True)
         sums(LAST - 5)
         sums(LAST - 4)
-        means(LK - 1, 1, True)
-        stats_root(2)
-        deviations(DONE, tail=True)
-        deviations(DONE + 1, tail=True)
         regroup(LAST - 1, True)
-        variances(LK - 1, 0)
         flip(LAST)
+        means(LK - 1, 1, True)
+        variances(LK - 1, 0)
+        deviations(DONE + 1, tail=True)
         sums(LAST - 3)
         sums(LAST - 2)
-        variances(LK - 1, 1)
+        end_times(DONE)
+        final_flip(DONE, tail=True)
         regroup(LAST, True)
+        variances(LK - 1, 1)
         quant(LK, 2, GROUP)
         stats_invert(2)
         means(LK, 0, True)
         deviations(DONE + 2, tail=True)
-        end_times(DONE)
-        final_flip(DONE, tail=True)
+        end_times(DONE + 1)
+        final_out(DONE, False)
         sums(LAST - 1)
         sums(LAST)
         variances(LK, 0)
-        end_times(DONE + 1)
-        final_out(DONE, False)
         means(LK, 1, True)
         for j in range(DONE + 3, LK):
             deviations(j, tail=True)

@@ -9,6 +9,7 @@ U32 = mybir.dt.uint32
 U8 = mybir.dt.uint8
 FP8X4 = mybir.dt.float8_e4m3fn_x4
 ALU = mybir.AluOpType
+AX = mybir.AxisListType
 ACT = mybir.ActivationFunctionType
 
 P = 128
@@ -168,15 +169,18 @@ def tile_adaattn3dstylizer_pb_t_kernel(tc, qp, kp, s, Ws, bs_, c, out):
                 )
 
         def negate(i, h):
+            if i % 2 == 0 and h == 0:
+                T["mn", i // 2] = sb.tile([P, 2, 2], F32, name="mn", tag="mn", bufs=5)
             if h == 0:
-                T["mn", i] = sb.tile([P, 2], F32, name="mn", tag="mn", bufs=TBUFS + 1)
                 T["t", i] = sb.tile([P, M], F32, name="t_sb", tag="t_sb", bufs=TBUFS)
-            mn = T["mn", i]
             nc.vector.tensor_scalar(
-                out=T["t", i][:, 512 * h : 512 * (h + 1)], in0=T["lg", i, h][:],
-                scalar1=-1.0, scalar2=None if h == 0 else mn[:, 0:1],
-                op0=ALU.mult, op1=ALU.min, accum_out=mn[:, h : h + 1],
+                out=T["t", i][:, 512 * h : 512 * (h + 1)], in0=T["lg", i, h][:], scalar1=-1.0, scalar2=None,
+                op0=ALU.mult, op1=ALU.min, accum_out=T["mn", i // 2][:, i % 2, h : h + 1],
             )
+
+        def minima(q):
+            T["negmax", q] = sb.tile([P, 2], F32, name="negmax", tag="negmax", bufs=6)
+            nc.vector.tensor_reduce(out=T["negmax", q][:], in_=T["mn", q][:], axis=AX.X, op=ALU.min)
 
         def exps(i):
             k, r = i // GROUP, i % GROUP
@@ -185,7 +189,7 @@ def tile_adaattn3dstylizer_pb_t_kernel(tc, qp, kp, s, Ws, bs_, c, out):
             T["e", i] = sb.tile([P, M], BF16, name="e_sb", tag="e_sb", bufs=3)
             nc.scalar.activation(
                 out=T["e", i][:], in_=T["t", i][:], func=ACT.Exp,
-                bias=T["mn", i][:, 1:2], scale=-1.0, accum_out=T["dens", k][:, r : r + 1],
+                bias=T["negmax", i // 2][:, i % 2 : i % 2 + 1], scale=-1.0, accum_out=T["dens", k][:, r : r + 1],
             )
 
         def flip(i):
@@ -377,6 +381,9 @@ def tile_adaattn3dstylizer_pb_t_kernel(tc, qp, kp, s, Ws, bs_, c, out):
                 negate(i + LEAD, 1)
             if i >= 0 and live(i + LEAD + 1):
                 negate(i + LEAD + 1, 0)
+            j = i + LEAD - 1
+            if live(j) and j % 2 == 1:
+                minima(j // 2)
             if live(i - 2) and i - 1 not in (BLOCK,):
                 regroup(i - 2, i - 2 >= VCOPY)
             if i == -3:

from contextlib import ExitStack

import concourse.mybir as mybir
from concourse.masks import make_identity

F32 = mybir.dt.float32
BF16 = mybir.dt.bfloat16
U32 = mybir.dt.uint32
U8 = mybir.dt.uint8
FP8X4 = mybir.dt.float8_e4m3fn_x4
ALU = mybir.AluOpType
AX = mybir.AxisListType
ACT = mybir.ActivationFunctionType

P = 128
B, C, VI, V, N, M = 3, 128, 512, 128, 4096, 1024
EPS = 1e-5
TILES_B = N // P
TILES = B * TILES_B
GROUP = 4
GN = GROUP * P
GROUPS_B = TILES_B // GROUP
GROUPS = TILES // GROUP
FLOPS = 2 * B * (V * VI * M + C * M * N + 2 * V * M * N)
LEAD = 3
QT = 2
VCOPY = 91
FC = 2
LAG = 6
TBUFS = 8


def tile_adaattn3dstylizer_pb_t_kernel(tc, qp, kp, s, Ws, bs_, c, out):
    nc = tc.nc
    with ExitStack() as ctx:
        sb = ctx.enter_context(tc.tile_pool(name="sb", bufs=1))
        ps = ctx.enter_context(tc.psum_pool(name="ps", bufs=1))
        ctx.enter_context(tc.manual_schedule())
        T = {}

        ident = sb.tile([P, P], F32, name="ident")

        def load_keys(b, g=None):
            if g in (None, 0):
                T["kp", b] = sb.tile([P, M], BF16, name="kp_raw", tag="kp_raw", bufs=2)
            ms = slice(0, M) if g is None else slice(512 * g, 512 * (g + 1))
            nc.sync.dma_start(out=T["kp", b][:, ms], in_=kp[b][:, ms])

        def load_queries(b, lo, hi):
            if lo == 0:
                T["qp", b] = sb.tile([P, N], BF16, name="qp_sb", tag="qp", bufs=2)
            nc.sync.dma_start(out=T["qp", b][:, lo:hi], in_=qp[b][:, lo:hi])

        def load_s(b):
            T["s", b] = sb.tile([P, 4, M], BF16, name="s_raw", tag="s_raw", bufs=1)
            nc.sync.dma_start(out=T["s", b][:], in_=s[b].rearrange("(p j) m -> p j m", j=4))

        def load_c(b):
            T["c", b] = sb.tile([P, N], BF16, name="c_sb", tag="c", bufs=3)
            nc.sync.dma_start(out=T["c", b][:], in_=c[b])

        def weights_flip():
            words = T["ws"][:].bitcast(F32)
            T["wt_ps"] = ps.tile([P, 2, P], F32, name="wt_ps", tag="mt", bufs=1)
            for u in range(2):
                nc.tensor.transpose(T["wt_ps"][:, u, :], words[:, u : 2 * P : 2], ident[:])

        def weights_out():
            T["ws_g"] = sb.tile([P, V * 4], BF16, name="ws_g", align_bytes=64)
            nc.scalar.copy(
                out=T["ws_g"][:].bitcast(F32).rearrange("p (v u) -> p v u", u=2),
                in_=T["wt_ps"][:].rearrange("p u v -> p v u"),
            )

        def weights_quant():
            T["ws_w"] = sb.tile([P, V], U32, name="ws_w", align_bytes=64)
            T["ws_s"] = sb.tile([P, V], U8, name="ws_s", align_bytes=64)
            nc.vector.quantize_mx(out=T["ws_w"][:].bitcast(FP8X4), scales=T["ws_s"][:], in_=T["ws_g"][:])

        def style_regroup(b, piece):
            if piece == 0:
                T["s_g", b] = sb.tile([P, 2, 4, P, 4], BF16, name="s_g", tag="s_g", align_bytes=64)
            g, t = piece // 4, piece % 4
            src = T["s", b][:].rearrange("q j (g p t) -> q g t p j", g=2, t=4)[:, g, t]
            nc.gpsimd.tensor_scalar(
                out=T["s_g", b][:, g, t], in0=src, scalar1=1.0, scalar2=0.0, op0=ALU.mult, op1=ALU.add
            )

        def style_words(b, g):
            if g == 0:
                T["s_w", b] = sb.tile([P, M], U32, name="s_w", tag="s_w", align_bytes=64)
                T["s_s", b] = sb.tile([P, M], U8, name="s_s", tag="s_s", align_bytes=64)
            ms = slice(512 * g, 512 * (g + 1))
            nc.vector.quantize_mx(
                out=T["s_w", b][:, ms].bitcast(FP8X4), scales=T["s_s", b][:, ms],
                in_=T["s_g", b][:, g].rearrange("q t p j -> q (t p j)"),
            )

        def style_project(b, g):
            T["sp_ps", b, g] = ps.tile([P, 4, V], F32, name="sp_ps", tag="mt", bufs=1)
            for t in range(4):
                cols = slice(P * (4 * g + t), P * (4 * g + t + 1))
                nc.tensor.matmul_mx(
                    out=T["sp_ps", b, g][:, t, :],
                    lhsT=T["s_w", b][:, cols].bitcast(FP8X4), lhsT_scale=T["s_s", b][:, cols],
                    rhs=T["ws_w"][:].bitcast(FP8X4), rhs_scale=T["ws_s"][:],
                    start=True, stop=True,
                )

        def style_bias(b, g):
            if g == 0:
                T["sp_f", b] = sb.tile([P, 2, V, 4], F32, name="sp_f", tag="sp_f")
            nc.vector.tensor_tensor(
                out=T["sp_f", b][:, g], in0=T["sp_ps", b, g][:].rearrange("p t v -> p v t"),
                in1=T["bs"][:].unsqueeze(2).to_broadcast([P, V, 4]), op=ALU.add,
            )

        def style_round(b, g):
            if g == 0:
                T["sp_g", b] = sb.tile([P, 2, 2, V * 4], BF16, name="sp_g", tag="sp_g", align_bytes=64)
            flat = T["sp_f", b][:, g].rearrange("p v t -> p (v t)")
            nc.gpsimd.tensor_scalar(
                out=T["sp_g", b][:, g, 0, :], in0=flat, scalar1=1.0, scalar2=0.0, op0=ALU.mult, op1=ALU.add
            )
            nc.scalar.activation(out=T["sp_g", b][:, g, 1, :], in_=flat, func=ACT.Square)

        def style_quant(b):
            T["sp_w", b] = sb.tile([P, 4 * V], U32, name="sp_w", tag="sp_w", bufs=2, align_bytes=64)
            T["sp_s", b] = sb.tile([P, 4 * V], U8, name="sp_s", tag="sp_s", bufs=2, align_bytes=64)
            nc.vector.quantize_mx(
                out=T["sp_w", b][:].bitcast(FP8X4), scales=T["sp_s", b][:],
                in_=T["sp_g", b][:].rearrange("p g q x -> p (g q x)"),
            )

        def stats_chunk(b, i):
            if i == 0:
                T["stats", b] = sb.tile([P, 8, 6], F32, name="stats", tag="stats", bufs=2)
            nc.vector.bn_stats(out=T["stats", b][:, i, :], in_=T["c", b][:, 512 * i : 512 * (i + 1)])

        def stats_end(b):
            mv = sb.tile([P, 2], F32, name="mv", tag="mv", bufs=3)
            nc.vector.bn_aggr(out=mv[:], in_=T["stats", b][:].rearrange("p a b -> p (a b)"))
            negmu = sb.tile([P, 1], F32, name="negmu", tag="negmu", bufs=3)
            nc.gpsimd.tensor_scalar(
                out=negmu[:], in0=mv[:, 0:1], scalar1=-1.0, scalar2=0.0, op0=ALU.mult, op1=ALU.add
            )
            ve = sb.tile([P, 1], F32, name="ve", tag="ve", bufs=3)
            nc.gpsimd.tensor_scalar(
                out=ve[:], in0=mv[:, 1:2], scalar1=1.0, scalar2=EPS, op0=ALU.mult, op1=ALU.add
            )
            T["mv", b], T["negmu", b], T["ve", b] = mv, negmu, ve

        def stats_root(b):
            T["sd", b] = sb.tile([P, 1], F32, name="sd", tag="sd", bufs=3)
            nc.scalar.activation(out=T["sd", b][:], in_=T["ve", b][:], func=ACT.Sqrt)

        def stats_invert(b):
            T["rstd", b] = sb.tile([P, 1], F32, name="rstd", tag="rstd", bufs=3)
            nc.vector.reciprocal(out=T["rstd", b][:], in_=T["sd", b][:])

        def logits(i, halves=(0, 1)):
            b, n0 = i // TILES_B, P * (i % TILES_B)
            for h in halves:
                T["lg", i, h] = ps.tile([P, 512], F32, name="lg", tag="lg", bufs=3)
                nc.tensor.matmul(
                    T["lg", i, h][:], lhsT=T["qp", b][:, n0 : n0 + P],
                    rhs=T["kp", b][:, 512 * h : 512 * (h + 1)].rearrange("c (p u e) -> c u p e", u=2, e=2),
                    start=True, stop=True,
                )

        def negate(i, h):
            if i % 2 == 0 and h == 0:
                T["mn", i // 2] = sb.tile([P, 2, 2], F32, name="mn", tag="mn", bufs=5)
            if h == 0:
                T["t", i] = sb.tile([P, M], F32, name="t_sb", tag="t_sb", bufs=TBUFS)
            nc.vector.tensor_scalar(
                out=T["t", i][:, 512 * h : 512 * (h + 1)], in0=T["lg", i, h][:], scalar1=-1.0, scalar2=None,
                op0=ALU.mult, op1=ALU.min, accum_out=T["mn", i // 2][:, i % 2, h : h + 1],
            )

        def minima(q):
            T["negmax", q] = sb.tile([P, 2], F32, name="negmax", tag="negmax", bufs=6)
            nc.vector.tensor_reduce(out=T["negmax", q][:], in_=T["mn", q][:], axis=AX.X, op=ALU.min)

        def exps(i):
            k, r = i // GROUP, i % GROUP
            if r == 0:
                T["dens", k] = sb.tile([P, GROUP], F32, name="dens", tag="dens", bufs=4)
            T["e", i] = sb.tile([P, M], BF16, name="e_sb", tag="e_sb", bufs=3)
            nc.scalar.activation(
                out=T["e", i][:], in_=T["t", i][:], func=ACT.Exp,
                bias=T["negmax", i // 2][:, i % 2 : i % 2 + 1], scale=-1.0, accum_out=T["dens", k][:, r : r + 1],
            )

        def flip(i):
            words = T["e", i][:].bitcast(F32)
            T["xt", i] = ps.tile([P, 4, P], F32, name="xt", tag="tr", bufs=2)
            for j in range(4):
                nc.tensor.transpose(T["xt", i][:, j, :], words[:, P * j : P * (j + 1)], ident[:])

        def regroup(i, on_vector):
            k, r = i // GROUP, i % GROUP
            if r == 0:
                T["e_g", k] = sb.tile([P, GROUP, 2 * P * 4], BF16, name="e_g", tag="e_g", bufs=2, align_bytes=64)
            src = T["xt", i][:].rearrange("p (g u) n -> p g n u", g=2)
            dst = T["e_g", k][:, r, :].bitcast(F32).rearrange("p (g n u) -> p g n u", g=2, u=2)
            if on_vector:
                nc.vector.tensor_copy(out=dst, in_=src)
            else:
                nc.scalar.copy(out=dst, in_=src)

        def quant(k, lo, hi):
            if lo == 0:
                T["r4", k] = sb.tile([P, GROUP], F32, name="r4", tag="r4", bufs=4)
                T["e_w", k] = sb.tile([P, GROUP * 2 * P], U32, name="e_w", tag="e_w", bufs=3, align_bytes=64)
                T["e_s", k] = sb.tile([P, GROUP * 2 * P], U8, name="e_s", tag="e_s", bufs=3, align_bytes=64)
            if hi == GROUP:
                nc.vector.reciprocal(out=T["r4", k][:], in_=T["dens", k][:])
            cols = slice(2 * P * lo, 2 * P * hi)
            nc.vector.quantize_mx(
                out=T["e_w", k][:, cols].bitcast(FP8X4), scales=T["e_s", k][:, cols],
                in_=T["e_g", k][:, lo:hi, :].rearrange("p r x -> p (r x)"),
            )

        def sums(i):
            k, r = i // GROUP, i % GROUP
            b, h, a = k // GROUPS_B, r // 2, r % 2
            if a == 0:
                T["ab", k, h] = ps.tile([P, 2, 2 * V], F32, name="ab", tag="ab", bufs=2)
            for g in range(2):
                cols = slice(P * (2 * r + g), P * (2 * r + g + 1))
                vs = slice(2 * V * g, 2 * V * (g + 1))
                nc.tensor.matmul_mx(
                    out=T["ab", k, h][:, a, :],
                    lhsT=T["e_w", k][:, cols].bitcast(FP8X4), lhsT_scale=T["e_s", k][:, cols],
                    rhs=T["sp_w", b][:, vs].bitcast(FP8X4), rhs_scale=T["sp_s", b][:, vs],
                    start=g == 0, stop=g == 1,
                )

        def means(k, h, on_scalar=False):
            if h == 0:
                T["mean", k] = sb.tile([P, GROUP, V], F32, name="mean", tag="mean", bufs=16)
                T["x", k] = sb.tile([P, GN], F32, name="x", tag="x", bufs=16)
            for a in range(2):
                r = 2 * h + a
                nc.scalar.activation(
                    out=T["mean", k][:, r, :], in_=T["ab", k, h][:, a, 0:V], func=ACT.Copy,
                    scale=T["r4", k][:, r : r + 1],
                )
            T["m2", k, h] = sb.tile([P, 2, V], F32, name="m2", tag="m2", bufs=3)
            pair = T["mean", k][:, 2 * h : 2 * h + 2, :]
            if on_scalar:
                nc.scalar.activation(out=T["m2", k, h][:], in_=pair, func=ACT.Square)
            else:
                nc.gpsimd.tensor_tensor(out=T["m2", k, h][:], in0=pair, in1=pair, op=ALU.mult)

        def variances(k, h, on_vector=False):
            x = T["x", k]
            for a in range(2):
                r = 2 * h + a
                nc.vector.scalar_tensor_tensor(
                    out=x[:, P * r : P * (r + 1)], in0=T["ab", k, h][:, a, V : 2 * V],
                    scalar=T["r4", k][:, r : r + 1], in1=T["m2", k, h][:, a, :],
                    op0=ALU.mult, op1=ALU.subtract,
                )
            pair = x[:, GN // 2 * h : GN // 2 * (h + 1)]
            if on_vector:
                nc.vector.tensor_scalar_max(out=pair, in0=pair, scalar1=0.0)
            else:
                nc.gpsimd.tensor_scalar(
                    out=pair, in0=pair, scalar1=3.0e38, scalar2=0.0, op0=ALU.min, op1=ALU.max
                )

        def deviations(k, lo=0, hi=GROUP, tail=False):
            tag, bufs = ("lg", 3) if tail else (("tr", 2), ("mt", 1), ("tr", 2))[k % 3]
            xt = ps.tile([P, GROUP, P], F32, name="x_ps", tag=tag, bufs=bufs)
            for r in range(lo, hi):
                nc.tensor.transpose(xt[:, r, :], T["x", k][:, P * r : P * (r + 1)], ident[:])
            nc.scalar.activation(
                out=T["x", k][:, P * lo : P * hi], in_=xt[:, lo:hi, :].rearrange("p r n -> p (r n)"),
                func=ACT.Sqrt,
            )

        def final_content(k):
            b, ns = k // GROUPS_B, slice(GN * (k % GROUPS_B), GN * (k % GROUPS_B + 1))
            cn = sb.tile([P, GN], F32, name="cn", tag="cn", bufs=2)
            nc.gpsimd.tensor_scalar(
                out=cn[:], in0=T["c", b][:, ns], scalar1=T["negmu", b][:, 0:1], scalar2=T["rstd", b][:, 0:1],
                op0=ALU.add, op1=ALU.mult,
            )
            nc.gpsimd.tensor_tensor(out=T["x", k][:], in0=cn[:], in1=T["x", k][:], op=ALU.mult)

        def final_flip(k, lo=0, hi=GROUP, tail=False):
            tag, bufs = ("tr", 2) if tail and k % 3 else ("mt", 1)
            T["mt", k] = ps.tile([P, GROUP, P], F32, name="m_ps", tag=tag, bufs=bufs)
            for r in range(lo, hi):
                nc.tensor.transpose(T["mt", k][:, r, :], T["mean", k][:, r, :], ident[:])

        def end_times(k, lo=0, hi=GROUP):
            b, n0 = k // GROUPS_B, GN * (k % GROUPS_B)
            x = T["x", k][:, P * lo : P * hi]
            nc.vector.scalar_tensor_tensor(
                out=x, in0=T["c", b][:, n0 + P * lo : n0 + P * hi], scalar=T["mv", b][:, 0:1], in1=x,
                op0=ALU.subtract, op1=ALU.mult,
            )

        def final_out(k, plain, lo=0, hi=GROUP):
            b, n0 = k // GROUPS_B, GN * (k % GROUPS_B)
            ns = slice(n0 + P * lo, n0 + P * hi)
            x, mt = T["x", k][:, P * lo : P * hi], T["mt", k][:, lo:hi, :].rearrange("p r n -> p (r n)")
            if plain:
                nc.vector.tensor_tensor(out=x, in0=mt, in1=x, op=ALU.add)
            else:
                nc.vector.scalar_tensor_tensor(
                    out=x, in0=x, scalar=T["rstd", b][:, 0:1], in1=mt, op0=ALU.mult, op1=ALU.add
                )
            nc.sync.dma_start(out=out[b][:, ns], in_=x)

        FIRST = 512
        warm = sb.tile([P, 1], F32, name="warm")
        nc.vector.memset(warm[:], 0.0)
        nc.scalar.activation(out=warm[:], in_=warm[:], func=ACT.Exp)
        load_keys(0, 0)
        load_queries(0, 0, P)
        load_keys(0, 1)
        load_queries(0, P, FIRST)
        T["ws"] = sb.tile([P, VI], BF16, name="ws_sb")
        nc.sync.dma_start(out=T["ws"][:], in_=Ws)
        load_s(0)
        T["bs"] = sb.tile([P, V], BF16, name="bs_b")
        nc.sync.dma_start(out=T["bs"][:], in_=bs_.partition_broadcast(P))
        load_queries(0, FIRST, N)
        load_c(0)
        make_identity(nc, ident[:])
        for piece in range(8):
            style_regroup(0, piece)

        def live(i):
            return 0 <= i < TILES

        DONE = 13
        LAST, LK = TILES - 1, GROUPS - 1

        def sums_slot(j):
            return j + max(11 - j // 8, LAG)

        BLOCK = sums_slot(GROUP * DONE - 1) + 3
        finals = {}
        for n in range(DONE):
            finals[BLOCK + 4 + 2 * (n + n // 4)] = n

        for i in range(-LEAD - 1, TILES):
            k, r = i // GROUP, i % GROUP
            b, ib = i // TILES_B, i % TILES_B
            nb = b + 1 if 0 <= b and b + 1 < B else None
            for j in range(max(i - 16, 0), i):
                if j % 2 == 1 and sums_slot(j) + 2 == i:
                    variances(j // GROUP, j % GROUP // 2)
            if i == BLOCK + 1:
                logits(i + LEAD + 2)
            if live(i - 1):
                flip(i - 1)
            if i < 0:
                logits(i + LEAD + 1, (0,))
                if live(i + LEAD):
                    logits(i + LEAD, (1,))
            elif live(i + LEAD + 1) and i not in (BLOCK + 1, BLOCK + 2):
                if i == 0:
                    logits(LEAD, (1,))
                logits(i + LEAD + 1)
            for j in range(max(i - 12, 0), i):
                if sums_slot(j) == i:
                    sums(j)
            if i in finals:
                final_flip(finals[i])
            if i == -3:
                weights_flip()
            if i < 0:
                negate(i + LEAD + 1, 0)
            if live(i + LEAD):
                negate(i + LEAD, 1)
            if i >= 0 and live(i + LEAD + 1):
                negate(i + LEAD + 1, 0)
            j = i + LEAD - 1
            if live(j) and j % 2 == 1:
                minima(j // 2)
            if live(i - 2) and i - 1 not in (BLOCK,):
                regroup(i - 2, i - 2 >= VCOPY)
            if i == -3:
                weights_out()
            for j in range(max(i - 16, 0), i):
                if j % 2 == 1 and sums_slot(j) + 1 == i:
                    means(j // GROUP, j % GROUP // 2)
            if i == 2:
                weights_quant()
            if i in (3, 4):
                style_words(0, i - 3)
            if i in (5, 6):
                style_project(0, i - 5)
                style_bias(0, i - 5)
            if i in (8, 9):
                style_round(0, i - 8)
            if i == 10:
                style_quant(0)
            j = i - 2 - QT + 1
            if live(j) and j % QT == 0:
                quant(j // GROUP, j % GROUP, j % GROUP + QT)
            if 26 <= i < 58 and r == 2:
                stats_chunk(0, (i - 26) // 4)
            if i == 58:
                stats_end(0)
            if i in finals:
                final_out(finals[i], True)
            if nb is not None:
                if ib == 0:
                    load_s(nb)
                    load_keys(nb)
                    load_queries(nb, 0, N)
                    load_c(nb)
                if 8 <= ib < 24 and ib % 2 == 0:
                    style_regroup(nb, (ib - 8) // 2)
                if ib in (16, 24):
                    style_words(nb, (ib - 16) // 8)
                if ib in (18, 26):
                    style_project(nb, (ib - 18) // 8)
                    style_bias(nb, (ib - 18) // 8)
                if ib in (20, 28):
                    style_round(nb, (ib - 20) // 8)
                if ib == 30:
                    style_quant(nb)
            if i in (BLOCK,):
                regroup(i - 1, False)
            if i == BLOCK:
                stats_root(0)
                for j in range(DONE):
                    deviations(j)
                logits(i + LEAD + 2)
                for j in range(8):
                    stats_chunk(1, j)
                stats_end(1)
                stats_root(1)
                for j in range(8):
                    stats_chunk(2, j)
                stats_end(2)
                stats_invert(0)
                stats_invert(1)
            if i + FC in finals:
                final_content(finals[i + FC])
            if live(i):
                exps(i)
        variances(LK - 2, 1)
        stats_root(2)
        deviations(DONE, tail=True)
        means(LK - 1, 0, True)
        sums(LAST - 5)
        sums(LAST - 4)
        regroup(LAST - 1, True)
        flip(LAST)
        means(LK - 1, 1, True)
        variances(LK - 1, 0)
        deviations(DONE + 1, tail=True)
        sums(LAST - 3)
        sums(LAST - 2)
        end_times(DONE)
        final_flip(DONE, tail=True)
        regroup(LAST, True)
        variances(LK - 1, 1)
        quant(LK, 2, GROUP)
        stats_invert(2)
        means(LK, 0, True)
        deviations(DONE + 2, tail=True)
        end_times(DONE + 1)
        final_out(DONE, False)
        sums(LAST - 1)
        sums(LAST)
        variances(LK, 0)
        means(LK, 1, True)
        for j in range(DONE + 3, LK):
            deviations(j, tail=True)
            end_times(j - 1)
            final_flip(j - 2, tail=True)
            final_out(j - 2, False)
            if j == DONE + 3:
                variances(LK, 1)
        deviations(LK, 0, 2, tail=True)
        end_times(LK - 1)
        final_flip(LK - 2, tail=True)
        final_out(LK - 2, False)
        deviations(LK, 2, 4, tail=True)
        end_times(LK, 0, 2)
        final_flip(LK - 1, tail=True)
        final_out(LK - 1, False)
        end_times(LK, 2, 4)
        for h in range(2):
            final_flip(LK, 2 * h, 2 * h + 2, tail=True)
            final_out(LK, False, 2 * h, 2 * h + 2)
